import numpy as np
import ml_dtypes


def mxq(x, axis, fmt="e4m3"):
    dtype, down = {"e4m3": (ml_dtypes.float8_e4m3fn, 7), "e5m2": (ml_dtypes.float8_e5m2, 14)}[fmt]
    v = np.moveaxis(np.asarray(x, np.float32).astype(ml_dtypes.bfloat16).astype(np.float64), axis, -1)
    blocks = v.reshape(v.shape[:-1] + (-1, 32))
    amax = np.abs(blocks).max(-1, keepdims=True)
    byte = np.maximum(np.where(amax > 0, np.frexp(amax)[1] - 1 + 127, 0) - down, 1)
    scale = np.exp2(byte - 127.0)
    codes = (blocks / scale).astype(np.float32).astype(dtype).astype(np.float64)
    return np.moveaxis((codes * scale).reshape(v.shape), -1, axis)


WIDE = False


def mx_kscale(k):
    if not WIDE:
        return np.ones(k)
    levels = np.array([10, -10, 5, -5, 0])
    if k % 512:
        return np.exp2(np.random.permutation(np.resize(levels, k // 32))).repeat(32)
    a = np.empty((k // 512, 16))
    for p in range(k // 512):
        a[p, :8] = np.random.permutation(np.resize(levels, 8))
        for g in range(8):
            far = levels[np.abs(levels - a[p, g]) >= 10]
            a[p, g + 8] = far[np.random.randint(len(far))]
    return np.exp2(a.ravel()).repeat(32)


BF16 = ml_dtypes.bfloat16


def bf(x):
    return np.asarray(x, np.float32).astype(BF16)


def f64(x):
    return np.asarray(x).astype(np.float64)


B, T, C, H, D, R = 4, 1024, 1024, 4, 128, 512
EPS = 1e-6
THETA = 10000.0


def rmsnorm(v, w):
    var = np.mean(v * v, axis=-1, keepdims=True)
    return v * (1.0 / np.sqrt(var + EPS)) * w


def rope(v, cos, sin):
    re, im = v[..., 0::2], v[..., 1::2]
    c, s = cos[None, :, None, :], sin[None, :, None, :]
    return np.stack([re * c - im * s, re * s + im * c], axis=-1).reshape(v.shape)


def draw0():
    s, t = mx_kscale(C), mx_kscale(R)
    ang = np.outer(np.arange(T), 1.0 / THETA ** (np.arange(0, D, 2) / D))
    return {"x": bf(np.random.standard_normal((B, T, C)) * s),
            "w_kv_down": bf(np.random.standard_normal((R, C)) / np.sqrt(C) / s[None, :] * t[:, None]),
            "w_kv_up": bf(np.random.standard_normal((2 * H * D, R)) / np.sqrt(R) / t[None, :]),
            "k_norm_w": bf(1.0 + 0.1 * np.random.standard_normal(D)),
            "freqs_cos": bf(np.cos(ang)), "freqs_sin": bf(np.sin(ang))}


def core(x, w_kv_down, w_kv_up, k_norm_w, freqs_cos, freqs_sin):
    latent = mxq(f64(x), 2, "e4m3") @ mxq(f64(w_kv_down), 1, "e4m3").T
    kv = (mxq(latent, 2, "e4m3") @ mxq(f64(w_kv_up), 1, "e4m3").T).reshape(B, T, 2, H, D)
    xk, xv = kv[:, :, 0], kv[:, :, 1]
    return rope(rmsnorm(xk, f64(k_norm_w)), f64(freqs_cos), f64(freqs_sin)), xv


def e4m3fn_bytes(y):
    return np.clip(np.asarray(y, np.float64), -448.0, 448.0).astype(np.float32).astype(ml_dtypes.float8_e4m3fn).view(np.uint8)


def e4m3fn_values(b):
    return np.asarray(b, np.uint8).view(ml_dtypes.float8_e4m3fn).astype(np.float64)


def setup_inputs():
    d = draw0()
    x0 = np.asarray(d['x']).astype(np.float64)
    s = (np.max(np.abs(x0), axis=(0, 1), keepdims=True) / 448.0).astype(np.float32)
    out = {}
    for k, v in d.items():
        if k == 'x':
            out['x_bytes'] = e4m3fn_bytes(x0 / s.astype(np.float64))
            out['x_scale'] = s
        else:
            out[k] = v
    return out


def reference(x_bytes, x_scale, w_kv_down, w_kv_up, k_norm_w, freqs_cos, freqs_sin):
    return core(e4m3fn_values(x_bytes) * x_scale.astype(np.float64), w_kv_down, w_kv_up, k_norm_w, freqs_cos, freqs_sin)

@@ -1,0 +1,446 @@
+from contextlib import ExitStack
+
+import concourse.mybir as mybir
+from concourse.masks import make_identity
+
+B, T, C, H, D, R = 4, 1024, 1024, 4, 128, 512
+EPS = 1e-6
+P = 128
+SUB = 128
+PAIRS = B * T // (2 * SUB)
+FEAT = H * D
+FLOPS = 2 * B * T * C * R + 2 * B * T * R * 2 * FEAT + 10 * B * T * FEAT
+
+F32 = mybir.dt.float32
+BF16 = mybir.dt.bfloat16
+U32 = mybir.dt.uint32
+U8 = mybir.dt.uint8
+FP8 = mybir.dt.float8_e4m3fn
+FP8X4 = mybir.dt.float8_e4m3fn_x4
+ACT = mybir.ActivationFunctionType
+ALU = mybir.AluOpType
+
+BUFS = {"lat": 2, "kb": 2, "vb": 2, "xt0": 1, "xt1": 1}
+EARLY = 2
+AHEAD = 2
+WARM = 8
+
+
+def tile_mla_pa_t_kernel(tc, x_bytes, x_scale, w_kv_down, w_kv_up, k_norm_w, freqs_cos, freqs_sin, out_0, out_1):
+    nc = tc.nc
+    with ExitStack() as ctx:
+        keep = ctx.enter_context(tc.tile_pool(name="keep", bufs=1))
+        work = ctx.enter_context(tc.tile_pool(name="work", bufs=3))
+        psum = ctx.enter_context(tc.psum_pool(name="psum", bufs=2))
+        ctx.enter_context(tc.manual_schedule())
+
+        eps_in = keep.tile([P, 1], F32)
+        nc.vector.memset(eps_in[:], 1.0)
+        eps_out = keep.tile([P, 1], F32)
+        nc.scalar.activation(out=eps_out[:], in_=eps_in[:], func=ACT.Abs_reciprocal_sqrt, bias=EPS, scale=1.0 / D)
+
+        warm = keep.tile([P, 512], BF16)
+        nc.vector.memset(warm[:], 0.0)
+        ident = keep.tile([P, P], F32)
+        make_identity(nc, ident[:])
+
+        scale = keep.tile([P, 2, 4], F32)
+        scale_row = keep.tile([P, C], F32)
+        cos_sb = keep.tile([P, 2, 4, D // 2], BF16)
+        sin_sb = keep.tile([P, 2, 4, D // 2], BF16)
+        gain = keep.tile([P, D], BF16)
+        wd_raw = keep.tile([P, 4, C], BF16, align_bytes=64)
+        wu_raw = keep.tile([P, 8, R], BF16, align_bytes=64)
+        wd_view = w_kv_down.rearrange("(m t) k -> m t k", t=4)
+        wu_view = w_kv_up.rearrange("(c m) r -> m c r", m=P)
+        x_views = [x_bytes[b].rearrange("(s p q) k -> s p q k", p=P, q=4) for b in range(B)]
+        x_tiles = {}
+
+        def load_x(pair):
+            b, s, h = pair // 4, pair // 2 % 2, pair % 2
+            x_codes = work.tile([P, 2, C], U8, tag="x_codes", bufs=PAIRS, align_bytes=64, name="x_codes")
+            nc.sync.dma_start(out=x_codes[:], in_=x_views[b][s][:, 2 * h : 2 * h + 2, :])
+            x_tiles[pair] = x_codes
+
+        nc.scalar.dma_start(out=gain[:], in_=k_norm_w.partition_broadcast(P))
+        load_x(0)
+        nc.sync.dma_start(out=scale[:], in_=x_scale[0, 0].rearrange("(g p t) -> p g t", p=P, t=4))
+        nc.sync.dma_start(out=wd_raw[:, 0:2, :], in_=wd_view[:, 0:2, :])
+        nc.sync.dma_start(out=cos_sb[:], in_=freqs_cos.rearrange("(s p q) j -> p s q j", p=P, q=4))
+        nc.sync.dma_start(out=sin_sb[:], in_=freqs_sin.rearrange("(s p q) j -> p s q j", p=P, q=4))
+        load_x(1)
+        nc.sync.dma_start(out=wd_raw[:, 2:4, :], in_=wd_view[:, 2:4, :])
+        nc.sync.dma_start(out=scale_row[:], in_=x_scale[0, 0].partition_broadcast(P))
+        load_x(2)
+        nc.sync.dma_start(out=wu_raw[:, 0:4, :], in_=wu_view[:, 0:4, :])
+        nc.sync.dma_start(out=wu_raw[:, 4:8, :], in_=wu_view[:, 4:8, :])
+        for pair in range(3, PAIRS):
+            load_x(pair)
+
+        half = D // 2
+        gain_pairs = gain[:].rearrange("p (j e) -> p j e", e=2)
+        gain_crossed = keep.tile([P, 2, half], F32)
+        nc.gpsimd.tensor_scalar(out=gain_crossed[:, 0], in0=gain_pairs[:, :, 1], scalar1=-1.0, scalar2=None, op0=ALU.mult)
+        nc.gpsimd.tensor_copy(out=gain_crossed[:, 1], in_=gain_pairs[:, :, 0])
+        table_a = keep.tile([P, 8, half, 2], F32)
+        table_b = keep.tile([P, 8, 2, half], F32)
+        nc.gpsimd.tensor_tensor(
+            out=table_a[:],
+            in0=cos_sb[:].rearrange("p s q j -> p (s q) j").unsqueeze(3).broadcast_to([P, 8, half, 2]),
+            in1=gain_pairs.unsqueeze(1).broadcast_to([P, 8, half, 2]),
+            op=ALU.mult,
+        )
+        nc.gpsimd.tensor_tensor(
+            out=table_b[:],
+            in0=sin_sb[:].rearrange("p s q j -> p (s q) j").unsqueeze(2).broadcast_to([P, 8, 2, half]),
+            in1=gain_crossed[:].unsqueeze(1).broadcast_to([P, 8, 2, half]),
+            op=ALU.mult,
+        )
+
+        wd_grouped = keep.tile([P, 2, 2, 256, 4], BF16, align_bytes=64)
+        wu_grouped = keep.tile([P, 2, 512, 4], BF16, align_bytes=64)
+        wd_codes = keep.tile([P, 2, 2, 256], U32, align_bytes=64)
+        wd_scales = keep.tile([P, 2, 2, 256], U8, align_bytes=64)
+        wu_codes = keep.tile([P, 2, 512], U32, align_bytes=64)
+        wu_scales = keep.tile([P, 2, 512], U8, align_bytes=64)
+
+        banks = {}
+
+        def bank_tile(tag, shape):
+            bank = psum.tile(shape, F32, tag=tag, bufs=BUFS[tag], name="bank")
+            return bank
+
+        def warm_up(count):
+            for n in range(count):
+                bank = bank_tile("vb", [P, 512])
+                nc.tensor.matmul(bank[:], lhsT=warm[:, 0:P], rhs=warm[:], start=True, stop=True)
+
+        def turn_words(out, words, first):
+            for u in range(2):
+                nc.tensor.transpose(out[:, u], words[:, first + u : first + 256 : 2], ident[:])
+
+        def wd_turn(th, tag):
+            for g in range(2):
+                bank = bank_tile(tag, [P, 2, 256])
+                for i in range(2):
+                    turn_words(bank[:, :, SUB * i : SUB * (i + 1)], wd_raw[:, 2 * th + i, :].bitcast(F32), 256 * g)
+                banks["wd", th, g] = bank
+
+        def wu_turn(part, tags):
+            for i in range(2):
+                bank = bank_tile(tags[i], [P, 2, 256])
+                for j in range(2):
+                    turn_words(bank[:, :, SUB * j : SUB * (j + 1)], wu_raw[:, 4 * part + 2 * i + j, :].bitcast(F32), 0)
+                banks["wu", part, i] = bank
+
+        def copy_words(copy, grouped, bank):
+            copy(out=grouped.rearrange("p n t -> p (n t)").bitcast(F32).rearrange("p (n u) -> p n u", u=2), in_=bank[:].rearrange("p u n -> p n u"))
+
+        def wd_out(copy, th, g):
+            copy_words(copy, wd_grouped[:, th, g], banks["wd", th, g])
+
+        def wu_out(copy, part, i):
+            copy_words(copy, wu_grouped[:, part, 256 * i : 256 * (i + 1)], banks["wu", part, i])
+
+        def wd_quant(th):
+            nc.vector.quantize_mx(
+                out=wd_codes[:, th].rearrange("p g n -> p (g n)").bitcast(FP8X4),
+                scales=wd_scales[:, th].rearrange("p g n -> p (g n)"),
+                in_=wd_grouped[:, th].rearrange("p g n t -> p (g n t)"),
+            )
+
+        def wu_quant(part):
+            nc.vector.quantize_mx(out=wu_codes[:, part].bitcast(FP8X4), scales=wu_scales[:, part], in_=wu_grouped[:, part].rearrange("p n t -> p (n t)"))
+
+        wide, xg, xq, xs, lat, lq, ls, rs, products = {}, {}, {}, {}, {}, {}, {}, {}, {}
+        kout, vout = {}, {}
+
+        def live(pair):
+            return 0 <= pair < PAIRS
+
+        def wide_tile(pair):
+            x_wide = work.tile([P, 2, C], BF16, tag="x_wide", bufs=AHEAD + 1, align_bytes=64, name="x_wide")
+            wide[pair] = x_wide
+
+        def widen(pair, a, copy):
+            if a == 0:
+                wide_tile(pair)
+            copy(out=wide[pair][:, a, :], in_=x_tiles[pair][:, a, :].bitcast(FP8))
+
+        def premult(pair, a):
+            if not EARLY <= pair < PAIRS:
+                return
+            if a == 0:
+                wide_tile(pair)
+            nc.vector.tensor_tensor(out=wide[pair][:, a, :], in0=x_tiles[pair][:, a, :].bitcast(FP8), in1=scale_row[:], op=ALU.mult)
+
+        def turn(pair, g):
+            if not live(pair):
+                return
+            bank = bank_tile("xt%d" % g, [P, 2, 256])
+            for a in range(2):
+                turn_words(bank[:, :, SUB * a : SUB * (a + 1)], wide[pair][:, a, :].bitcast(F32), 256 * g)
+            banks["xt", pair, g] = bank
+
+        def x_out(pair, g, copy=nc.scalar.copy):
+            if not live(pair):
+                return
+            if g == 0:
+                x_grouped = work.tile([P, 2, 256, 4], BF16, tag="x_grouped", align_bytes=64, name="x_grouped")
+                xg[pair] = x_grouped
+            bank = banks["xt", pair, g]
+            if pair >= EARLY:
+                copy_words(copy, xg[pair][:, g], bank)
+            else:
+                nc.vector.tensor_tensor(
+                    out=xg[pair][:, g].rearrange("p n (u e) -> p n u e", u=2),
+                    in0=bank[:].rearrange("p u n -> p (u n)").bitcast(BF16).rearrange("p (u n e) -> p n u e", u=2, e=2),
+                    in1=scale[:, g, :].rearrange("p (u e) -> p u e", u=2).unsqueeze(1).broadcast_to([P, 256, 2, 2]),
+                    op=ALU.mult,
+                )
+
+        def quant(pair):
+            if not live(pair):
+                return
+            x_q = work.tile([P, 2, 256], U32, tag="x_q", bufs=AHEAD + 1, align_bytes=64, name="x_q")
+            x_s = work.tile([P, 2, 256], U8, tag="x_s", bufs=AHEAD + 1, align_bytes=64, name="x_s")
+            nc.vector.quantize_mx(
+                out=x_q[:].rearrange("p g n -> p (g n)").bitcast(FP8X4),
+                scales=x_s[:].rearrange("p g n -> p (g n)"),
+                in_=xg[pair][:].rearrange("p g n t -> p (g n t)"),
+            )
+            xq[pair], xs[pair] = x_q, x_s
+
+        def down(pair, a):
+            if not live(pair):
+                return
+            bank = bank_tile("lat", [P, 4, SUB])
+            cols = slice(SUB * a, SUB * (a + 1))
+            for t in range(4):
+                th, wcols = t // 2, slice(SUB * (t % 2), SUB * (t % 2 + 1))
+                for g in range(2):
+                    nc.tensor.matmul_mx(
+                        out=bank[:, t, :],
+                        lhsT=wd_codes[:, th, g, wcols].bitcast(FP8X4),
+                        lhsT_scale=wd_scales[:, th, g, wcols],
+                        rhs=xq[pair][:, g, cols].bitcast(FP8X4),
+                        rhs_scale=xs[pair][:, g, cols],
+                        start=(g == 0),
+                        stop=(g == 1),
+                    )
+            banks["lat", pair, a] = bank
+
+        def latent_out(pair, a, copy=nc.scalar.copy):
+            if not live(pair):
+                return
+            latent = work.tile([P, SUB, 4], BF16, tag="latent", bufs=4, align_bytes=64, name="latent")
+            copy(out=latent[:], in_=banks["lat", pair, a][:].rearrange("p t n -> p n t"))
+            lat[pair, a] = latent
+
+        def latent_quant(pair, a):
+            if not live(pair):
+                return
+            l_q = work.tile([P, SUB], U32, tag="l_q", bufs=4, align_bytes=64, name="l_q")
+            l_s = work.tile([P, SUB], U8, tag="l_s", bufs=4, align_bytes=64, name="l_s")
+            nc.vector.quantize_mx(out=l_q[:].bitcast(FP8X4), scales=l_s[:], in_=lat[pair, a][:].rearrange("p n t -> p (n t)"))
+            lq[pair, a], ls[pair, a] = l_q, l_s
+
+        def up_pass(bank, pair, a, part):
+            nc.tensor.matmul_mx(
+                out=bank[:],
+                lhsT=lq[pair, a][:].bitcast(FP8X4),
+                lhsT_scale=ls[pair, a][:],
+                rhs=wu_codes[:, part].bitcast(FP8X4),
+                rhs_scale=wu_scales[:, part],
+                start=True,
+                stop=True,
+            )
+
+        def up(pair):
+            if not live(pair):
+                return
+            for part, tag in ((0, "kb"), (1, "vb")):
+                for a in range(2):
+                    if (tag, pair, a) not in banks:
+                        bank = bank_tile(tag, [P, FEAT])
+                        banks[tag, pair, a] = bank
+                    up_pass(banks[tag, pair, a], pair, a, part)
+
+        def keep_warm(pair, count):
+            if not live(pair):
+                return
+            bank = bank_tile("kb", [P, FEAT])
+            for n in range(count):
+                nc.tensor.matmul_mx(
+                    out=bank[:],
+                    lhsT=wd_codes[:, 0, 0, 0:P].bitcast(FP8X4),
+                    lhsT_scale=wd_scales[:, 0, 0, 0:P],
+                    rhs=wu_codes[:, 0].bitcast(FP8X4),
+                    rhs_scale=wu_scales[:, 0],
+                    start=True,
+                    stop=True,
+                )
+            banks["kb", pair, 0] = bank
+
+        def norm(pair, a):
+            if not live(pair):
+                return
+            squares = work.tile([P, H], F32, tag="squares", bufs=4, name="squares")
+            rstd = work.tile([P, H], F32, tag="rstd", bufs=4, name="rstd")
+            for h in range(H):
+                junk = work.tile([P, D], BF16, tag="junk", bufs=4, name="junk")
+                nc.scalar.activation(out=junk[:], in_=banks["kb", pair, a][:, D * h : D * (h + 1)], func=ACT.Square, accum_out=squares[:, h : h + 1])
+            nc.scalar.activation(out=rstd[:], in_=squares[:], func=ACT.Abs_reciprocal_sqrt, bias=EPS, scale=1.0 / D)
+            rs[pair, a] = rstd
+
+        def store(out, tile, pair, a):
+            b, s, h = pair // 4, pair // 2 % 2, pair % 2
+            view = out[b].rearrange("(s p q) h d -> s p q (h d)", p=P, q=4)[s]
+            if pair == PAIRS - 1:
+                nc.sync.dma_start(out=view[:, 2 * h + a, :], in_=tile[:, a, :])
+            elif a == 1:
+                nc.sync.dma_start(out=view[:, 2 * h : 2 * h + 2, :], in_=tile[:])
+
+        def values_out(pair, a, copy):
+            if not live(pair):
+                return
+            if a == 0:
+                v_tile = work.tile([P, 2, FEAT], F32, tag="v_tile", bufs=4, name="v_tile")
+                vout[pair] = v_tile
+            copy(out=vout[pair][:, a, :], in_=banks["vb", pair, a][:])
+            store(out_1, vout[pair], pair, a)
+
+        def posted(pair, a):
+            return a == 0
+
+        def rotate(pair, a, first, last):
+            if not live(pair):
+                return
+            row = (2 * pair + a) % 8
+            if first == 0:
+                t1 = work.tile([P, H, D], F32, tag="t1", name="t1")
+                t2 = work.tile([P, H, 2, half], F32, tag="t2", name="t2")
+                products[pair, a] = t1, t2
+            t1, t2 = products[pair, a]
+            k = banks["kb", pair, a][:].rearrange("p (h d) -> p h d", h=H)
+            straight = table_a[:, row].rearrange("p j e -> p (j e)")
+            if posted(pair, a):
+                if first == 0:
+                    nc.vector.tensor_tensor(out=t1[:], in0=k, in1=straight.unsqueeze(1).broadcast_to([P, H, D]), op=ALU.mult)
+                if last == 8:
+                    nc.vector.tensor_tensor(
+                        out=t2[:].rearrange("p h e j -> p e h j"),
+                        in0=k.rearrange("p h (j e) -> p e h j", e=2)[:, ::-1],
+                        in1=table_b[:, row].unsqueeze(2).broadcast_to([P, 2, H, half]),
+                        op=ALU.mult,
+                    )
+                return
+            for n in range(first, last):
+                h = n // 2
+                if n % 2 == 0:
+                    nc.vector.scalar_tensor_tensor(out=t1[:, h], in0=k[:, h], scalar=rs[pair, a][:, h : h + 1], in1=straight, op0=ALU.mult, op1=ALU.mult)
+                else:
+                    nc.vector.scalar_tensor_tensor(
+                        out=t2[:, h], in0=k[:, h].rearrange("p (j e) -> p e j", e=2)[:, ::-1], scalar=rs[pair, a][:, h : h + 1],
+                        in1=table_b[:, row], op0=ALU.mult, op1=ALU.mult,
+                    )
+
+        def keys_out(pair, a, adder):
+            if not live(pair):
+                return
+            if a == 0:
+                k_tile = work.tile([P, 2, FEAT], F32, tag="k_tile", bufs=4, name="k_tile")
+                kout[pair] = k_tile
+            t1, t2 = products[pair, a]
+            adder.tensor_tensor(
+                out=kout[pair][:, a, :].rearrange("p (h j e) -> p h j e", h=H, e=2),
+                in0=t1[:].rearrange("p h (j e) -> p h j e", e=2),
+                in1=t2[:].rearrange("p h e j -> p h j e"),
+                op=ALU.add,
+            )
+
+        def post(pair, a):
+            if not live(pair):
+                return
+            if not posted(pair, a):
+                store(out_0, kout[pair], pair, a)
+                return
+            for h in range(H):
+                head = kout[pair][:, a, D * h : D * (h + 1)]
+                nc.scalar.activation(out=head, in_=head, func=ACT.Copy, scale=rs[pair, a][:, h : h + 1])
+            store(out_0, kout[pair], pair, a)
+
+        warm_up(WARM)
+        widen(0, 0, nc.vector.tensor_copy)
+        widen(0, 1, nc.scalar.copy)
+        turn(0, 0)
+        turn(0, 1)
+        warm_up(2)
+        widen(1, 0, nc.scalar.copy)
+        widen(1, 1, nc.scalar.copy)
+        x_out(0, 0)
+        x_out(0, 1)
+        wd_turn(0, "lat")
+        warm_up(2)
+        wd_turn(1, "kb")
+        warm_up(2)
+        turn(1, 0)
+        turn(1, 1)
+        warm_up(1)
+        wd_out(nc.scalar.copy, 0, 0)
+        wd_out(nc.vector.tensor_copy, 0, 1)
+        wd_out(nc.scalar.copy, 1, 0)
+        wd_out(nc.vector.tensor_copy, 1, 1)
+        quant(0)
+        wd_quant(0)
+        wd_quant(1)
+        wu_turn(0, ("vb", "vb"))
+        down(0, 0)
+        down(0, 1)
+        wu_out(nc.scalar.copy, 0, 0)
+        wu_out(nc.scalar.copy, 0, 1)
+        premult(2, 0)
+        x_out(1, 0)
+        wu_turn(1, ("kb", "kb"))
+        latent_out(0, 0)
+        latent_out(0, 1)
+        premult(2, 1)
+        x_out(1, 1)
+        wu_quant(0)
+        latent_quant(0, 0)
+        latent_quant(0, 1)
+        wu_out(nc.scalar.copy, 1, 0)
+        wu_out(nc.scalar.copy, 1, 1)
+        quant(1)
+        wu_quant(1)
+        for pair in range(3, AHEAD + 1):
+            premult(pair, 0)
+            premult(pair, 1)
+
+        for s in range(1, PAIRS + 1):
+            up(s - 1)
+            down(s, 0)
+            down(s, 1)
+            turn(s + 1, 0)
+            turn(s + 1, 1)
+            post(s - 2, 0)
+            post(s - 2, 1)
+            norm(s - 1, 0)
+            norm(s - 1, 1)
+            premult(s + AHEAD, 0)
+            premult(s + AHEAD, 1)
+            for a in range(2):
+                rotate(s - 1, a, 0, 8)
+                keys_out(s - 1, a, nc.vector if s == PAIRS and a == 1 else nc.gpsimd)
+            keep_warm(s, 2)
+            latent_out(s, 0)
+            latent_out(s, 1)
+            x_out(s + 1, 0)
+            x_out(s + 1, 1)
+            values_out(s - 1, 0, nc.scalar.copy)
+            values_out(s - 1, 1, nc.scalar.copy)
+            latent_quant(s, 0)
+            latent_quant(s, 1)
+            quant(s + 1)
+        post(PAIRS - 1, 0)
+        post(PAIRS - 1, 1)

@@ -9,6 +9,8 @@ P = 128
 SUB = 128
 PAIRS = B * T // (2 * SUB)
 FEAT = H * D
+HALF = D // 2
+ROWS = T // P
 FLOPS = 2 * B * T * C * R + 2 * B * T * R * 2 * FEAT + 10 * B * T * FEAT
 
 F32 = mybir.dt.float32
@@ -20,10 +22,8 @@ FP8X4 = mybir.dt.float8_e4m3fn_x4
 ACT = mybir.ActivationFunctionType
 ALU = mybir.AluOpType
 
-BUFS = {"lat": 2, "kb": 2, "vb": 2, "xt0": 1, "xt1": 1}
 EARLY = 2
-AHEAD = 2
-WARM = 8
+STAGES = 3
 
 
 def tile_mla_pa_t_kernel(tc, x_bytes, x_scale, w_kv_down, w_kv_up, k_norm_w, freqs_cos, freqs_sin, out_0, out_1):
@@ -31,26 +31,18 @@ def tile_mla_pa_t_kernel(tc, x_bytes, x_scale, w_kv_down, w_kv_up, k_norm_w, fre
     with ExitStack() as ctx:
         keep = ctx.enter_context(tc.tile_pool(name="keep", bufs=1))
         work = ctx.enter_context(tc.tile_pool(name="work", bufs=3))
-        psum = ctx.enter_context(tc.psum_pool(name="psum", bufs=2))
+        psum = ctx.enter_context(tc.psum_pool(name="psum", bufs=1))
         ctx.enter_context(tc.manual_schedule())
 
-        eps_in = keep.tile([P, 1], F32)
-        nc.vector.memset(eps_in[:], 1.0)
-        eps_out = keep.tile([P, 1], F32)
-        nc.scalar.activation(out=eps_out[:], in_=eps_in[:], func=ACT.Abs_reciprocal_sqrt, bias=EPS, scale=1.0 / D)
-
-        warm = keep.tile([P, 512], BF16)
-        nc.vector.memset(warm[:], 0.0)
         ident = keep.tile([P, P], F32)
         make_identity(nc, ident[:])
 
         scale = keep.tile([P, 2, 4], F32)
         scale_row = keep.tile([P, C], F32)
-        cos_sb = keep.tile([P, 2, 4, D // 2], BF16)
-        sin_sb = keep.tile([P, 2, 4, D // 2], BF16)
+        trig = keep.tile([P, 3, ROWS * HALF], BF16)
         gain = keep.tile([P, D], BF16)
-        wd_raw = keep.tile([P, 4, C], BF16, align_bytes=64)
-        wu_raw = keep.tile([P, 8, R], BF16, align_bytes=64)
+        wd_raw = [keep.tile([P, 2, C], BF16, align_bytes=64, name="wd_raw%d" % i) for i in range(2)]
+        wu_raw = [keep.tile([P, 4, R], BF16, align_bytes=64, name="wu_raw%d" % i) for i in range(2)]
         wd_view = w_kv_down.rearrange("(m t) k -> m t k", t=4)
         wu_view = w_kv_up.rearrange("(c m) r -> m c r", m=P)
         x_views = [x_bytes[b].rearrange("(s p q) k -> s p q k", p=P, q=4) for b in range(B)]
@@ -62,40 +54,40 @@ def tile_mla_pa_t_kernel(tc, x_bytes, x_scale, w_kv_down, w_kv_up, k_norm_w, fre
             nc.sync.dma_start(out=x_codes[:], in_=x_views[b][s][:, 2 * h : 2 * h + 2, :])
             x_tiles[pair] = x_codes
 
+        def load_trig(slot, table):
+            nc.sync.dma_start(out=trig[:, slot].rearrange("p (s q j) -> p s q j", s=2, q=4), in_=table.rearrange("(s p q) j -> p s q j", p=P, q=4))
+
         nc.scalar.dma_start(out=gain[:], in_=k_norm_w.partition_broadcast(P))
         load_x(0)
         nc.sync.dma_start(out=scale[:], in_=x_scale[0, 0].rearrange("(g p t) -> p g t", p=P, t=4))
-        nc.sync.dma_start(out=wd_raw[:, 0:2, :], in_=wd_view[:, 0:2, :])
-        nc.sync.dma_start(out=cos_sb[:], in_=freqs_cos.rearrange("(s p q) j -> p s q j", p=P, q=4))
-        nc.sync.dma_start(out=sin_sb[:], in_=freqs_sin.rearrange("(s p q) j -> p s q j", p=P, q=4))
+        nc.sync.dma_start(out=wd_raw[0][:], in_=wd_view[:, 0:2, :])
         load_x(1)
-        nc.sync.dma_start(out=wd_raw[:, 2:4, :], in_=wd_view[:, 2:4, :])
+        nc.sync.dma_start(out=wd_raw[1][:], in_=wd_view[:, 2:4, :])
+        load_trig(0, freqs_cos)
+        load_trig(1, freqs_sin)
+        load_trig(2, freqs_cos)
+        nc.sync.dma_start(out=wu_raw[0][:], in_=wu_view[:, 0:4, :])
         nc.sync.dma_start(out=scale_row[:], in_=x_scale[0, 0].partition_broadcast(P))
         load_x(2)
-        nc.sync.dma_start(out=wu_raw[:, 0:4, :], in_=wu_view[:, 0:4, :])
-        nc.sync.dma_start(out=wu_raw[:, 4:8, :], in_=wu_view[:, 4:8, :])
+        nc.sync.dma_start(out=wu_raw[1][:], in_=wu_view[:, 4:8, :])
         for pair in range(3, PAIRS):
             load_x(pair)
 
-        half = D // 2
         gain_pairs = gain[:].rearrange("p (j e) -> p j e", e=2)
-        gain_crossed = keep.tile([P, 2, half], F32)
-        nc.gpsimd.tensor_scalar(out=gain_crossed[:, 0], in0=gain_pairs[:, :, 1], scalar1=-1.0, scalar2=None, op0=ALU.mult)
-        nc.gpsimd.tensor_copy(out=gain_crossed[:, 1], in_=gain_pairs[:, :, 0])
-        table_a = keep.tile([P, 8, half, 2], F32)
-        table_b = keep.tile([P, 8, 2, half], F32)
-        nc.gpsimd.tensor_tensor(
-            out=table_a[:],
-            in0=cos_sb[:].rearrange("p s q j -> p (s q) j").unsqueeze(3).broadcast_to([P, 8, half, 2]),
-            in1=gain_pairs.unsqueeze(1).broadcast_to([P, 8, half, 2]),
-            op=ALU.mult,
-        )
-        nc.gpsimd.tensor_tensor(
-            out=table_b[:],
-            in0=sin_sb[:].rearrange("p s q j -> p (s q) j").unsqueeze(2).broadcast_to([P, 8, 2, half]),
-            in1=gain_crossed[:].unsqueeze(1).broadcast_to([P, 8, 2, half]),
-            op=ALU.mult,
-        )
+        gain_quads = keep.tile([P, HALF, 2, 2], F32)
+        nc.vector.tensor_copy(out=gain_quads[:], in_=gain_pairs.unsqueeze(3).broadcast_to([P, HALF, 2, 2]))
+        nc.vector.tensor_scalar(out=gain_quads[:, :, 1, 0], in0=gain_pairs[:, :, 1], scalar1=-1.0, scalar2=None, op0=ALU.mult)
+        table = keep.tile([P, ROWS, HALF, 2, 2], F32)
+
+        def table_rows(first, last):
+            for row in range(first, last):
+                for e in range(2):
+                    nc.gpsimd.tensor_tensor(
+                        out=table[:, row, :, e, :],
+                        in0=trig[:, e : e + 2, HALF * row : HALF * (row + 1)].rearrange("p r j -> p j r"),
+                        in1=gain_quads[:, :, e, :],
+                        op=ALU.mult,
+                    )
 
         wd_grouped = keep.tile([P, 2, 2, 256, 4], BF16, align_bytes=64)
         wu_grouped = keep.tile([P, 2, 512, 4], BF16, align_bytes=64)
@@ -103,44 +95,40 @@ def tile_mla_pa_t_kernel(tc, x_bytes, x_scale, w_kv_down, w_kv_up, k_norm_w, fre
         wd_scales = keep.tile([P, 2, 2, 256], U8, align_bytes=64)
         wu_codes = keep.tile([P, 2, 512], U32, align_bytes=64)
         wu_scales = keep.tile([P, 2, 512], U8, align_bytes=64)
+        stages = [keep.tile([P, 2 * FEAT], F32, align_bytes=64, name="stage%d" % i) for i in range(STAGES)]
 
         banks = {}
 
         def bank_tile(tag, shape):
-            bank = psum.tile(shape, F32, tag=tag, bufs=BUFS[tag], name="bank")
+            bank = psum.tile(shape, F32, tag=tag, name="bank")
             return bank
-
-        def warm_up(count):
-            for n in range(count):
-                bank = bank_tile("vb", [P, 512])
-                nc.tensor.matmul(bank[:], lhsT=warm[:, 0:P], rhs=warm[:], start=True, stop=True)
 
         def turn_words(out, words, first):
             for u in range(2):
                 nc.tensor.transpose(out[:, u], words[:, first + u : first + 256 : 2], ident[:])
 
-        def wd_turn(th, tag):
+        def wd_turn(th, tags):
             for g in range(2):
-                bank = bank_tile(tag, [P, 2, 256])
+                bank = bank_tile(tags[g], [P, 2, 256])
                 for i in range(2):
-                    turn_words(bank[:, :, SUB * i : SUB * (i + 1)], wd_raw[:, 2 * th + i, :].bitcast(F32), 256 * g)
+                    turn_words(bank[:, :, SUB * i : SUB * (i + 1)], wd_raw[th][:, i, :].bitcast(F32), 256 * g)
                 banks["wd", th, g] = bank
 
         def wu_turn(part, tags):
             for i in range(2):
                 bank = bank_tile(tags[i], [P, 2, 256])
                 for j in range(2):
-                    turn_words(bank[:, :, SUB * j : SUB * (j + 1)], wu_raw[:, 4 * part + 2 * i + j, :].bitcast(F32), 0)
+                    turn_words(bank[:, :, SUB * j : SUB * (j + 1)], wu_raw[part][:, 2 * i + j, :].bitcast(F32), 0)
                 banks["wu", part, i] = bank
 
-        def copy_words(copy, grouped, bank):
-            copy(out=grouped.rearrange("p n t -> p (n t)").bitcast(F32).rearrange("p (n u) -> p n u", u=2), in_=bank[:].rearrange("p u n -> p n u"))
+        def copy_words(copy, words, bank):
+            copy(out=words.rearrange("p (n u) -> p n u", u=2), in_=bank[:].rearrange("p u n -> p n u"))
 
         def wd_out(copy, th, g):
-            copy_words(copy, wd_grouped[:, th, g], banks["wd", th, g])
+            copy_words(copy, wd_grouped[:, th, g].rearrange("p n t -> p (n t)").bitcast(F32), banks["wd", th, g])
 
         def wu_out(copy, part, i):
-            copy_words(copy, wu_grouped[:, part, 256 * i : 256 * (i + 1)], banks["wu", part, i])
+            copy_words(copy, wu_grouped[:, part, 256 * i : 256 * (i + 1)].rearrange("p n t -> p (n t)").bitcast(F32), banks["wu", part, i])
 
         def wd_quant(th):
             nc.vector.quantize_mx(
@@ -152,14 +140,13 @@ def tile_mla_pa_t_kernel(tc, x_bytes, x_scale, w_kv_down, w_kv_up, k_norm_w, fre
         def wu_quant(part):
             nc.vector.quantize_mx(out=wu_codes[:, part].bitcast(FP8X4), scales=wu_scales[:, part], in_=wu_grouped[:, part].rearrange("p n t -> p (n t)"))
 
-        wide, xg, xq, xs, lat, lq, ls, rs, products = {}, {}, {}, {}, {}, {}, {}, {}, {}
-        kout, vout = {}, {}
+        wide, xq, xs, lat, lq, ls, squares, rs, products, vout = {}, {}, {}, {}, {}, {}, {}, {}, {}, {}
 
         def live(pair):
             return 0 <= pair < PAIRS
 
         def wide_tile(pair):
-            x_wide = work.tile([P, 2, C], BF16, tag="x_wide", bufs=AHEAD + 1, align_bytes=64, name="x_wide")
+            x_wide = work.tile([P, 2, C], BF16, tag="x_wide", align_bytes=64, name="x_wide")
             wide[pair] = x_wide
 
         def widen(pair, a, copy):
@@ -182,18 +169,16 @@ def tile_mla_pa_t_kernel(tc, x_bytes, x_scale, w_kv_down, w_kv_up, k_norm_w, fre
                 turn_words(bank[:, :, SUB * a : SUB * (a + 1)], wide[pair][:, a, :].bitcast(F32), 256 * g)
             banks["xt", pair, g] = bank
 
-        def x_out(pair, g, copy=nc.scalar.copy):
+        def x_out(pair, g):
             if not live(pair):
                 return
-            if g == 0:
-                x_grouped = work.tile([P, 2, 256, 4], BF16, tag="x_grouped", align_bytes=64, name="x_grouped")
-                xg[pair] = x_grouped
+            words = stages[pair % STAGES][:, FEAT * g : FEAT * (g + 1)]
             bank = banks["xt", pair, g]
             if pair >= EARLY:
-                copy_words(copy, xg[pair][:, g], bank)
+                copy_words(nc.scalar.copy, words, bank)
             else:
                 nc.vector.tensor_tensor(
-                    out=xg[pair][:, g].rearrange("p n (u e) -> p n u e", u=2),
+                    out=words.bitcast(BF16).rearrange("p (n u e) -> p n u e", u=2, e=2),
                     in0=bank[:].rearrange("p u n -> p (u n)").bitcast(BF16).rearrange("p (u n e) -> p n u e", u=2, e=2),
                     in1=scale[:, g, :].rearrange("p (u e) -> p u e", u=2).unsqueeze(1).broadcast_to([P, 256, 2, 2]),
                     op=ALU.mult,
@@ -202,19 +187,19 @@ def tile_mla_pa_t_kernel(tc, x_bytes, x_scale, w_kv_down, w_kv_up, k_norm_w, fre
         def quant(pair):
             if not live(pair):
                 return
-            x_q = work.tile([P, 2, 256], U32, tag="x_q", bufs=AHEAD + 1, align_bytes=64, name="x_q")
-            x_s = work.tile([P, 2, 256], U8, tag="x_s", bufs=AHEAD + 1, align_bytes=64, name="x_s")
+            x_q = work.tile([P, 2, 256], U32, tag="x_q", align_bytes=64, name="x_q")
+            x_s = work.tile([P, 2, 256], U8, tag="x_s", align_bytes=64, name="x_s")
             nc.vector.quantize_mx(
                 out=x_q[:].rearrange("p g n -> p (g n)").bitcast(FP8X4),
                 scales=x_s[:].rearrange("p g n -> p (g n)"),
-                in_=xg[pair][:].rearrange("p g n t -> p (g n t)"),
+                in_=stages[pair % STAGES][:].bitcast(BF16),
             )
             xq[pair], xs[pair] = x_q, x_s
 
         def down(pair, a):
             if not live(pair):
                 return
-            bank = bank_tile("lat", [P, 4, SUB])
+            bank = bank_tile("lat%d" % a, [P, 4, SUB])
             cols = slice(SUB * a, SUB * (a + 1))
             for t in range(4):
                 th, wcols = t // 2, slice(SUB * (t % 2), SUB * (t % 2 + 1))
@@ -230,11 +215,11 @@ def tile_mla_pa_t_kernel(tc, x_bytes, x_scale, w_kv_down, w_kv_up, k_norm_w, fre
                     )
             banks["lat", pair, a] = bank
 
-        def latent_out(pair, a, copy=nc.scalar.copy):
+        def latent_out(pair, a):
             if not live(pair):
                 return
             latent = work.tile([P, SUB, 4], BF16, tag="latent", bufs=4, align_bytes=64, name="latent")
-            copy(out=latent[:], in_=banks["lat", pair, a][:].rearrange("p t n -> p n t"))
+            nc.scalar.copy(out=latent[:], in_=banks["lat", pair, a][:].rearrange("p t n -> p n t"))
             lat[pair, a] = latent
 
         def latent_quant(pair, a):
@@ -245,202 +230,156 @@ def tile_mla_pa_t_kernel(tc, x_bytes, x_scale, w_kv_down, w_kv_up, k_norm_w, fre
             nc.vector.quantize_mx(out=l_q[:].bitcast(FP8X4), scales=l_s[:], in_=lat[pair, a][:].rearrange("p n t -> p (n t)"))
             lq[pair, a], ls[pair, a] = l_q, l_s
 
-        def up_pass(bank, pair, a, part):
-            nc.tensor.matmul_mx(
-                out=bank[:],
-                lhsT=lq[pair, a][:].bitcast(FP8X4),
-                lhsT_scale=ls[pair, a][:],
-                rhs=wu_codes[:, part].bitcast(FP8X4),
-                rhs_scale=wu_scales[:, part],
-                start=True,
-                stop=True,
-            )
-
-        def up(pair):
+        def up(pair, a):
             if not live(pair):
                 return
-            for part, tag in ((0, "kb"), (1, "vb")):
-                for a in range(2):
-                    if (tag, pair, a) not in banks:
-                        bank = bank_tile(tag, [P, FEAT])
-                        banks[tag, pair, a] = bank
-                    up_pass(banks[tag, pair, a], pair, a, part)
-
-        def keep_warm(pair, count):
-            if not live(pair):
-                return
-            bank = bank_tile("kb", [P, FEAT])
-            for n in range(count):
+            for part, kind in enumerate("kv"):
+                bank = bank_tile("%s%d" % (kind, a), [P, FEAT])
                 nc.tensor.matmul_mx(
                     out=bank[:],
-                    lhsT=wd_codes[:, 0, 0, 0:P].bitcast(FP8X4),
-                    lhsT_scale=wd_scales[:, 0, 0, 0:P],
-                    rhs=wu_codes[:, 0].bitcast(FP8X4),
-                    rhs_scale=wu_scales[:, 0],
+                    lhsT=lq[pair, a][:].bitcast(FP8X4),
+                    lhsT_scale=ls[pair, a][:],
+                    rhs=wu_codes[:, part].bitcast(FP8X4),
+                    rhs_scale=wu_scales[:, part],
                     start=True,
                     stop=True,
                 )
-            banks["kb", pair, 0] = bank
+                banks[kind, pair, a] = bank
 
-        def norm(pair, a):
+        def square_sums(pair, a):
             if not live(pair):
                 return
-            squares = work.tile([P, H], F32, tag="squares", bufs=4, name="squares")
-            rstd = work.tile([P, H], F32, tag="rstd", bufs=4, name="rstd")
+            sums = work.tile([P, H], F32, tag="sums", bufs=4, name="sums")
             for h in range(H):
                 junk = work.tile([P, D], BF16, tag="junk", bufs=4, name="junk")
-                nc.scalar.activation(out=junk[:], in_=banks["kb", pair, a][:, D * h : D * (h + 1)], func=ACT.Square, accum_out=squares[:, h : h + 1])
-            nc.scalar.activation(out=rstd[:], in_=squares[:], func=ACT.Abs_reciprocal_sqrt, bias=EPS, scale=1.0 / D)
+                nc.scalar.activation(out=junk[:], in_=banks["k", pair, a][:, D * h : D * (h + 1)], func=ACT.Square, accum_out=sums[:, h : h + 1])
+            squares[pair, a] = sums
+
+        def inverse_rms(pair, a):
+            if not live(pair):
+                return
+            rstd = work.tile([P, H], F32, tag="rstd", bufs=4, name="rstd")
+            nc.scalar.activation(out=rstd[:], in_=squares[pair, a][:], func=ACT.Abs_reciprocal_sqrt, bias=EPS, scale=1.0 / D)
             rs[pair, a] = rstd
 
-        def store(out, tile, pair, a):
+        def store(out, tile, pair, first, last):
             b, s, h = pair // 4, pair // 2 % 2, pair % 2
             view = out[b].rearrange("(s p q) h d -> s p q (h d)", p=P, q=4)[s]
-            if pair == PAIRS - 1:
-                nc.sync.dma_start(out=view[:, 2 * h + a, :], in_=tile[:, a, :])
-            elif a == 1:
-                nc.sync.dma_start(out=view[:, 2 * h : 2 * h + 2, :], in_=tile[:])
+            nc.sync.dma_start(out=view[:, 2 * h + first : 2 * h + last, :], in_=tile.rearrange("p (a f) -> p a f", a=2)[:, first:last])
 
-        def values_out(pair, a, copy):
+        def values_out(pair, a):
             if not live(pair):
                 return
             if a == 0:
-                v_tile = work.tile([P, 2, FEAT], F32, tag="v_tile", bufs=4, name="v_tile")
+                v_tile = work.tile([P, 2 * FEAT], F32, tag="v_tile", name="v_tile")
                 vout[pair] = v_tile
-            copy(out=vout[pair][:, a, :], in_=banks["vb", pair, a][:])
-            store(out_1, vout[pair], pair, a)
+            nc.scalar.copy(out=vout[pair][:, FEAT * a : FEAT * (a + 1)], in_=banks["v", pair, a][:])
+            if pair == PAIRS - 1:
+                store(out_1, vout[pair][:], pair, a, a + 1)
+            elif a == 1:
+                store(out_1, vout[pair][:], pair, 0, 2)
 
-        def posted(pair, a):
-            return a == 0
-
-        def rotate(pair, a, first, last):
-            if not live(pair):
-                return
-            row = (2 * pair + a) % 8
-            if first == 0:
-                t1 = work.tile([P, H, D], F32, tag="t1", name="t1")
-                t2 = work.tile([P, H, 2, half], F32, tag="t2", name="t2")
-                products[pair, a] = t1, t2
-            t1, t2 = products[pair, a]
-            k = banks["kb", pair, a][:].rearrange("p (h d) -> p h d", h=H)
-            straight = table_a[:, row].rearrange("p j e -> p (j e)")
-            if posted(pair, a):
-                if first == 0:
-                    nc.vector.tensor_tensor(out=t1[:], in0=k, in1=straight.unsqueeze(1).broadcast_to([P, H, D]), op=ALU.mult)
-                if last == 8:
-                    nc.vector.tensor_tensor(
-                        out=t2[:].rearrange("p h e j -> p e h j"),
-                        in0=k.rearrange("p h (j e) -> p e h j", e=2)[:, ::-1],
-                        in1=table_b[:, row].unsqueeze(2).broadcast_to([P, 2, H, half]),
-                        op=ALU.mult,
-                    )
-                return
-            for n in range(first, last):
-                h = n // 2
-                if n % 2 == 0:
-                    nc.vector.scalar_tensor_tensor(out=t1[:, h], in0=k[:, h], scalar=rs[pair, a][:, h : h + 1], in1=straight, op0=ALU.mult, op1=ALU.mult)
-                else:
-                    nc.vector.scalar_tensor_tensor(
-                        out=t2[:, h], in0=k[:, h].rearrange("p (j e) -> p e j", e=2)[:, ::-1], scalar=rs[pair, a][:, h : h + 1],
-                        in1=table_b[:, row], op0=ALU.mult, op1=ALU.mult,
-                    )
-
-        def keys_out(pair, a, adder):
+        def rotate(pair, a):
             if not live(pair):
                 return
             if a == 0:
-                k_tile = work.tile([P, 2, FEAT], F32, tag="k_tile", bufs=4, name="k_tile")
-                kout[pair] = k_tile
-            t1, t2 = products[pair, a]
+                quads = work.tile([P, 2, H, D, 2], F32, tag="quads", name="quads")
+                products[pair] = quads
+            row = (2 * pair + a) % ROWS
+            for h in range(H):
+                nc.vector.scalar_tensor_tensor(
+                    out=products[pair][:, a, h],
+                    in0=banks["k", pair, a][:, D * h : D * (h + 1)].unsqueeze(2).broadcast_to([P, D, 2]),
+                    scalar=rs[pair, a][:, h : h + 1],
+                    in1=table[:, row].rearrange("p j e r -> p (j e) r"),
+                    op0=ALU.mult,
+                    op1=ALU.mult,
+                )
+
+        def keys_out(pair, first, last, adder):
+            if not live(pair):
+                return
+            keys = stages[(pair + 2) % STAGES]
+            quads = products[pair][:, first:last].rearrange("p a h (j e) r -> p (a h j) e r", e=2)
             adder.tensor_tensor(
-                out=kout[pair][:, a, :].rearrange("p (h j e) -> p h j e", h=H, e=2),
-                in0=t1[:].rearrange("p h (j e) -> p h j e", e=2),
-                in1=t2[:].rearrange("p h e j -> p h j e"),
+                out=keys[:, FEAT * first : FEAT * last].rearrange("p (n r) -> p n r", r=2),
+                in0=quads[:, :, 0, :],
+                in1=quads[:, :, 1, :],
                 op=ALU.add,
             )
+            store(out_0, keys[:], pair, first, last)
 
-        def post(pair, a):
-            if not live(pair):
-                return
-            if not posted(pair, a):
-                store(out_0, kout[pair], pair, a)
-                return
-            for h in range(H):
-                head = kout[pair][:, a, D * h : D * (h + 1)]
-                nc.scalar.activation(out=head, in_=head, func=ACT.Copy, scale=rs[pair, a][:, h : h + 1])
-            store(out_0, kout[pair], pair, a)
-
-        warm_up(WARM)
+        table_rows(0, ROWS)
         widen(0, 0, nc.vector.tensor_copy)
         widen(0, 1, nc.scalar.copy)
         turn(0, 0)
         turn(0, 1)
-        warm_up(2)
         widen(1, 0, nc.scalar.copy)
         widen(1, 1, nc.scalar.copy)
         x_out(0, 0)
         x_out(0, 1)
-        wd_turn(0, "lat")
-        warm_up(2)
-        wd_turn(1, "kb")
-        warm_up(2)
+        wd_turn(0, ("lat0", "lat1"))
+        wd_turn(1, ("k0", "k1"))
         turn(1, 0)
         turn(1, 1)
-        warm_up(1)
         wd_out(nc.scalar.copy, 0, 0)
         wd_out(nc.vector.tensor_copy, 0, 1)
         wd_out(nc.scalar.copy, 1, 0)
-        wd_out(nc.vector.tensor_copy, 1, 1)
+        wd_out(nc.scalar.copy, 1, 1)
         quant(0)
         wd_quant(0)
+        x_out(1, 0)
         wd_quant(1)
-        wu_turn(0, ("vb", "vb"))
+        wu_turn(0, ("v0", "v1"))
         down(0, 0)
         down(0, 1)
+        wu_turn(1, ("k0", "k1"))
         wu_out(nc.scalar.copy, 0, 0)
         wu_out(nc.scalar.copy, 0, 1)
-        premult(2, 0)
-        x_out(1, 0)
-        wu_turn(1, ("kb", "kb"))
         latent_out(0, 0)
-        latent_out(0, 1)
-        premult(2, 1)
         x_out(1, 1)
         wu_quant(0)
-        latent_quant(0, 0)
-        latent_quant(0, 1)
         wu_out(nc.scalar.copy, 1, 0)
         wu_out(nc.scalar.copy, 1, 1)
-        quant(1)
+        latent_out(0, 1)
+        latent_quant(0, 0)
+        premult(2, 0)
         wu_quant(1)
-        for pair in range(3, AHEAD + 1):
-            premult(pair, 0)
-            premult(pair, 1)
+        latent_quant(0, 1)
+        up(0, 0)
+        up(0, 1)
+        square_sums(0, 0)
+        values_out(0, 0)
+        inverse_rms(0, 0)
+        square_sums(0, 1)
+        premult(2, 1)
+        quant(1)
 
         for s in range(1, PAIRS + 1):
-            up(s - 1)
+            keys_out(s - 2, 0, 2, nc.gpsimd)
+            values_out(s - 1, 1)
+            inverse_rms(s - 1, 1)
             down(s, 0)
-            down(s, 1)
             turn(s + 1, 0)
+            down(s, 1)
             turn(s + 1, 1)
-            post(s - 2, 0)
-            post(s - 2, 1)
-            norm(s - 1, 0)
-            norm(s - 1, 1)
-            premult(s + AHEAD, 0)
-            premult(s + AHEAD, 1)
-            for a in range(2):
-                rotate(s - 1, a, 0, 8)
-                keys_out(s - 1, a, nc.vector if s == PAIRS and a == 1 else nc.gpsimd)
-            keep_warm(s, 2)
+            rotate(s - 1, 0)
+            if s == PAIRS:
+                keys_out(s - 1, 0, 1, nc.gpsimd)
+            rotate(s - 1, 1)
             latent_out(s, 0)
-            latent_out(s, 1)
             x_out(s + 1, 0)
+            latent_out(s, 1)
             x_out(s + 1, 1)
-            values_out(s - 1, 0, nc.scalar.copy)
-            values_out(s - 1, 1, nc.scalar.copy)
             latent_quant(s, 0)
+            up(s, 0)
+            premult(s + 2, 0)
             latent_quant(s, 1)
+            up(s, 1)
+            premult(s + 2, 1)
             quant(s + 1)
-        post(PAIRS - 1, 0)
-        post(PAIRS - 1, 1)
+            square_sums(s, 0)
+            values_out(s, 0)
+            inverse_rms(s, 0)
+            square_sums(s, 1)
+        keys_out(PAIRS - 1, 1, 2, nc.vector)

@@ -22,7 +22,6 @@ FP8X4 = mybir.dt.float8_e4m3fn_x4
 ACT = mybir.ActivationFunctionType
 ALU = mybir.AluOpType
 
-EARLY = 2
 STAGES = 3
 
 
@@ -38,8 +37,7 @@ def tile_mla_pa_t_kernel(tc, x_bytes, x_scale, w_kv_down, w_kv_up, k_norm_w, fre
         make_identity(nc, ident[:])
 
         scale = keep.tile([P, 2, 4], F32)
-        scale_row = keep.tile([P, C], F32)
-        trig = keep.tile([P, 3, ROWS * HALF], BF16)
+        trig = [keep.tile([P, 3, 4 * HALF], BF16, name="trig%d" % i) for i in range(2)]
         gain = keep.tile([P, D], BF16)
         wd_raw = [keep.tile([P, 2, C], BF16, align_bytes=64, name="wd_raw%d" % i) for i in range(2)]
         wu_raw = [keep.tile([P, 4, R], BF16, align_bytes=64, name="wu_raw%d" % i) for i in range(2)]
@@ -54,40 +52,48 @@ def tile_mla_pa_t_kernel(tc, x_bytes, x_scale, w_kv_down, w_kv_up, k_norm_w, fre
             nc.sync.dma_start(out=x_codes[:], in_=x_views[b][s][:, 2 * h : 2 * h + 2, :])
             x_tiles[pair] = x_codes
 
-        def load_trig(slot, table):
-            nc.sync.dma_start(out=trig[:, slot].rearrange("p (s q j) -> p s q j", s=2, q=4), in_=table.rearrange("(s p q) j -> p s q j", p=P, q=4))
+        def load_trig(queue, s):
+            for slot, angles in enumerate((freqs_cos, freqs_sin, freqs_cos)):
+                queue.dma_start(out=trig[s][:, slot], in_=angles.rearrange("(s p q) j -> s p (q j)", p=P, q=4)[s])
 
-        nc.scalar.dma_start(out=gain[:], in_=k_norm_w.partition_broadcast(P))
         load_x(0)
-        nc.sync.dma_start(out=scale[:], in_=x_scale[0, 0].rearrange("(g p t) -> p g t", p=P, t=4))
         nc.sync.dma_start(out=wd_raw[0][:], in_=wd_view[:, 0:2, :])
-        load_x(1)
+        nc.sync.dma_start(out=scale[:], in_=x_scale[0, 0].rearrange("(g p t) -> p g t", p=P, t=4))
         nc.sync.dma_start(out=wd_raw[1][:], in_=wd_view[:, 2:4, :])
-        load_trig(0, freqs_cos)
-        load_trig(1, freqs_sin)
-        load_trig(2, freqs_cos)
+        load_x(1)
         nc.sync.dma_start(out=wu_raw[0][:], in_=wu_view[:, 0:4, :])
-        nc.sync.dma_start(out=scale_row[:], in_=x_scale[0, 0].partition_broadcast(P))
+        nc.sync.dma_start(out=gain[:], in_=k_norm_w.partition_broadcast(P))
+        load_trig(nc.sync, 0)
         load_x(2)
         nc.sync.dma_start(out=wu_raw[1][:], in_=wu_view[:, 4:8, :])
+        load_trig(nc.sync, 1)
         for pair in range(3, PAIRS):
             load_x(pair)
 
         gain_pairs = gain[:].rearrange("p (j e) -> p j e", e=2)
-        gain_quads = keep.tile([P, HALF, 2, 2], F32)
-        nc.vector.tensor_copy(out=gain_quads[:], in_=gain_pairs.unsqueeze(3).broadcast_to([P, HALF, 2, 2]))
-        nc.vector.tensor_scalar(out=gain_quads[:, :, 1, 0], in0=gain_pairs[:, :, 1], scalar1=-1.0, scalar2=None, op0=ALU.mult)
-        table = keep.tile([P, ROWS, HALF, 2, 2], F32)
+        gain_quads = keep.tile([P, 2, HALF, 2], F32)
+        table_ends = keep.tile([P, 4, 2 * D], F32)
+        table_mid = keep.tile([P, 4 * 2 * D], F32, align_bytes=64)
 
-        def table_rows(first, last):
-            for row in range(first, last):
-                for e in range(2):
-                    nc.gpsimd.tensor_tensor(
-                        out=table[:, row, :, e, :],
-                        in0=trig[:, e : e + 2, HALF * row : HALF * (row + 1)].rearrange("p r j -> p j r"),
-                        in1=gain_quads[:, :, e, :],
-                        op=ALU.mult,
-                    )
+        def spread_gain():
+            nc.vector.tensor_copy(out=gain_quads[:], in_=gain_pairs.rearrange("p j e -> p e j").unsqueeze(3).broadcast_to([P, 2, HALF, 2]))
+            nc.vector.tensor_scalar(out=gain_quads[:, 1, :, 0], in0=gain_pairs[:, :, 1], scalar1=-1.0, scalar2=None, op0=ALU.mult)
+
+        def table(first, last):
+            if 2 <= first < 6:
+                return table_mid[:].rearrange("p (n c) -> p n c", n=4)[:, first - 2 : last - 2]
+            shift = 0 if first < 2 else 4
+            return table_ends[:, first - shift : last - shift]
+
+        def table_rows(engine, first, last):
+            rows = last - first
+            for e in range(2):
+                engine.tensor_tensor(
+                    out=table(first, last).rearrange("p n (e j r) -> p n e j r", e=2, r=2)[:, :, e],
+                    in0=trig[first // 4][:, e : e + 2, HALF * (first % 4) : HALF * (first % 4 + rows)].rearrange("p r (n j) -> p n j r", j=HALF),
+                    in1=gain_quads[:, e].unsqueeze(1).broadcast_to([P, rows, HALF, 2]),
+                    op=ALU.mult,
+                )
 
         wd_grouped = keep.tile([P, 2, 2, 256, 4], BF16, align_bytes=64)
         wu_grouped = keep.tile([P, 2, 512, 4], BF16, align_bytes=64)
@@ -98,6 +104,9 @@ def tile_mla_pa_t_kernel(tc, x_bytes, x_scale, w_kv_down, w_kv_up, k_norm_w, fre
         stages = [keep.tile([P, 2 * FEAT], F32, align_bytes=64, name="stage%d" % i) for i in range(STAGES)]
 
         banks = {}
+
+        def stage(pair):
+            return table_mid if pair == 1 else stages[pair % STAGES]
 
         def bank_tile(tag, shape):
             bank = psum.tile(shape, F32, tag=tag, name="bank")
@@ -128,7 +137,12 @@ def tile_mla_pa_t_kernel(tc, x_bytes, x_scale, w_kv_down, w_kv_up, k_norm_w, fre
             copy_words(copy, wd_grouped[:, th, g].rearrange("p n t -> p (n t)").bitcast(F32), banks["wd", th, g])
 
         def wu_out(copy, part, i):
-            copy_words(copy, wu_grouped[:, part, 256 * i : 256 * (i + 1)].rearrange("p n t -> p (n t)").bitcast(F32), banks["wu", part, i])
+            words = wu_grouped[:, part, 256 * i : 256 * (i + 1)].rearrange("p n t -> p (n t)").bitcast(F32)
+            bank = banks["wu", part, i]
+            if part == 1:
+                copy_words(copy, words, bank)
+            else:
+                copy(out=words.rearrange("p (h e j u) -> p h e j u", h=2, e=2, u=2), in_=bank[:].rearrange("p u (h j e) -> p h e j u", h=2, e=2))
 
         def wd_quant(th):
             nc.vector.quantize_mx(
@@ -149,40 +163,32 @@ def tile_mla_pa_t_kernel(tc, x_bytes, x_scale, w_kv_down, w_kv_up, k_norm_w, fre
             x_wide = work.tile([P, 2, C], BF16, tag="x_wide", align_bytes=64, name="x_wide")
             wide[pair] = x_wide
 
-        def widen(pair, a, copy):
+        def widen(pair, a, copy=nc.scalar.copy):
+            if not live(pair):
+                return
             if a == 0:
                 wide_tile(pair)
             copy(out=wide[pair][:, a, :], in_=x_tiles[pair][:, a, :].bitcast(FP8))
 
-        def premult(pair, a):
-            if not EARLY <= pair < PAIRS:
-                return
-            if a == 0:
-                wide_tile(pair)
-            nc.vector.tensor_tensor(out=wide[pair][:, a, :], in0=x_tiles[pair][:, a, :].bitcast(FP8), in1=scale_row[:], op=ALU.mult)
-
-        def turn(pair, g):
+        def turn(pair, a):
             if not live(pair):
                 return
-            bank = bank_tile("xt%d" % g, [P, 2, 256])
-            for a in range(2):
-                turn_words(bank[:, :, SUB * a : SUB * (a + 1)], wide[pair][:, a, :].bitcast(F32), 256 * g)
-            banks["xt", pair, g] = bank
+            bank = bank_tile("xt%d" % a, [P, 2, SUB, 2])
+            words = wide[pair][:, a, :].bitcast(F32)
+            for g in range(2):
+                for u in range(2):
+                    nc.tensor.transpose(bank[:, g, :, u], words[:, 256 * g + u : 256 * (g + 1) : 2], ident[:])
+            banks["xt", pair, a] = bank
 
-        def x_out(pair, g):
+        def x_out(pair, a):
             if not live(pair):
                 return
-            words = stages[pair % STAGES][:, FEAT * g : FEAT * (g + 1)]
-            bank = banks["xt", pair, g]
-            if pair >= EARLY:
-                copy_words(nc.scalar.copy, words, bank)
-            else:
-                nc.vector.tensor_tensor(
-                    out=words.bitcast(BF16).rearrange("p (n u e) -> p n u e", u=2, e=2),
-                    in0=bank[:].rearrange("p u n -> p (u n)").bitcast(BF16).rearrange("p (u n e) -> p n u e", u=2, e=2),
-                    in1=scale[:, g, :].rearrange("p (u e) -> p u e", u=2).unsqueeze(1).broadcast_to([P, 256, 2, 2]),
-                    op=ALU.mult,
-                )
+            nc.vector.tensor_tensor(
+                out=stage(pair)[:].bitcast(BF16).rearrange("p (g a n t) -> p a g n t", g=2, a=2, t=4)[:, a],
+                in0=banks["xt", pair, a][:].rearrange("p g n u -> p (g n u)").bitcast(BF16).rearrange("p (g n t) -> p g n t", g=2, t=4),
+                in1=scale[:].unsqueeze(2).broadcast_to([P, 2, SUB, 4]),
+                op=ALU.mult,
+            )
 
         def quant(pair):
             if not live(pair):
@@ -192,7 +198,7 @@ def tile_mla_pa_t_kernel(tc, x_bytes, x_scale, w_kv_down, w_kv_up, k_norm_w, fre
             nc.vector.quantize_mx(
                 out=x_q[:].rearrange("p g n -> p (g n)").bitcast(FP8X4),
                 scales=x_s[:].rearrange("p g n -> p (g n)"),
-                in_=stages[pair % STAGES][:].bitcast(BF16),
+                in_=stage(pair)[:].bitcast(BF16),
             )
             xq[pair], xs[pair] = x_q, x_s
 
@@ -215,11 +221,11 @@ def tile_mla_pa_t_kernel(tc, x_bytes, x_scale, w_kv_down, w_kv_up, k_norm_w, fre
                     )
             banks["lat", pair, a] = bank
 
-        def latent_out(pair, a):
+        def latent_out(pair, a, copy=nc.scalar.copy):
             if not live(pair):
                 return
             latent = work.tile([P, SUB, 4], BF16, tag="latent", bufs=4, align_bytes=64, name="latent")
-            nc.scalar.copy(out=latent[:], in_=banks["lat", pair, a][:].rearrange("p t n -> p n t"))
+            copy(out=latent[:], in_=banks["lat", pair, a][:].rearrange("p t n -> p n t"))
             lat[pair, a] = latent
 
         def latent_quant(pair, a):
@@ -230,10 +236,11 @@ def tile_mla_pa_t_kernel(tc, x_bytes, x_scale, w_kv_down, w_kv_up, k_norm_w, fre
             nc.vector.quantize_mx(out=l_q[:].bitcast(FP8X4), scales=l_s[:], in_=lat[pair, a][:].rearrange("p n t -> p (n t)"))
             lq[pair, a], ls[pair, a] = l_q, l_s
 
-        def up(pair, a):
+        def up(pair, a, kinds="kv"):
             if not live(pair):
                 return
-            for part, kind in enumerate("kv"):
+            for kind in kinds:
+                part = "kv".index(kind)
                 bank = bank_tile("%s%d" % (kind, a), [P, FEAT])
                 nc.tensor.matmul_mx(
                     out=bank[:],
@@ -267,13 +274,13 @@ def tile_mla_pa_t_kernel(tc, x_bytes, x_scale, w_kv_down, w_kv_up, k_norm_w, fre
             view = out[b].rearrange("(s p q) h d -> s p q (h d)", p=P, q=4)[s]
             nc.sync.dma_start(out=view[:, 2 * h + first : 2 * h + last, :], in_=tile.rearrange("p (a f) -> p a f", a=2)[:, first:last])
 
-        def values_out(pair, a):
+        def values_out(pair, a, copy=nc.scalar.copy):
             if not live(pair):
                 return
             if a == 0:
                 v_tile = work.tile([P, 2 * FEAT], F32, tag="v_tile", name="v_tile")
                 vout[pair] = v_tile
-            nc.scalar.copy(out=vout[pair][:, FEAT * a : FEAT * (a + 1)], in_=banks["v", pair, a][:])
+            copy(out=vout[pair][:, FEAT * a : FEAT * (a + 1)], in_=banks["v", pair, a][:])
             if pair == PAIRS - 1:
                 store(out_1, vout[pair][:], pair, a, a + 1)
             elif a == 1:
@@ -291,7 +298,7 @@ def tile_mla_pa_t_kernel(tc, x_bytes, x_scale, w_kv_down, w_kv_up, k_norm_w, fre
                     out=products[pair][:, a, h],
                     in0=banks["k", pair, a][:, D * h : D * (h + 1)].unsqueeze(2).broadcast_to([P, D, 2]),
                     scalar=rs[pair, a][:, h : h + 1],
-                    in1=table[:, row].rearrange("p j e r -> p (j e) r"),
+                    in1=table(row, row + 1).rearrange("p n (d r) -> p (n d) r", r=2),
                     op0=ALU.mult,
                     op1=ALU.mult,
                 )
@@ -300,86 +307,92 @@ def tile_mla_pa_t_kernel(tc, x_bytes, x_scale, w_kv_down, w_kv_up, k_norm_w, fre
             if not live(pair):
                 return
             keys = stages[(pair + 2) % STAGES]
-            quads = products[pair][:, first:last].rearrange("p a h (j e) r -> p (a h j) e r", e=2)
+            quads = products[pair][:, first:last].rearrange("p a h (e j) r -> p (a h) e (j r)", e=2)
             adder.tensor_tensor(
-                out=keys[:, FEAT * first : FEAT * last].rearrange("p (n r) -> p n r", r=2),
+                out=keys[:, FEAT * first : FEAT * last].rearrange("p (n d) -> p n d", d=D),
                 in0=quads[:, :, 0, :],
                 in1=quads[:, :, 1, :],
                 op=ALU.add,
             )
             store(out_0, keys[:], pair, first, last)
 
-        table_rows(0, ROWS)
         widen(0, 0, nc.vector.tensor_copy)
-        widen(0, 1, nc.scalar.copy)
+        widen(0, 1, nc.vector.tensor_copy)
         turn(0, 0)
         turn(0, 1)
-        widen(1, 0, nc.scalar.copy)
-        widen(1, 1, nc.scalar.copy)
-        x_out(0, 0)
-        x_out(0, 1)
         wd_turn(0, ("lat0", "lat1"))
         wd_turn(1, ("k0", "k1"))
-        turn(1, 0)
-        turn(1, 1)
+        x_out(0, 0)
+        x_out(0, 1)
         wd_out(nc.scalar.copy, 0, 0)
-        wd_out(nc.vector.tensor_copy, 0, 1)
+        wd_out(nc.scalar.copy, 0, 1)
+        widen(1, 0)
         wd_out(nc.scalar.copy, 1, 0)
         wd_out(nc.scalar.copy, 1, 1)
-        quant(0)
+        widen(1, 1)
         wd_quant(0)
-        x_out(1, 0)
+        quant(0)
         wd_quant(1)
         wu_turn(0, ("v0", "v1"))
         down(0, 0)
+        turn(1, 0)
         down(0, 1)
-        wu_turn(1, ("k0", "k1"))
-        wu_out(nc.scalar.copy, 0, 0)
+        turn(1, 1)
+        wu_out(nc.vector.tensor_copy, 0, 0)
         wu_out(nc.scalar.copy, 0, 1)
         latent_out(0, 0)
-        x_out(1, 1)
+        widen(2, 0)
+        latent_out(0, 1)
+        widen(2, 1)
+        spread_gain()
         wu_quant(0)
+        table_rows(nc.vector, 0, 2)
+        wu_turn(1, ("v0", "v1"))
+        x_out(1, 0)
+        latent_quant(0, 0)
+        x_out(1, 1)
+        latent_quant(0, 1)
+        up(0, 0, "k")
+        up(0, 1, "k")
+        turn(2, 0)
+        turn(2, 1)
         wu_out(nc.scalar.copy, 1, 0)
         wu_out(nc.scalar.copy, 1, 1)
-        latent_out(0, 1)
-        latent_quant(0, 0)
-        premult(2, 0)
+        widen(3, 0)
+        widen(3, 1)
+        table_rows(nc.vector, 6, 8)
         wu_quant(1)
-        latent_quant(0, 1)
-        up(0, 0)
-        up(0, 1)
-        square_sums(0, 0)
-        values_out(0, 0)
-        inverse_rms(0, 0)
-        square_sums(0, 1)
-        premult(2, 1)
         quant(1)
+        table_rows(nc.gpsimd, 2, 4)
+        table_rows(nc.gpsimd, 4, 6)
+        up(0, 0, "v")
 
         for s in range(1, PAIRS + 1):
             keys_out(s - 2, 0, 2, nc.gpsimd)
-            values_out(s - 1, 1)
-            inverse_rms(s - 1, 1)
             down(s, 0)
-            turn(s + 1, 0)
+            x_out(s + 1, 0)
+            turn(s + 2, 0)
+            up(s - 1, 1, "v")
             down(s, 1)
-            turn(s + 1, 1)
+            x_out(s + 1, 1)
+            turn(s + 2, 1)
+            square_sums(s - 1, 0)
+            values_out(s - 1, 0)
+            inverse_rms(s - 1, 0)
+            square_sums(s - 1, 1)
+            latent_out(s, 0)
+            inverse_rms(s - 1, 1)
+            values_out(s - 1, 1)
+            widen(s + 3, 0)
+            latent_out(s, 1)
+            widen(s + 3, 1)
             rotate(s - 1, 0)
             if s == PAIRS:
                 keys_out(s - 1, 0, 1, nc.gpsimd)
             rotate(s - 1, 1)
-            latent_out(s, 0)
-            x_out(s + 1, 0)
-            latent_out(s, 1)
-            x_out(s + 1, 1)
             latent_quant(s, 0)
             up(s, 0)
-            premult(s + 2, 0)
             latent_quant(s, 1)
-            up(s, 1)
-            premult(s + 2, 1)
+            up(s, 1, "k")
             quant(s + 1)
-            square_sums(s, 0)
-            values_out(s, 0)
-            inverse_rms(s, 0)
-            square_sums(s, 1)
         keys_out(PAIRS - 1, 1, 2, nc.vector)

@@ -33,11 +33,16 @@ def tile_mla_pa_t_kernel(tc, x_bytes, x_scale, w_kv_down, w_kv_up, k_norm_w, fre
         psum = ctx.enter_context(tc.psum_pool(name="psum", bufs=1))
         ctx.enter_context(tc.manual_schedule())
 
+        one = keep.tile([P, 1], F32)
+        nc.vector.memset(one[:], 1.0)
+        table_warm = keep.tile([P, 1], F32)
+        nc.scalar.activation(out=table_warm[:], in_=one[:], func=ACT.Abs_reciprocal_sqrt)
+
         ident = keep.tile([P, P], F32)
         make_identity(nc, ident[:])
 
         scale = keep.tile([P, 2, 4], F32)
-        trig = [keep.tile([P, 3, 4 * HALF], BF16, name="trig%d" % i) for i in range(2)]
+        trig = keep.tile([P, 3, ROWS * HALF], BF16)
         gain = keep.tile([P, D], BF16)
         wd_raw = [keep.tile([P, 2, C], BF16, align_bytes=64, name="wd_raw%d" % i) for i in range(2)]
         wu_raw = [keep.tile([P, 4, R], BF16, align_bytes=64, name="wu_raw%d" % i) for i in range(2)]
@@ -54,43 +59,43 @@ def tile_mla_pa_t_kernel(tc, x_bytes, x_scale, w_kv_down, w_kv_up, k_norm_w, fre
 
         def load_trig(queue, s):
             for slot, angles in enumerate((freqs_cos, freqs_sin, freqs_cos)):
-                queue.dma_start(out=trig[s][:, slot], in_=angles.rearrange("(s p q) j -> s p (q j)", p=P, q=4)[s])
+                queue.dma_start(out=trig[:, slot, 4 * HALF * s : 4 * HALF * (s + 1)], in_=angles.rearrange("(s p q) j -> s p (q j)", p=P, q=4)[s])
 
         load_x(0)
-        nc.sync.dma_start(out=wd_raw[0][:], in_=wd_view[:, 0:2, :])
         nc.sync.dma_start(out=scale[:], in_=x_scale[0, 0].rearrange("(g p t) -> p g t", p=P, t=4))
-        nc.sync.dma_start(out=wd_raw[1][:], in_=wd_view[:, 2:4, :])
+        nc.sync.dma_start(out=wd_raw[0][:], in_=wd_view[:, 0:2, :])
         load_x(1)
+        nc.sync.dma_start(out=wd_raw[1][:], in_=wd_view[:, 2:4, :])
+        load_x(2)
         nc.sync.dma_start(out=wu_raw[0][:], in_=wu_view[:, 0:4, :])
         nc.sync.dma_start(out=gain[:], in_=k_norm_w.partition_broadcast(P))
         load_trig(nc.sync, 0)
-        load_x(2)
+        load_x(3)
         nc.sync.dma_start(out=wu_raw[1][:], in_=wu_view[:, 4:8, :])
         load_trig(nc.sync, 1)
-        for pair in range(3, PAIRS):
+        for pair in range(4, PAIRS):
             load_x(pair)
 
         gain_pairs = gain[:].rearrange("p (j e) -> p j e", e=2)
         gain_quads = keep.tile([P, 2, HALF, 2], F32)
-        table_ends = keep.tile([P, 4, 2 * D], F32)
-        table_mid = keep.tile([P, 4 * 2 * D], F32, align_bytes=64)
+        table_first = keep.tile([P, 2, 2 * D], F32)
+        table_rest = keep.tile([P, (ROWS - 2) * 2 * D], F32, align_bytes=64)
 
         def spread_gain():
             nc.vector.tensor_copy(out=gain_quads[:], in_=gain_pairs.rearrange("p j e -> p e j").unsqueeze(3).broadcast_to([P, 2, HALF, 2]))
             nc.vector.tensor_scalar(out=gain_quads[:, 1, :, 0], in0=gain_pairs[:, :, 1], scalar1=-1.0, scalar2=None, op0=ALU.mult)
 
         def table(first, last):
-            if 2 <= first < 6:
-                return table_mid[:].rearrange("p (n c) -> p n c", n=4)[:, first - 2 : last - 2]
-            shift = 0 if first < 2 else 4
-            return table_ends[:, first - shift : last - shift]
+            if first < 2:
+                return table_first[:, first:last]
+            return table_rest[:].rearrange("p (n c) -> p n c", c=2 * D)[:, first - 2 : last - 2]
 
         def table_rows(engine, first, last):
             rows = last - first
             for e in range(2):
                 engine.tensor_tensor(
                     out=table(first, last).rearrange("p n (e j r) -> p n e j r", e=2, r=2)[:, :, e],
-                    in0=trig[first // 4][:, e : e + 2, HALF * (first % 4) : HALF * (first % 4 + rows)].rearrange("p r (n j) -> p n j r", j=HALF),
+                    in0=trig[:, e : e + 2, HALF * first : HALF * last].rearrange("p r (n j) -> p n j r", j=HALF),
                     in1=gain_quads[:, e].unsqueeze(1).broadcast_to([P, rows, HALF, 2]),
                     op=ALU.mult,
                 )
@@ -104,30 +109,41 @@ def tile_mla_pa_t_kernel(tc, x_bytes, x_scale, w_kv_down, w_kv_up, k_norm_w, fre
         stages = [keep.tile([P, 2 * FEAT], F32, align_bytes=64, name="stage%d" % i) for i in range(STAGES)]
 
         banks = {}
+        sorted_words = {}
 
         def stage(pair):
-            return table_mid if pair == 1 else stages[pair % STAGES]
+            return stages[pair % STAGES][:]
 
         def bank_tile(tag, shape):
             bank = psum.tile(shape, F32, tag=tag, name="bank")
             return bank
 
-        def turn_words(out, words, first):
+        def turn_words(out, words):
             for u in range(2):
-                nc.tensor.transpose(out[:, u], words[:, first + u : first + 256 : 2], ident[:])
+                nc.tensor.transpose(out[:, u], words[:, u], ident[:])
+
+        def sort_words(copy, key, raw):
+            words = keep.tile([P, 4, 2, P], F32, name="sorted_%s%d" % key)
+            copy(out=words[:], in_=raw[:].rearrange("p r k -> p (r k)").bitcast(F32).rearrange("p (c n u) -> p c u n", c=4, u=2))
+            sorted_words[key] = words[:]
+
+        def parity_view(key, raw):
+            if key in sorted_words:
+                return sorted_words[key]
+            return raw[:].rearrange("p r k -> p (r k)").bitcast(F32).rearrange("p (c n u) -> p c u n", c=4, u=2)
 
         def wd_turn(th, tags):
             for g in range(2):
                 bank = bank_tile(tags[g], [P, 2, 256])
                 for i in range(2):
-                    turn_words(bank[:, :, SUB * i : SUB * (i + 1)], wd_raw[th][:, i, :].bitcast(F32), 256 * g)
+                    turn_words(bank[:, :, SUB * i : SUB * (i + 1)], parity_view(("wd", th), wd_raw[th])[:, 2 * i + g])
                 banks["wd", th, g] = bank
 
         def wu_turn(part, tags):
             for i in range(2):
                 bank = bank_tile(tags[i], [P, 2, 256])
                 for j in range(2):
-                    turn_words(bank[:, :, SUB * j : SUB * (j + 1)], wu_raw[part][:, 2 * i + j, :].bitcast(F32), 0)
+                    turn_words(bank[:, :, SUB * j : SUB * (j + 1)], parity_view(("wu", part), wu_raw[part])[:, 2 * i + j])
                 banks["wu", part, i] = bank
 
         def copy_words(copy, words, bank):
@@ -160,7 +176,7 @@ def tile_mla_pa_t_kernel(tc, x_bytes, x_scale, w_kv_down, w_kv_up, k_norm_w, fre
             return 0 <= pair < PAIRS
 
         def wide_tile(pair):
-            x_wide = work.tile([P, 2, C], BF16, tag="x_wide", align_bytes=64, name="x_wide")
+            x_wide = work.tile([P, 2, C], BF16, tag="x_wide", bufs=4, align_bytes=64, name="x_wide")
             wide[pair] = x_wide
 
         def widen(pair, a, copy=nc.scalar.copy):
@@ -184,7 +200,7 @@ def tile_mla_pa_t_kernel(tc, x_bytes, x_scale, w_kv_down, w_kv_up, k_norm_w, fre
             if not live(pair):
                 return
             nc.vector.tensor_tensor(
-                out=stage(pair)[:].bitcast(BF16).rearrange("p (g a n t) -> p a g n t", g=2, a=2, t=4)[:, a],
+                out=stage(pair).bitcast(BF16).rearrange("p (g a n t) -> p a g n t", g=2, a=2, t=4)[:, a],
                 in0=banks["xt", pair, a][:].rearrange("p g n u -> p (g n u)").bitcast(BF16).rearrange("p (g n t) -> p g n t", g=2, t=4),
                 in1=scale[:].unsqueeze(2).broadcast_to([P, 2, SUB, 4]),
                 op=ALU.mult,
@@ -198,7 +214,7 @@ def tile_mla_pa_t_kernel(tc, x_bytes, x_scale, w_kv_down, w_kv_up, k_norm_w, fre
             nc.vector.quantize_mx(
                 out=x_q[:].rearrange("p g n -> p (g n)").bitcast(FP8X4),
                 scales=x_s[:].rearrange("p g n -> p (g n)"),
-                in_=stage(pair)[:].bitcast(BF16),
+                in_=stage(pair).bitcast(BF16),
             )
             xq[pair], xs[pair] = x_q, x_s
 
@@ -236,12 +252,12 @@ def tile_mla_pa_t_kernel(tc, x_bytes, x_scale, w_kv_down, w_kv_up, k_norm_w, fre
             nc.vector.quantize_mx(out=l_q[:].bitcast(FP8X4), scales=l_s[:], in_=lat[pair, a][:].rearrange("p n t -> p (n t)"))
             lq[pair, a], ls[pair, a] = l_q, l_s
 
-        def up(pair, a, kinds="kv"):
+        def up(pair, a, kinds="kv", tag=None):
             if not live(pair):
                 return
             for kind in kinds:
                 part = "kv".index(kind)
-                bank = bank_tile("%s%d" % (kind, a), [P, FEAT])
+                bank = bank_tile("%s%d" % (tag or kind, a), [P, FEAT])
                 nc.tensor.matmul_mx(
                     out=bank[:],
                     lhsT=lq[pair, a][:].bitcast(FP8X4),
@@ -281,7 +297,7 @@ def tile_mla_pa_t_kernel(tc, x_bytes, x_scale, w_kv_down, w_kv_up, k_norm_w, fre
                 v_tile = work.tile([P, 2 * FEAT], F32, tag="v_tile", name="v_tile")
                 vout[pair] = v_tile
             copy(out=vout[pair][:, FEAT * a : FEAT * (a + 1)], in_=banks["v", pair, a][:])
-            if pair == PAIRS - 1:
+            if pair >= PAIRS - 2:
                 store(out_1, vout[pair][:], pair, a, a + 1)
             elif a == 1:
                 store(out_1, vout[pair][:], pair, 0, 2)
@@ -317,58 +333,109 @@ def tile_mla_pa_t_kernel(tc, x_bytes, x_scale, w_kv_down, w_kv_up, k_norm_w, fre
             store(out_0, keys[:], pair, first, last)
 
         widen(0, 0, nc.vector.tensor_copy)
-        widen(0, 1, nc.vector.tensor_copy)
+        widen(0, 1)
         turn(0, 0)
         turn(0, 1)
         wd_turn(0, ("lat0", "lat1"))
-        wd_turn(1, ("k0", "k1"))
+        widen(1, 0)
+        widen(1, 1)
         x_out(0, 0)
+        turn(1, 0)
         x_out(0, 1)
+        turn(1, 1)
+        wd_turn(1, ("k0", "k1"))
         wd_out(nc.scalar.copy, 0, 0)
         wd_out(nc.scalar.copy, 0, 1)
-        widen(1, 0)
+        widen(2, 0)
+        widen(2, 1)
         wd_out(nc.scalar.copy, 1, 0)
         wd_out(nc.scalar.copy, 1, 1)
-        widen(1, 1)
-        wd_quant(0)
         quant(0)
+        x_out(1, 0)
+        turn(2, 0)
+        x_out(1, 1)
+        turn(2, 1)
+        wd_quant(0)
         wd_quant(1)
         wu_turn(0, ("v0", "v1"))
         down(0, 0)
-        turn(1, 0)
         down(0, 1)
-        turn(1, 1)
-        wu_out(nc.vector.tensor_copy, 0, 0)
+        x_out(2, 0)
+        x_out(2, 1)
+        widen(3, 0)
+        wu_out(nc.scalar.copy, 0, 0)
         wu_out(nc.scalar.copy, 0, 1)
+        widen(3, 1)
         latent_out(0, 0)
-        widen(2, 0)
         latent_out(0, 1)
-        widen(2, 1)
-        spread_gain()
+        quant(1)
         wu_quant(0)
-        table_rows(nc.vector, 0, 2)
-        wu_turn(1, ("v0", "v1"))
-        x_out(1, 0)
+        spread_gain()
         latent_quant(0, 0)
-        x_out(1, 1)
-        latent_quant(0, 1)
         up(0, 0, "k")
+        table_rows(nc.vector, 0, 2)
+        latent_quant(0, 1)
+        table_rows(nc.vector, 2, 4)
+        down(1, 0)
         up(0, 1, "k")
-        turn(2, 0)
-        turn(2, 1)
+        down(1, 1)
+        wu_turn(1, ("v0", "v1"))
+        turn(3, 0)
+        turn(3, 1)
+        square_sums(0, 0)
+        latent_out(1, 0)
+        inverse_rms(0, 0)
+        square_sums(0, 1)
+        latent_out(1, 1)
+        inverse_rms(0, 1)
         wu_out(nc.scalar.copy, 1, 0)
         wu_out(nc.scalar.copy, 1, 1)
-        widen(3, 0)
-        widen(3, 1)
-        table_rows(nc.vector, 6, 8)
+        rotate(0, 0)
+        rotate(0, 1)
+        latent_quant(1, 0)
+        up(1, 0, "k")
+        latent_quant(1, 1)
+        up(1, 1, "k")
         wu_quant(1)
-        quant(1)
-        table_rows(nc.gpsimd, 2, 4)
-        table_rows(nc.gpsimd, 4, 6)
         up(0, 0, "v")
+        up(0, 1, "v")
+        widen(4, 0)
+        widen(4, 1)
+        quant(2)
+        keys_out(0, 0, 2, nc.gpsimd)
+        table_rows(nc.gpsimd, 4, 6)
+        square_sums(1, 0)
+        values_out(0, 0)
+        inverse_rms(1, 0)
+        square_sums(1, 1)
+        values_out(0, 1)
+        inverse_rms(1, 1)
+        down(2, 0)
+        x_out(3, 0)
+        turn(4, 0)
+        up(1, 0, "v")
+        down(2, 1)
+        x_out(3, 1)
+        up(1, 1, "v")
+        turn(4, 1)
+        latent_out(2, 0)
+        values_out(1, 0)
+        latent_out(2, 1)
+        values_out(1, 1)
+        widen(5, 0)
+        widen(5, 1)
+        rotate(1, 0)
+        rotate(1, 1)
+        latent_quant(2, 0)
+        up(2, 0)
+        latent_quant(2, 1)
+        up(2, 1, "k")
+        quant(3)
 
-        for s in range(1, PAIRS + 1):
+        for s in range(3, PAIRS - 2):
             keys_out(s - 2, 0, 2, nc.gpsimd)
+            if s < 4:
+                table_rows(nc.gpsimd, 2 * s, 2 * s + 2)
             down(s, 0)
             x_out(s + 1, 0)
             turn(s + 2, 0)
@@ -383,16 +450,69 @@ def tile_mla_pa_t_kernel(tc, x_bytes, x_scale, w_kv_down, w_kv_up, k_norm_w, fre
             latent_out(s, 0)
             inverse_rms(s - 1, 1)
             values_out(s - 1, 1)
-            widen(s + 3, 0)
             latent_out(s, 1)
+            widen(s + 3, 0)
             widen(s + 3, 1)
             rotate(s - 1, 0)
-            if s == PAIRS:
-                keys_out(s - 1, 0, 1, nc.gpsimd)
             rotate(s - 1, 1)
             latent_quant(s, 0)
             up(s, 0)
             latent_quant(s, 1)
             up(s, 1, "k")
             quant(s + 1)
-        keys_out(PAIRS - 1, 1, 2, nc.vector)
+        third, second, last = PAIRS - 3, PAIRS - 2, PAIRS - 1
+        keys_out(third - 1, 0, 2, nc.gpsimd)
+        down(second, 0)
+        up(third, 1, "v")
+        down(second, 1)
+        x_out(last, 0)
+        x_out(last, 1)
+        square_sums(third, 0)
+        latent_out(second, 0)
+        inverse_rms(third, 0)
+        square_sums(third, 1)
+        latent_out(second, 1)
+        inverse_rms(third, 1)
+        values_out(third, 0)
+        values_out(third, 1)
+        rotate(third, 0)
+        latent_quant(second, 0)
+        latent_quant(second, 1)
+        quant(last)
+        up(second, 0, "k", "xt")
+        up(second, 1, "k", "xt")
+        up(second, 0, "v")
+        down(last, 0)
+        down(last, 1)
+        up(second, 1, "v")
+        rotate(third, 1)
+        keys_out(third, 0, 1, nc.gpsimd)
+        square_sums(second, 0)
+        latent_out(last, 0)
+        inverse_rms(second, 0)
+        latent_out(last, 1)
+        square_sums(second, 1)
+        values_out(second, 0, nc.vector.tensor_copy)
+        keys_out(third, 1, 2, nc.vector)
+        latent_quant(last, 0)
+        up(last, 0, "k")
+        latent_quant(last, 1)
+        up(last, 1, "k")
+        up(last, 0, "v", "lat")
+        up(last, 1, "v", "lat")
+        inverse_rms(second, 1)
+        square_sums(last, 0)
+        values_out(second, 1)
+        inverse_rms(last, 0)
+        rotate(second, 0)
+        keys_out(second, 0, 1, nc.gpsimd)
+        square_sums(last, 1)
+        values_out(last, 0)
+        inverse_rms(last, 1)
+        rotate(second, 1)
+        keys_out(second, 1, 2, nc.gpsimd)
+        values_out(last, 1)
+        rotate(last, 0)
+        rotate(last, 1)
+        keys_out(last, 0, 1, nc.vector)
+        keys_out(last, 1, 2, nc.vector)

@@ -240,8 +240,12 @@ def tile_mla_pa_t_kernel(tc, x_bytes, x_scale, w_kv_down, w_kv_up, k_norm_w, fre
         def latent_out(pair, a, copy=nc.scalar.copy):
             if not live(pair):
                 return
-            latent = work.tile([P, SUB, 4], BF16, tag="latent", bufs=4, align_bytes=64, name="latent")
-            copy(out=latent[:], in_=banks["lat", pair, a][:].rearrange("p t n -> p n t"))
+            if pair == 0:
+                latent = table(4 + a, 5 + a).rearrange("p o c -> p (o c)").bitcast(BF16).rearrange("p (n t) -> p n t", t=4)
+            else:
+                latent_tile = work.tile([P, SUB, 4], BF16, tag="latent", bufs=4, align_bytes=64, name="latent")
+                latent = latent_tile[:]
+            copy(out=latent, in_=banks["lat", pair, a][:].rearrange("p t n -> p n t"))
             lat[pair, a] = latent
 
         def latent_quant(pair, a):
@@ -249,7 +253,7 @@ def tile_mla_pa_t_kernel(tc, x_bytes, x_scale, w_kv_down, w_kv_up, k_norm_w, fre
                 return
             l_q = work.tile([P, SUB], U32, tag="l_q", bufs=4, align_bytes=64, name="l_q")
             l_s = work.tile([P, SUB], U8, tag="l_s", bufs=4, align_bytes=64, name="l_s")
-            nc.vector.quantize_mx(out=l_q[:].bitcast(FP8X4), scales=l_s[:], in_=lat[pair, a][:].rearrange("p n t -> p (n t)"))
+            nc.vector.quantize_mx(out=l_q[:].bitcast(FP8X4), scales=l_s[:], in_=lat[pair, a].rearrange("p n t -> p (n t)"))
             lq[pair, a], ls[pair, a] = l_q, l_s
 
         def up(pair, a, kinds="kv", tag=None):
@@ -269,14 +273,15 @@ def tile_mla_pa_t_kernel(tc, x_bytes, x_scale, w_kv_down, w_kv_up, k_norm_w, fre
                 )
                 banks[kind, pair, a] = bank
 
-        def square_sums(pair, a):
+        def square_sums(pair, a, first=0, last=H):
             if not live(pair):
                 return
-            sums = work.tile([P, H], F32, tag="sums", bufs=4, name="sums")
-            for h in range(H):
+            if first == 0:
+                sums = work.tile([P, H], F32, tag="sums", bufs=4, name="sums")
+                squares[pair, a] = sums
+            for h in range(first, last):
                 junk = work.tile([P, D], BF16, tag="junk", bufs=4, name="junk")
-                nc.scalar.activation(out=junk[:], in_=banks["k", pair, a][:, D * h : D * (h + 1)], func=ACT.Square, accum_out=sums[:, h : h + 1])
-            squares[pair, a] = sums
+                nc.scalar.activation(out=junk[:], in_=banks["k", pair, a][:, D * h : D * (h + 1)], func=ACT.Square, accum_out=squares[pair, a][:, h : h + 1])
 
         def inverse_rms(pair, a):
             if not live(pair):
@@ -374,8 +379,9 @@ def tile_mla_pa_t_kernel(tc, x_bytes, x_scale, w_kv_down, w_kv_up, k_norm_w, fre
         latent_quant(0, 0)
         up(0, 0, "k")
         table_rows(nc.vector, 0, 2)
-        latent_quant(0, 1)
         table_rows(nc.vector, 2, 4)
+        latent_quant(0, 1)
+        table_rows(nc.gpsimd, 4, 8)
         down(1, 0)
         up(0, 1, "k")
         down(1, 1)
@@ -383,11 +389,12 @@ def tile_mla_pa_t_kernel(tc, x_bytes, x_scale, w_kv_down, w_kv_up, k_norm_w, fre
         turn(3, 0)
         turn(3, 1)
         square_sums(0, 0)
-        latent_out(1, 0)
+        square_sums(0, 1, 0, 1)
         inverse_rms(0, 0)
-        square_sums(0, 1)
-        latent_out(1, 1)
+        square_sums(0, 1, 1, H)
+        latent_out(1, 0)
         inverse_rms(0, 1)
+        latent_out(1, 1)
         wu_out(nc.scalar.copy, 1, 0)
         wu_out(nc.scalar.copy, 1, 1)
         rotate(0, 0)
@@ -403,13 +410,13 @@ def tile_mla_pa_t_kernel(tc, x_bytes, x_scale, w_kv_down, w_kv_up, k_norm_w, fre
         widen(4, 1)
         quant(2)
         keys_out(0, 0, 2, nc.gpsimd)
-        table_rows(nc.gpsimd, 4, 6)
         square_sums(1, 0)
-        values_out(0, 0)
+        square_sums(1, 1, 0, 1)
         inverse_rms(1, 0)
-        square_sums(1, 1)
-        values_out(0, 1)
+        square_sums(1, 1, 1, H)
+        values_out(0, 0)
         inverse_rms(1, 1)
+        values_out(0, 1)
         down(2, 0)
         x_out(3, 0)
         turn(4, 0)
@@ -434,23 +441,22 @@ def tile_mla_pa_t_kernel(tc, x_bytes, x_scale, w_kv_down, w_kv_up, k_norm_w, fre
 
         for s in range(3, PAIRS - 2):
             keys_out(s - 2, 0, 2, nc.gpsimd)
-            if s < 4:
-                table_rows(nc.gpsimd, 2 * s, 2 * s + 2)
             down(s, 0)
             x_out(s + 1, 0)
             turn(s + 2, 0)
-            up(s - 1, 1, "v")
             down(s, 1)
+            up(s - 1, 1, "v")
             x_out(s + 1, 1)
             turn(s + 2, 1)
             square_sums(s - 1, 0)
-            values_out(s - 1, 0)
+            square_sums(s - 1, 1, 0, 1)
             inverse_rms(s - 1, 0)
-            square_sums(s - 1, 1)
+            square_sums(s - 1, 1, 1, H)
             latent_out(s, 0)
             inverse_rms(s - 1, 1)
-            values_out(s - 1, 1)
+            values_out(s - 1, 0)
             latent_out(s, 1)
+            values_out(s - 1, 1)
             widen(s + 3, 0)
             widen(s + 3, 1)
             rotate(s - 1, 0)

@@ -22,6 +22,8 @@ FP8X4 = mybir.dt.float8_e4m3fn_x4
 ACT = mybir.ActivationFunctionType
 ALU = mybir.AluOpType
 
+FIRST_SHARED = 5
+SHARE = 2
 STAGES = 3
 
 
@@ -42,6 +44,7 @@ def tile_mla_pa_t_kernel(tc, x_bytes, x_scale, w_kv_down, w_kv_up, k_norm_w, fre
         make_identity(nc, ident[:])
 
         scale = keep.tile([P, 2, 4], F32)
+        scale_row = keep.tile([P, 512], F32)
         trig = keep.tile([P, 3, ROWS * HALF], BF16)
         gain = keep.tile([P, D], BF16)
         wd_raw = [keep.tile([P, 2, C], BF16, align_bytes=64, name="wd_raw%d" % i) for i in range(2)]
@@ -73,7 +76,9 @@ def tile_mla_pa_t_kernel(tc, x_bytes, x_scale, w_kv_down, w_kv_up, k_norm_w, fre
         load_x(3)
         nc.sync.dma_start(out=wu_raw[1][:], in_=wu_view[:, 4:8, :])
         load_trig(nc.sync, 1)
-        for pair in range(4, PAIRS):
+        load_x(4)
+        nc.sync.dma_start(out=scale_row[:], in_=x_scale[0, 0, 0:512].partition_broadcast(P))
+        for pair in range(5, PAIRS):
             load_x(pair)
 
         gain_pairs = gain[:].rearrange("p (j e) -> p j e", e=2)
@@ -108,8 +113,12 @@ def tile_mla_pa_t_kernel(tc, x_bytes, x_scale, w_kv_down, w_kv_up, k_norm_w, fre
         wu_scales = keep.tile([P, 2, 512], U8, align_bytes=64)
         stages = [keep.tile([P, 2 * FEAT], F32, align_bytes=64, name="stage%d" % i) for i in range(STAGES)]
 
+        latents = [[keep.tile([P, SUB, 4], BF16, align_bytes=64, name="latent%d%d" % (a, i)) for i in range(2)] for a in range(2)]
         banks = {}
         sorted_words = {}
+
+        def shared(pair):
+            return FIRST_SHARED <= pair < PAIRS and pair % SHARE != 0
 
         def stage(pair):
             return stages[pair % STAGES][:]
@@ -182,29 +191,41 @@ def tile_mla_pa_t_kernel(tc, x_bytes, x_scale, w_kv_down, w_kv_up, k_norm_w, fre
         def widen(pair, a, copy=nc.scalar.copy):
             if not live(pair):
                 return
-            if a == 0:
+            if pair not in wide:
                 wide_tile(pair)
             copy(out=wide[pair][:, a, :], in_=x_tiles[pair][:, a, :].bitcast(FP8))
+
+        def scaled(pair):
+            return latents[1][(pair - 3) % 2][:].rearrange("p n t -> p (n t)")
+
+        def premult(pair):
+            if shared(pair):
+                nc.gpsimd.tensor_tensor(out=scaled(pair), in0=wide[pair][:, 1, 0:512], in1=scale_row[:], op=ALU.mult)
 
         def turn(pair, a):
             if not live(pair):
                 return
             bank = bank_tile("xt%d" % a, [P, 2, SUB, 2])
-            words = wide[pair][:, a, :].bitcast(F32)
             for g in range(2):
+                rows = scaled(pair) if shared(pair) and (a, g) == (1, 0) else wide[pair][:, a, 512 * g : 512 * (g + 1)]
                 for u in range(2):
-                    nc.tensor.transpose(bank[:, g, :, u], words[:, 256 * g + u : 256 * (g + 1) : 2], ident[:])
+                    nc.tensor.transpose(bank[:, g, :, u], rows.bitcast(F32)[:, u:256:2], ident[:])
             banks["xt", pair, a] = bank
 
         def x_out(pair, a):
             if not live(pair):
                 return
+            first = 1 if shared(pair) and a == 1 else 0
             nc.vector.tensor_tensor(
-                out=stage(pair).bitcast(BF16).rearrange("p (g a n t) -> p a g n t", g=2, a=2, t=4)[:, a],
-                in0=banks["xt", pair, a][:].rearrange("p g n u -> p (g n u)").bitcast(BF16).rearrange("p (g n t) -> p g n t", g=2, t=4),
-                in1=scale[:].unsqueeze(2).broadcast_to([P, 2, SUB, 4]),
+                out=stage(pair).bitcast(BF16).rearrange("p (g a n t) -> p a g n t", g=2, a=2, t=4)[:, a, first:],
+                in0=banks["xt", pair, a][:].rearrange("p g n u -> p (g n u)").bitcast(BF16).rearrange("p (g n t) -> p g n t", g=2, t=4)[:, first:],
+                in1=scale[:, first:].unsqueeze(2).broadcast_to([P, 2 - first, SUB, 4]),
                 op=ALU.mult,
             )
+
+        def words_out(pair, copy=nc.scalar.copy):
+            if shared(pair):
+                copy(out=stage(pair)[:, 256:512], in_=banks["xt", pair, 1][:, 0].rearrange("p n u -> p (n u)"))
 
         def quant(pair):
             if not live(pair):
@@ -243,8 +264,7 @@ def tile_mla_pa_t_kernel(tc, x_bytes, x_scale, w_kv_down, w_kv_up, k_norm_w, fre
             if pair == 0:
                 latent = table(4 + a, 5 + a).rearrange("p o c -> p (o c)").bitcast(BF16).rearrange("p (n t) -> p n t", t=4)
             else:
-                latent_tile = work.tile([P, SUB, 4], BF16, tag="latent", bufs=4, align_bytes=64, name="latent")
-                latent = latent_tile[:]
+                latent = latents[a][pair % 2][:]
             copy(out=latent, in_=banks["lat", pair, a][:].rearrange("p t n -> p n t"))
             lat[pair, a] = latent
 
@@ -440,6 +460,7 @@ def tile_mla_pa_t_kernel(tc, x_bytes, x_scale, w_kv_down, w_kv_up, k_norm_w, fre
         quant(3)
 
         for s in range(3, PAIRS - 2):
+            premult(s + 2)
             keys_out(s - 2, 0, 2, nc.gpsimd)
             down(s, 0)
             x_out(s + 1, 0)
@@ -447,18 +468,19 @@ def tile_mla_pa_t_kernel(tc, x_bytes, x_scale, w_kv_down, w_kv_up, k_norm_w, fre
             down(s, 1)
             up(s - 1, 1, "v")
             x_out(s + 1, 1)
-            turn(s + 2, 1)
             square_sums(s - 1, 0)
             square_sums(s - 1, 1, 0, 1)
             inverse_rms(s - 1, 0)
             square_sums(s - 1, 1, 1, H)
             latent_out(s, 0)
             inverse_rms(s - 1, 1)
+            words_out(s + 1)
+            turn(s + 2, 1)
             values_out(s - 1, 0)
             latent_out(s, 1)
             values_out(s - 1, 1)
-            widen(s + 3, 0)
             widen(s + 3, 1)
+            widen(s + 3, 0)
             rotate(s - 1, 0)
             rotate(s - 1, 1)
             latent_quant(s, 0)
@@ -477,6 +499,7 @@ def tile_mla_pa_t_kernel(tc, x_bytes, x_scale, w_kv_down, w_kv_up, k_norm_w, fre
         latent_out(second, 0)
         inverse_rms(third, 0)
         square_sums(third, 1)
+        words_out(last)
         latent_out(second, 1)
         inverse_rms(third, 1)
         values_out(third, 0)

@@ -261,10 +261,7 @@ def tile_mla_pa_t_kernel(tc, x_bytes, x_scale, w_kv_down, w_kv_up, k_norm_w, fre
         def latent_out(pair, a, copy=nc.scalar.copy):
             if not live(pair):
                 return
-            if pair == 0:
-                latent = table(4 + a, 5 + a).rearrange("p o c -> p (o c)").bitcast(BF16).rearrange("p (n t) -> p n t", t=4)
-            else:
-                latent = latents[a][pair % 2][:]
+            latent = latents[a][pair % 2][:]
             copy(out=latent, in_=banks["lat", pair, a][:].rearrange("p t n -> p n t"))
             lat[pair, a] = latent
 
@@ -399,9 +396,9 @@ def tile_mla_pa_t_kernel(tc, x_bytes, x_scale, w_kv_down, w_kv_up, k_norm_w, fre
         latent_quant(0, 0)
         up(0, 0, "k")
         table_rows(nc.vector, 0, 2)
-        table_rows(nc.vector, 2, 4)
         latent_quant(0, 1)
-        table_rows(nc.gpsimd, 4, 8)
+        table_rows(nc.vector, 2, 4)
+        table_rows(nc.vector, 4, 8)
         down(1, 0)
         up(0, 1, "k")
         down(1, 1)

@@ -23,7 +23,6 @@ ACT = mybir.ActivationFunctionType
 ALU = mybir.AluOpType
 
 FIRST_SHARED = 5
-SHARE = 2
 STAGES = 3
 
 
@@ -118,7 +117,7 @@ def tile_mla_pa_t_kernel(tc, x_bytes, x_scale, w_kv_down, w_kv_up, k_norm_w, fre
         sorted_words = {}
 
         def shared(pair):
-            return FIRST_SHARED <= pair < PAIRS and pair % SHARE != 0
+            return FIRST_SHARED <= pair < PAIRS
 
         def stage(pair):
             return stages[pair % STAGES][:]
@@ -446,8 +445,8 @@ def tile_mla_pa_t_kernel(tc, x_bytes, x_scale, w_kv_down, w_kv_up, k_norm_w, fre
         values_out(1, 0)
         latent_out(2, 1)
         values_out(1, 1)
-        widen(5, 0)
         widen(5, 1)
+        widen(5, 0)
         rotate(1, 0)
         rotate(1, 1)
         latent_quant(2, 0)
@@ -465,18 +464,18 @@ def tile_mla_pa_t_kernel(tc, x_bytes, x_scale, w_kv_down, w_kv_up, k_norm_w, fre
             down(s, 1)
             up(s - 1, 1, "v")
             x_out(s + 1, 1)
+            words_out(s + 1, nc.vector.tensor_copy)
+            turn(s + 2, 1)
             square_sums(s - 1, 0)
             square_sums(s - 1, 1, 0, 1)
             inverse_rms(s - 1, 0)
             square_sums(s - 1, 1, 1, H)
             latent_out(s, 0)
             inverse_rms(s - 1, 1)
-            words_out(s + 1)
-            turn(s + 2, 1)
             values_out(s - 1, 0)
             latent_out(s, 1)
-            values_out(s - 1, 1)
             widen(s + 3, 1)
+            values_out(s - 1, 1)
             widen(s + 3, 0)
             rotate(s - 1, 0)
             rotate(s - 1, 1)
@@ -492,14 +491,15 @@ def tile_mla_pa_t_kernel(tc, x_bytes, x_scale, w_kv_down, w_kv_up, k_norm_w, fre
         down(second, 1)
         x_out(last, 0)
         x_out(last, 1)
+        words_out(last, nc.vector.tensor_copy)
         square_sums(third, 0)
-        latent_out(second, 0)
+        square_sums(third, 1, 0, 1)
         inverse_rms(third, 0)
-        square_sums(third, 1)
-        words_out(last)
+        latent_out(second, 0)
         latent_out(second, 1)
-        inverse_rms(third, 1)
+        square_sums(third, 1, 1, H)
         values_out(third, 0)
+        inverse_rms(third, 1)
         values_out(third, 1)
         rotate(third, 0)
         latent_quant(second, 0)

@@ -8,6 +8,8 @@ EPS = 1e-6
 P = 128
 SUB = 128
 PAIRS = B * T // (2 * SUB)
+PASS = 512
+WORDS = PASS // 2
 FEAT = H * D
 HALF = D // 2
 ROWS = T // P
@@ -22,8 +24,11 @@ FP8X4 = mybir.dt.float8_e4m3fn_x4
 ACT = mybir.ActivationFunctionType
 ALU = mybir.AluOpType
 
-FIRST_SHARED = 5
+FIRST_STEP = 3
+FIRST_PRESCALED = FIRST_STEP + 2
 STAGES = 3
+WIDE_BUFS = 4
+SMALL_BUFS = 4
 
 
 def tile_mla_pa_t_kernel(tc, x_bytes, x_scale, w_kv_down, w_kv_up, k_norm_w, freqs_cos, freqs_sin, out_0, out_1):
@@ -43,130 +48,121 @@ def tile_mla_pa_t_kernel(tc, x_bytes, x_scale, w_kv_down, w_kv_up, k_norm_w, fre
         make_identity(nc, ident[:])
 
         scale = keep.tile([P, 2, 4], F32)
-        scale_row = keep.tile([P, 512], F32)
-        trig = keep.tile([P, 3, ROWS * HALF], BF16)
-        gain = keep.tile([P, D], BF16)
-        wd_raw = [keep.tile([P, 2, C], BF16, align_bytes=64, name="wd_raw%d" % i) for i in range(2)]
-        wu_raw = [keep.tile([P, 4, R], BF16, align_bytes=64, name="wu_raw%d" % i) for i in range(2)]
+        scale_row = keep.tile([P, PASS], F32)
+        trig = [keep.tile([P, 2, 4 * HALF], BF16, name="trig%d" % s) for s in range(2)]
+        gain_row = keep.tile([P, D], BF16)
+        nc.vector.memset(gain_row[:], 0.0)
+        ones = keep.tile([P, P], BF16)
+        nc.vector.memset(ones[:], 1.0)
+        wd_raw = [keep.tile([P, 2, C], BF16, align_bytes=64, name="wd_raw%d" % th) for th in range(2)]
+        wu_raw = [keep.tile([P, 4, R], BF16, align_bytes=64, name="wu_raw%d" % part) for part in range(2)]
         wd_view = w_kv_down.rearrange("(m t) k -> m t k", t=4)
         wu_view = w_kv_up.rearrange("(c m) r -> m c r", m=P)
-        x_views = [x_bytes[b].rearrange("(s p q) k -> s p q k", p=P, q=4) for b in range(B)]
         x_tiles = {}
 
-        def load_x(pair):
-            b, s, h = pair // 4, pair // 2 % 2, pair % 2
-            x_codes = work.tile([P, 2, C], U8, tag="x_codes", bufs=PAIRS, align_bytes=64, name="x_codes")
-            nc.sync.dma_start(out=x_codes[:], in_=x_views[b][s][:, 2 * h : 2 * h + 2, :])
-            x_tiles[pair] = x_codes
+        def pair_rows(tensor, pair, first, last):
+            b, s, q = pair // 4, pair // 2 % 2, 2 * (pair % 2)
+            return tensor[b].rearrange("(s p q) f -> s p q f", p=P, q=4)[s][:, q + first : q + last, :]
 
-        def load_trig(queue, s):
-            for slot, angles in enumerate((freqs_cos, freqs_sin, freqs_cos)):
-                queue.dma_start(out=trig[:, slot, 4 * HALF * s : 4 * HALF * (s + 1)], in_=angles.rearrange("(s p q) j -> s p (q j)", p=P, q=4)[s])
+        def load_x(pair, first=0, last=2):
+            if first == 0:
+                x_codes = work.tile([P, 2, C], U8, tag="x_codes", bufs=PAIRS, align_bytes=64, name="x_codes")
+                x_tiles[pair] = x_codes
+            nc.sync.dma_start(out=x_tiles[pair][:, first:last], in_=pair_rows(x_bytes, pair, first, last))
 
-        load_x(0)
+        def load_trig(s):
+            for slot, angles in enumerate((freqs_cos, freqs_sin)):
+                nc.sync.dma_start(out=trig[s][:, slot], in_=angles.rearrange("(s p q) j -> s p (q j)", p=P, q=4)[s])
+
+        load_x(0, 0, 1)
         nc.sync.dma_start(out=scale[:], in_=x_scale[0, 0].rearrange("(g p t) -> p g t", p=P, t=4))
+        load_x(0, 1, 2)
         nc.sync.dma_start(out=wd_raw[0][:], in_=wd_view[:, 0:2, :])
         load_x(1)
         nc.sync.dma_start(out=wd_raw[1][:], in_=wd_view[:, 2:4, :])
+        nc.sync.dma_start(out=gain_row[0:1, :], in_=k_norm_w.unsqueeze(0))
         load_x(2)
         nc.sync.dma_start(out=wu_raw[0][:], in_=wu_view[:, 0:4, :])
-        nc.sync.dma_start(out=gain[:], in_=k_norm_w.partition_broadcast(P))
-        load_trig(nc.sync, 0)
         load_x(3)
+        load_trig(0)
         nc.sync.dma_start(out=wu_raw[1][:], in_=wu_view[:, 4:8, :])
-        load_trig(nc.sync, 1)
+        load_trig(1)
         load_x(4)
-        nc.sync.dma_start(out=scale_row[:], in_=x_scale[0, 0, 0:512].partition_broadcast(P))
-        for pair in range(5, PAIRS):
+        load_x(FIRST_PRESCALED)
+        nc.sync.dma_start(out=scale_row[:], in_=x_scale[0, 0, 0:PASS].partition_broadcast(P))
+        for pair in range(FIRST_PRESCALED + 1, PAIRS):
             load_x(pair)
 
-        gain_pairs = gain[:].rearrange("p (j e) -> p j e", e=2)
-        gain_quads = keep.tile([P, 2, HALF, 2], F32)
-        table_first = keep.tile([P, 2, 2 * D], F32)
-        table_rest = keep.tile([P, (ROWS - 2) * 2 * D], F32, align_bytes=64)
-
-        def spread_gain():
-            nc.vector.tensor_copy(out=gain_quads[:], in_=gain_pairs.rearrange("p j e -> p e j").unsqueeze(3).broadcast_to([P, 2, HALF, 2]))
-            nc.vector.tensor_scalar(out=gain_quads[:, 1, :, 0], in0=gain_pairs[:, :, 1], scalar1=-1.0, scalar2=None, op0=ALU.mult)
-
-        def table(first, last):
-            if first < 2:
-                return table_first[:, first:last]
-            return table_rest[:].rearrange("p (n c) -> p n c", c=2 * D)[:, first - 2 : last - 2]
-
-        def table_rows(engine, first, last):
-            rows = last - first
-            for e in range(2):
-                engine.tensor_tensor(
-                    out=table(first, last).rearrange("p n (e j r) -> p n e j r", e=2, r=2)[:, :, e],
-                    in0=trig[:, e : e + 2, HALF * first : HALF * last].rearrange("p r (n j) -> p n j r", j=HALF),
-                    in1=gain_quads[:, e].unsqueeze(1).broadcast_to([P, rows, HALF, 2]),
-                    op=ALU.mult,
-                )
-
-        wd_grouped = keep.tile([P, 2, 2, 256, 4], BF16, align_bytes=64)
-        wu_grouped = keep.tile([P, 2, 512, 4], BF16, align_bytes=64)
-        wd_codes = keep.tile([P, 2, 2, 256], U32, align_bytes=64)
-        wd_scales = keep.tile([P, 2, 2, 256], U8, align_bytes=64)
-        wu_codes = keep.tile([P, 2, 512], U32, align_bytes=64)
-        wu_scales = keep.tile([P, 2, 512], U8, align_bytes=64)
-        stages = [keep.tile([P, 2 * FEAT], F32, align_bytes=64, name="stage%d" % i) for i in range(STAGES)]
-
-        latents = [[keep.tile([P, SUB, 4], BF16, align_bytes=64, name="latent%d%d" % (a, i)) for i in range(2)] for a in range(2)]
         banks = {}
-        sorted_words = {}
-
-        def shared(pair):
-            return FIRST_SHARED <= pair < PAIRS
-
-        def stage(pair):
-            return stages[pair % STAGES][:]
 
         def bank_tile(tag, shape):
             bank = psum.tile(shape, F32, tag=tag, name="bank")
             return bank
 
-        def turn_words(out, words):
-            for u in range(2):
-                nc.tensor.transpose(out[:, u], words[:, u], ident[:])
+        gain_quads = keep.tile([P, 2, HALF, 2], F32)
+        table_first = keep.tile([P, 2, 2 * D], F32)
+        table_rest = keep.tile([P, ROWS - 2, 2 * D], F32, align_bytes=64)
 
-        def sort_words(copy, key, raw):
-            words = keep.tile([P, 4, 2, P], F32, name="sorted_%s%d" % key)
-            copy(out=words[:], in_=raw[:].rearrange("p r k -> p (r k)").bitcast(F32).rearrange("p (c n u) -> p c u n", c=4, u=2))
-            sorted_words[key] = words[:]
+        def spread_gain(tag):
+            bank = bank_tile(tag, [P, HALF, 2])
+            nc.tensor.matmul(bank[:].rearrange("p j e -> p (j e)"), lhsT=ones[:], rhs=gain_row[:], start=True, stop=True)
+            banks["gain"] = bank
 
-        def parity_view(key, raw):
-            if key in sorted_words:
-                return sorted_words[key]
-            return raw[:].rearrange("p r k -> p (r k)").bitcast(F32).rearrange("p (c n u) -> p c u n", c=4, u=2)
+        def gain_out():
+            bank = banks["gain"]
+            nc.scalar.copy(out=gain_quads[:], in_=bank[:].rearrange("p j e -> p e j").unsqueeze(3).broadcast_to([P, 2, HALF, 2]))
+            nc.scalar.activation(out=gain_quads[:, 1, :, 0], in_=bank[:, :, 1], func=ACT.Copy, scale=-1.0)
 
-        def wd_turn(th, tags):
+        def table(first, last):
+            return table_first[:, first:last] if first < 2 else table_rest[:, first - 2 : last - 2]
+
+        def table_rows(first, last):
+            rows, q = last - first, first % 4
+            for e in range(2):
+                nc.vector.tensor_tensor(
+                    out=table(first, last).rearrange("p n (e j r) -> p n e j r", e=2, r=2)[:, :, e],
+                    in0=trig[first // 4][:, :: 1 - 2 * e, HALF * q : HALF * (q + rows)].rearrange("p r (n j) -> p n j r", j=HALF),
+                    in1=gain_quads[:, e].unsqueeze(1).broadcast_to([P, rows, HALF, 2]),
+                    op=ALU.mult,
+                )
+
+        wd_grouped = keep.tile([P, 2, 2, 2 * P, 4], BF16, align_bytes=64)
+        wu_grouped = keep.tile([P, 2, FEAT, 4], BF16, align_bytes=64)
+        wd_codes = keep.tile([P, 2, 2, 2 * P], U32, align_bytes=64)
+        wd_scales = keep.tile([P, 2, 2, 2 * P], U8, align_bytes=64)
+        wu_codes = keep.tile([P, 2, FEAT], U32, align_bytes=64)
+        wu_scales = keep.tile([P, 2, FEAT], U8, align_bytes=64)
+        stages = [keep.tile([P, 2 * FEAT], F32, align_bytes=64, name="stage%d" % i) for i in range(STAGES)]
+        latents = [[keep.tile([P, SUB, 4], BF16, align_bytes=64, name="latent%d%d" % (a, i)) for i in range(2)] for a in range(2)]
+
+        def turn_weight_rows(tag, rows):
+            bank = bank_tile(tag, [P, 2, 2 * P])
+            for i, block in enumerate(rows):
+                for u in range(2):
+                    nc.tensor.transpose(bank[:, u, P * i : P * (i + 1)], block.bitcast(F32)[:, u:WORDS:2], ident[:])
+            return bank
+
+        def wd_turn(th, tag):
             for g in range(2):
-                bank = bank_tile(tags[g], [P, 2, 256])
-                for i in range(2):
-                    turn_words(bank[:, :, SUB * i : SUB * (i + 1)], parity_view(("wd", th), wd_raw[th])[:, 2 * i + g])
-                banks["wd", th, g] = bank
+                banks["wd", th, g] = turn_weight_rows("%s%d" % (tag, g), [wd_raw[th][:, i, PASS * g : PASS * (g + 1)] for i in range(2)])
 
-        def wu_turn(part, tags):
+        def wu_turn(part, tag):
             for i in range(2):
-                bank = bank_tile(tags[i], [P, 2, 256])
-                for j in range(2):
-                    turn_words(bank[:, :, SUB * j : SUB * (j + 1)], parity_view(("wu", part), wu_raw[part])[:, 2 * i + j])
-                banks["wu", part, i] = bank
+                banks["wu", part, i] = turn_weight_rows("%s%d" % (tag, i), [wu_raw[part][:, 2 * i + j, :] for j in range(2)])
 
-        def copy_words(copy, words, bank):
-            copy(out=words.rearrange("p (n u) -> p n u", u=2), in_=bank[:].rearrange("p u n -> p n u"))
+        def wd_out(th):
+            for g in range(2):
+                words = wd_grouped[:, th, g].rearrange("p n t -> p (n t)").bitcast(F32)
+                nc.scalar.copy(out=words.rearrange("p (n u) -> p n u", u=2), in_=banks["wd", th, g][:].rearrange("p u n -> p n u"))
 
-        def wd_out(copy, th, g):
-            copy_words(copy, wd_grouped[:, th, g].rearrange("p n t -> p (n t)").bitcast(F32), banks["wd", th, g])
-
-        def wu_out(copy, part, i):
-            words = wu_grouped[:, part, 256 * i : 256 * (i + 1)].rearrange("p n t -> p (n t)").bitcast(F32)
-            bank = banks["wu", part, i]
-            if part == 1:
-                copy_words(copy, words, bank)
-            else:
-                copy(out=words.rearrange("p (h e j u) -> p h e j u", h=2, e=2, u=2), in_=bank[:].rearrange("p u (h j e) -> p h e j u", h=2, e=2))
+        def wu_out(part):
+            for i in range(2):
+                words = wu_grouped[:, part, 2 * P * i : 2 * P * (i + 1)].rearrange("p n t -> p (n t)").bitcast(F32)
+                bank = banks["wu", part, i]
+                if part == 0:
+                    nc.scalar.copy(out=words.rearrange("p (h e j u) -> p h e j u", h=2, e=2, u=2), in_=bank[:].rearrange("p u (h j e) -> p h e j u", h=2, e=2))
+                else:
+                    nc.scalar.copy(out=words.rearrange("p (n u) -> p n u", u=2), in_=bank[:].rearrange("p u n -> p n u"))
 
         def wd_quant(th):
             nc.vector.quantize_mx(
@@ -178,258 +174,221 @@ def tile_mla_pa_t_kernel(tc, x_bytes, x_scale, w_kv_down, w_kv_up, k_norm_w, fre
         def wu_quant(part):
             nc.vector.quantize_mx(out=wu_codes[:, part].bitcast(FP8X4), scales=wu_scales[:, part], in_=wu_grouped[:, part].rearrange("p n t -> p (n t)"))
 
-        wide, xq, xs, lat, lq, ls, squares, rs, products, vout = {}, {}, {}, {}, {}, {}, {}, {}, {}, {}
-
-        def live(pair):
-            return 0 <= pair < PAIRS
-
-        def wide_tile(pair):
-            x_wide = work.tile([P, 2, C], BF16, tag="x_wide", bufs=4, align_bytes=64, name="x_wide")
-            wide[pair] = x_wide
+        wide, x_mx, latent_mx, sums, rstds, quads, values = {}, {}, {}, {}, {}, {}, {}
 
         def widen(pair, a, copy=nc.scalar.copy):
-            if not live(pair):
-                return
             if pair not in wide:
-                wide_tile(pair)
+                x_wide = work.tile([P, 2, C], BF16, tag="x_wide", bufs=WIDE_BUFS, align_bytes=64, name="x_wide")
+                wide[pair] = x_wide
             copy(out=wide[pair][:, a, :], in_=x_tiles[pair][:, a, :].bitcast(FP8))
 
-        def scaled(pair):
+        def prescaled(pair):
             return latents[1][(pair - 3) % 2][:].rearrange("p n t -> p (n t)")
 
-        def premult(pair):
-            if shared(pair):
-                nc.gpsimd.tensor_tensor(out=scaled(pair), in0=wide[pair][:, 1, 0:512], in1=scale_row[:], op=ALU.mult)
+        def prescale(pair):
+            nc.gpsimd.tensor_tensor(out=prescaled(pair), in0=wide[pair][:, 1, 0:PASS], in1=scale_row[:], op=ALU.mult)
 
         def turn(pair, a):
-            if not live(pair):
-                return
             bank = bank_tile("xt%d" % a, [P, 2, SUB, 2])
             for g in range(2):
-                rows = scaled(pair) if shared(pair) and (a, g) == (1, 0) else wide[pair][:, a, 512 * g : 512 * (g + 1)]
+                rows = prescaled(pair) if pair >= FIRST_PRESCALED and (a, g) == (1, 0) else wide[pair][:, a, PASS * g : PASS * (g + 1)]
                 for u in range(2):
-                    nc.tensor.transpose(bank[:, g, :, u], rows.bitcast(F32)[:, u:256:2], ident[:])
+                    nc.tensor.transpose(bank[:, g, :, u], rows.bitcast(F32)[:, u:WORDS:2], ident[:])
             banks["xt", pair, a] = bank
 
         def x_out(pair, a):
-            if not live(pair):
-                return
-            first = 1 if shared(pair) and a == 1 else 0
+            first = 1 if pair >= FIRST_PRESCALED and a == 1 else 0
             nc.vector.tensor_tensor(
-                out=stage(pair).bitcast(BF16).rearrange("p (g a n t) -> p a g n t", g=2, a=2, t=4)[:, a, first:],
+                out=stages[pair % STAGES][:].bitcast(BF16).rearrange("p (g a n t) -> p a g n t", g=2, a=2, t=4)[:, a, first:],
                 in0=banks["xt", pair, a][:].rearrange("p g n u -> p (g n u)").bitcast(BF16).rearrange("p (g n t) -> p g n t", g=2, t=4)[:, first:],
                 in1=scale[:, first:].unsqueeze(2).broadcast_to([P, 2 - first, SUB, 4]),
                 op=ALU.mult,
             )
 
-        def words_out(pair, copy=nc.scalar.copy):
-            if shared(pair):
-                copy(out=stage(pair)[:, 256:512], in_=banks["xt", pair, 1][:, 0].rearrange("p n u -> p (n u)"))
+        def words_out(pair, copy):
+            copy(out=stages[pair % STAGES][:, 2 * SUB : 4 * SUB], in_=banks["xt", pair, 1][:, 0].rearrange("p n u -> p (n u)"))
 
-        def quant(pair):
-            if not live(pair):
-                return
-            x_q = work.tile([P, 2, 256], U32, tag="x_q", align_bytes=64, name="x_q")
-            x_s = work.tile([P, 2, 256], U8, tag="x_s", align_bytes=64, name="x_s")
+        def x_quant(pair):
+            codes = work.tile([P, 2, 2 * SUB], U32, tag="x_q", align_bytes=64, name="x_q")
+            scales = work.tile([P, 2, 2 * SUB], U8, tag="x_s", align_bytes=64, name="x_s")
             nc.vector.quantize_mx(
-                out=x_q[:].rearrange("p g n -> p (g n)").bitcast(FP8X4),
-                scales=x_s[:].rearrange("p g n -> p (g n)"),
-                in_=stage(pair).bitcast(BF16),
+                out=codes[:].rearrange("p g n -> p (g n)").bitcast(FP8X4),
+                scales=scales[:].rearrange("p g n -> p (g n)"),
+                in_=stages[pair % STAGES][:].bitcast(BF16),
             )
-            xq[pair], xs[pair] = x_q, x_s
+            x_mx[pair] = codes, scales
 
         def down(pair, a):
-            if not live(pair):
-                return
             bank = bank_tile("lat%d" % a, [P, 4, SUB])
-            cols = slice(SUB * a, SUB * (a + 1))
+            codes, scales = x_mx[pair]
+            tokens = slice(SUB * a, SUB * (a + 1))
             for t in range(4):
-                th, wcols = t // 2, slice(SUB * (t % 2), SUB * (t % 2 + 1))
+                th, columns = t // 2, slice(P * (t % 2), P * (t % 2 + 1))
                 for g in range(2):
                     nc.tensor.matmul_mx(
                         out=bank[:, t, :],
-                        lhsT=wd_codes[:, th, g, wcols].bitcast(FP8X4),
-                        lhsT_scale=wd_scales[:, th, g, wcols],
-                        rhs=xq[pair][:, g, cols].bitcast(FP8X4),
-                        rhs_scale=xs[pair][:, g, cols],
+                        lhsT=wd_codes[:, th, g, columns].bitcast(FP8X4),
+                        lhsT_scale=wd_scales[:, th, g, columns],
+                        rhs=codes[:, g, tokens].bitcast(FP8X4),
+                        rhs_scale=scales[:, g, tokens],
                         start=(g == 0),
                         stop=(g == 1),
                     )
             banks["lat", pair, a] = bank
 
-        def latent_out(pair, a, copy=nc.scalar.copy):
-            if not live(pair):
-                return
-            latent = latents[a][pair % 2][:]
-            copy(out=latent, in_=banks["lat", pair, a][:].rearrange("p t n -> p n t"))
-            lat[pair, a] = latent
+        def latent_out(pair, a):
+            nc.scalar.copy(out=latents[a][pair % 2][:], in_=banks["lat", pair, a][:].rearrange("p t n -> p n t"))
 
         def latent_quant(pair, a):
-            if not live(pair):
-                return
-            l_q = work.tile([P, SUB], U32, tag="l_q", bufs=4, align_bytes=64, name="l_q")
-            l_s = work.tile([P, SUB], U8, tag="l_s", bufs=4, align_bytes=64, name="l_s")
-            nc.vector.quantize_mx(out=l_q[:].bitcast(FP8X4), scales=l_s[:], in_=lat[pair, a].rearrange("p n t -> p (n t)"))
-            lq[pair, a], ls[pair, a] = l_q, l_s
+            codes = work.tile([P, SUB], U32, tag="l_q", bufs=SMALL_BUFS, align_bytes=64, name="l_q")
+            scales = work.tile([P, SUB], U8, tag="l_s", bufs=SMALL_BUFS, align_bytes=64, name="l_s")
+            nc.vector.quantize_mx(out=codes[:].bitcast(FP8X4), scales=scales[:], in_=latents[a][pair % 2][:].rearrange("p n t -> p (n t)"))
+            latent_mx[pair, a] = codes, scales
 
-        def up(pair, a, kinds="kv", tag=None):
-            if not live(pair):
-                return
-            for kind in kinds:
-                part = "kv".index(kind)
-                bank = bank_tile("%s%d" % (tag or kind, a), [P, FEAT])
-                nc.tensor.matmul_mx(
-                    out=bank[:],
-                    lhsT=lq[pair, a][:].bitcast(FP8X4),
-                    lhsT_scale=ls[pair, a][:],
-                    rhs=wu_codes[:, part].bitcast(FP8X4),
-                    rhs_scale=wu_scales[:, part],
-                    start=True,
-                    stop=True,
-                )
-                banks[kind, pair, a] = bank
+        def up(pair, a, kind, tag=None):
+            part = "kv".index(kind)
+            bank = bank_tile("%s%d" % (tag or kind, a), [P, FEAT])
+            codes, scales = latent_mx[pair, a]
+            nc.tensor.matmul_mx(
+                out=bank[:],
+                lhsT=codes[:].bitcast(FP8X4),
+                lhsT_scale=scales[:],
+                rhs=wu_codes[:, part].bitcast(FP8X4),
+                rhs_scale=wu_scales[:, part],
+                start=True,
+                stop=True,
+            )
+            banks[kind, pair, a] = bank
 
         def square_sums(pair, a, first=0, last=H):
-            if not live(pair):
-                return
             if first == 0:
-                sums = work.tile([P, H], F32, tag="sums", bufs=4, name="sums")
-                squares[pair, a] = sums
+                head_sums = work.tile([P, H], F32, tag="sums", bufs=SMALL_BUFS, name="sums")
+                sums[pair, a] = head_sums
             for h in range(first, last):
-                junk = work.tile([P, D], BF16, tag="junk", bufs=4, name="junk")
-                nc.scalar.activation(out=junk[:], in_=banks["k", pair, a][:, D * h : D * (h + 1)], func=ACT.Square, accum_out=squares[pair, a][:, h : h + 1])
+                squares = work.tile([P, D], BF16, tag="squares", bufs=SMALL_BUFS, name="squares")
+                nc.scalar.activation(out=squares[:], in_=banks["k", pair, a][:, D * h : D * (h + 1)], func=ACT.Square, accum_out=sums[pair, a][:, h : h + 1])
 
         def inverse_rms(pair, a):
-            if not live(pair):
-                return
-            rstd = work.tile([P, H], F32, tag="rstd", bufs=4, name="rstd")
-            nc.scalar.activation(out=rstd[:], in_=squares[pair, a][:], func=ACT.Abs_reciprocal_sqrt, bias=EPS, scale=1.0 / D)
-            rs[pair, a] = rstd
+            rstd = work.tile([P, H], F32, tag="rstd", bufs=SMALL_BUFS, name="rstd")
+            nc.scalar.activation(out=rstd[:], in_=sums[pair, a][:], func=ACT.Abs_reciprocal_sqrt, bias=EPS, scale=1.0 / D)
+            rstds[pair, a] = rstd
+
+        def both_square_sums(pair):
+            square_sums(pair, 0)
+            square_sums(pair, 1, 0, 1)
+            inverse_rms(pair, 0)
+            square_sums(pair, 1, 1, H)
 
         def store(out, tile, pair, first, last):
-            b, s, h = pair // 4, pair // 2 % 2, pair % 2
-            view = out[b].rearrange("(s p q) h d -> s p q (h d)", p=P, q=4)[s]
-            nc.sync.dma_start(out=view[:, 2 * h + first : 2 * h + last, :], in_=tile.rearrange("p (a f) -> p a f", a=2)[:, first:last])
+            nc.sync.dma_start(
+                out=pair_rows(out.rearrange("b t h d -> b t (h d)"), pair, first, last),
+                in_=tile[:].rearrange("p (a f) -> p a f", a=2)[:, first:last],
+            )
 
         def values_out(pair, a, copy=nc.scalar.copy):
-            if not live(pair):
-                return
             if a == 0:
                 v_tile = work.tile([P, 2 * FEAT], F32, tag="v_tile", name="v_tile")
-                vout[pair] = v_tile
-            copy(out=vout[pair][:, FEAT * a : FEAT * (a + 1)], in_=banks["v", pair, a][:])
+                values[pair] = v_tile
+            copy(out=values[pair][:, FEAT * a : FEAT * (a + 1)], in_=banks["v", pair, a][:])
             if pair >= PAIRS - 2:
-                store(out_1, vout[pair][:], pair, a, a + 1)
+                store(out_1, values[pair], pair, a, a + 1)
             elif a == 1:
-                store(out_1, vout[pair][:], pair, 0, 2)
+                store(out_1, values[pair], pair, 0, 2)
 
         def rotate(pair, a):
-            if not live(pair):
-                return
             if a == 0:
-                quads = work.tile([P, 2, H, D, 2], F32, tag="quads", name="quads")
-                products[pair] = quads
+                pair_quads = work.tile([P, 2, H, D, 2], F32, tag="quads", name="quads")
+                quads[pair] = pair_quads
             row = (2 * pair + a) % ROWS
             for h in range(H):
                 nc.vector.scalar_tensor_tensor(
-                    out=products[pair][:, a, h],
+                    out=quads[pair][:, a, h],
                     in0=banks["k", pair, a][:, D * h : D * (h + 1)].unsqueeze(2).broadcast_to([P, D, 2]),
-                    scalar=rs[pair, a][:, h : h + 1],
+                    scalar=rstds[pair, a][:, h : h + 1],
                     in1=table(row, row + 1).rearrange("p n (d r) -> p (n d) r", r=2),
                     op0=ALU.mult,
                     op1=ALU.mult,
                 )
 
         def keys_out(pair, first, last, adder):
-            if not live(pair):
-                return
             keys = stages[(pair + 2) % STAGES]
-            quads = products[pair][:, first:last].rearrange("p a h (e j) r -> p (a h) e (j r)", e=2)
+            halves = quads[pair][:, first:last].rearrange("p a h (e j) r -> p (a h) e (j r)", e=2)
             adder.tensor_tensor(
                 out=keys[:, FEAT * first : FEAT * last].rearrange("p (n d) -> p n d", d=D),
-                in0=quads[:, :, 0, :],
-                in1=quads[:, :, 1, :],
+                in0=halves[:, :, 0, :],
+                in1=halves[:, :, 1, :],
                 op=ALU.add,
             )
-            store(out_0, keys[:], pair, first, last)
+            store(out_0, keys, pair, first, last)
 
         widen(0, 0, nc.vector.tensor_copy)
         widen(0, 1)
         turn(0, 0)
         turn(0, 1)
-        wd_turn(0, ("lat0", "lat1"))
+        wd_turn(0, "lat")
         widen(1, 0)
         widen(1, 1)
-        x_out(0, 0)
-        turn(1, 0)
-        x_out(0, 1)
-        turn(1, 1)
-        wd_turn(1, ("k0", "k1"))
-        wd_out(nc.scalar.copy, 0, 0)
-        wd_out(nc.scalar.copy, 0, 1)
+        for a in range(2):
+            x_out(0, a)
+            turn(1, a)
+        wd_turn(1, "k")
+        spread_gain("v0")
+        wd_out(0)
         widen(2, 0)
         widen(2, 1)
-        wd_out(nc.scalar.copy, 1, 0)
-        wd_out(nc.scalar.copy, 1, 1)
-        quant(0)
-        x_out(1, 0)
-        turn(2, 0)
-        x_out(1, 1)
-        turn(2, 1)
+        wd_out(1)
+        x_quant(0)
+        for a in range(2):
+            x_out(1, a)
+            turn(2, a)
         wd_quant(0)
         wd_quant(1)
-        wu_turn(0, ("v0", "v1"))
+        gain_out()
+
+        wu_turn(0, "v")
         down(0, 0)
         down(0, 1)
         x_out(2, 0)
         x_out(2, 1)
         widen(3, 0)
-        wu_out(nc.scalar.copy, 0, 0)
-        wu_out(nc.scalar.copy, 0, 1)
+        wu_out(0)
         widen(3, 1)
         latent_out(0, 0)
         latent_out(0, 1)
-        quant(1)
+        x_quant(1)
         wu_quant(0)
-        spread_gain()
         latent_quant(0, 0)
         up(0, 0, "k")
-        table_rows(nc.vector, 0, 2)
+        table_rows(0, 2)
         latent_quant(0, 1)
-        table_rows(nc.vector, 2, 4)
-        table_rows(nc.vector, 4, 8)
+        table_rows(2, 4)
+        table_rows(4, ROWS)
         down(1, 0)
         up(0, 1, "k")
         down(1, 1)
-        wu_turn(1, ("v0", "v1"))
+
+        wu_turn(1, "v")
         turn(3, 0)
         turn(3, 1)
-        square_sums(0, 0)
-        square_sums(0, 1, 0, 1)
-        inverse_rms(0, 0)
-        square_sums(0, 1, 1, H)
+        both_square_sums(0)
         latent_out(1, 0)
         inverse_rms(0, 1)
         latent_out(1, 1)
-        wu_out(nc.scalar.copy, 1, 0)
-        wu_out(nc.scalar.copy, 1, 1)
+        wu_out(1)
         rotate(0, 0)
         rotate(0, 1)
-        latent_quant(1, 0)
-        up(1, 0, "k")
-        latent_quant(1, 1)
-        up(1, 1, "k")
+        for a in range(2):
+            latent_quant(1, a)
+            up(1, a, "k")
         wu_quant(1)
         up(0, 0, "v")
         up(0, 1, "v")
         widen(4, 0)
         widen(4, 1)
-        quant(2)
+        x_quant(2)
+
         keys_out(0, 0, 2, nc.gpsimd)
-        square_sums(1, 0)
-        square_sums(1, 1, 0, 1)
-        inverse_rms(1, 0)
-        square_sums(1, 1, 1, H)
+        both_square_sums(1)
         values_out(0, 0)
         inverse_rms(1, 1)
         values_out(0, 1)
@@ -441,22 +400,22 @@ def tile_mla_pa_t_kernel(tc, x_bytes, x_scale, w_kv_down, w_kv_up, k_norm_w, fre
         x_out(3, 1)
         up(1, 1, "v")
         turn(4, 1)
-        latent_out(2, 0)
-        values_out(1, 0)
-        latent_out(2, 1)
-        values_out(1, 1)
+        for a in range(2):
+            latent_out(2, a)
+            values_out(1, a)
         widen(5, 1)
         widen(5, 0)
         rotate(1, 0)
         rotate(1, 1)
         latent_quant(2, 0)
-        up(2, 0)
+        up(2, 0, "k")
+        up(2, 0, "v")
         latent_quant(2, 1)
         up(2, 1, "k")
-        quant(3)
+        x_quant(3)
 
-        for s in range(3, PAIRS - 2):
-            premult(s + 2)
+        for s in range(FIRST_STEP, PAIRS - 2):
+            prescale(s + 2)
             keys_out(s - 2, 0, 2, nc.gpsimd)
             down(s, 0)
             x_out(s + 1, 0)
@@ -464,26 +423,30 @@ def tile_mla_pa_t_kernel(tc, x_bytes, x_scale, w_kv_down, w_kv_up, k_norm_w, fre
             down(s, 1)
             up(s - 1, 1, "v")
             x_out(s + 1, 1)
-            words_out(s + 1, nc.vector.tensor_copy)
-            turn(s + 2, 1)
-            square_sums(s - 1, 0)
-            square_sums(s - 1, 1, 0, 1)
-            inverse_rms(s - 1, 0)
-            square_sums(s - 1, 1, 1, H)
+            if s % 2 == 0:
+                words_out(s + 1, nc.vector.tensor_copy)
+            both_square_sums(s - 1)
             latent_out(s, 0)
             inverse_rms(s - 1, 1)
+            if s % 2 == 1 and s + 1 >= FIRST_PRESCALED:
+                words_out(s + 1, nc.scalar.copy)
+            turn(s + 2, 1)
             values_out(s - 1, 0)
             latent_out(s, 1)
-            widen(s + 3, 1)
+            if s + 3 < PAIRS:
+                widen(s + 3, 1)
             values_out(s - 1, 1)
-            widen(s + 3, 0)
+            if s + 3 < PAIRS:
+                widen(s + 3, 0)
             rotate(s - 1, 0)
             rotate(s - 1, 1)
             latent_quant(s, 0)
-            up(s, 0)
+            up(s, 0, "k")
+            up(s, 0, "v")
             latent_quant(s, 1)
             up(s, 1, "k")
-            quant(s + 1)
+            x_quant(s + 1)
+
         third, second, last = PAIRS - 3, PAIRS - 2, PAIRS - 1
         keys_out(third - 1, 0, 2, nc.gpsimd)
         down(second, 0)
@@ -491,11 +454,11 @@ def tile_mla_pa_t_kernel(tc, x_bytes, x_scale, w_kv_down, w_kv_up, k_norm_w, fre
         down(second, 1)
         x_out(last, 0)
         x_out(last, 1)
-        words_out(last, nc.vector.tensor_copy)
         square_sums(third, 0)
         square_sums(third, 1, 0, 1)
         inverse_rms(third, 0)
         latent_out(second, 0)
+        words_out(last, nc.scalar.copy)
         latent_out(second, 1)
         square_sums(third, 1, 1, H)
         values_out(third, 0)
@@ -504,7 +467,7 @@ def tile_mla_pa_t_kernel(tc, x_bytes, x_scale, w_kv_down, w_kv_up, k_norm_w, fre
         rotate(third, 0)
         latent_quant(second, 0)
         latent_quant(second, 1)
-        quant(last)
+        x_quant(last)
         up(second, 0, "k", "xt")
         up(second, 1, "k", "xt")
         up(second, 0, "v")
@@ -513,6 +476,7 @@ def tile_mla_pa_t_kernel(tc, x_bytes, x_scale, w_kv_down, w_kv_up, k_norm_w, fre
         up(second, 1, "v")
         rotate(third, 1)
         keys_out(third, 0, 1, nc.gpsimd)
+
         square_sums(second, 0)
         latent_out(last, 0)
         inverse_rms(second, 0)
@@ -520,12 +484,12 @@ def tile_mla_pa_t_kernel(tc, x_bytes, x_scale, w_kv_down, w_kv_up, k_norm_w, fre
         square_sums(second, 1)
         values_out(second, 0, nc.vector.tensor_copy)
         keys_out(third, 1, 2, nc.vector)
-        latent_quant(last, 0)
-        up(last, 0, "k")
-        latent_quant(last, 1)
-        up(last, 1, "k")
+        for a in range(2):
+            latent_quant(last, a)
+            up(last, a, "k")
         up(last, 0, "v", "lat")
         up(last, 1, "v", "lat")
+
         inverse_rms(second, 1)
         square_sums(last, 0)
         values_out(second, 1)

@@ -24,11 +24,15 @@ FP8X4 = mybir.dt.float8_e4m3fn_x4
 ACT = mybir.ActivationFunctionType
 ALU = mybir.AluOpType
 
-FIRST_STEP = 3
-FIRST_PRESCALED = FIRST_STEP + 2
 STAGES = 3
-WIDE_BUFS = 4
+WIDE_BUFS = 5
 SMALL_BUFS = 4
+CODE_BUFS = 8
+SHARE = 128
+
+
+def share(pair):
+    return 0 if pair == 0 else 2 * SUB if pair == 2 else SHARE
 
 
 def tile_mla_pa_t_kernel(tc, x_bytes, x_scale, w_kv_down, w_kv_up, k_norm_w, freqs_cos, freqs_sin, out_0, out_1):
@@ -48,12 +52,12 @@ def tile_mla_pa_t_kernel(tc, x_bytes, x_scale, w_kv_down, w_kv_up, k_norm_w, fre
         make_identity(nc, ident[:])
 
         scale = keep.tile([P, 2, 4], F32)
-        scale_row = keep.tile([P, PASS], F32)
-        trig = [keep.tile([P, 2, 4 * HALF], BF16, name="trig%d" % s) for s in range(2)]
+        trig = keep.tile([P, 2, ROWS * HALF], BF16)
         gain_row = keep.tile([P, D], BF16)
         nc.vector.memset(gain_row[:], 0.0)
-        ones = keep.tile([P, P], BF16)
-        nc.vector.memset(ones[:], 1.0)
+        signs = keep.tile([P, 2, P], BF16)
+        nc.vector.memset(signs[:, 0], -1.0)
+        nc.vector.memset(signs[:, 1], 1.0)
         wd_raw = [keep.tile([P, 2, C], BF16, align_bytes=64, name="wd_raw%d" % th) for th in range(2)]
         wu_raw = [keep.tile([P, 4, R], BF16, align_bytes=64, name="wu_raw%d" % part) for part in range(2)]
         wd_view = w_kv_down.rearrange("(m t) k -> m t k", t=4)
@@ -70,27 +74,37 @@ def tile_mla_pa_t_kernel(tc, x_bytes, x_scale, w_kv_down, w_kv_up, k_norm_w, fre
                 x_tiles[pair] = x_codes
             nc.sync.dma_start(out=x_tiles[pair][:, first:last], in_=pair_rows(x_bytes, pair, first, last))
 
-        def load_trig(s):
+        def load_scale():
+            nc.sync.dma_start(out=scale[:], in_=x_scale[0, 0].rearrange("(g p t) -> p g t", p=P, t=4))
+
+        def load_gain():
+            nc.sync.dma_start(out=gain_row[0:1, :], in_=k_norm_w.unsqueeze(0))
+
+        def load_trig():
             for slot, angles in enumerate((freqs_cos, freqs_sin)):
-                nc.sync.dma_start(out=trig[s][:, slot], in_=angles.rearrange("(s p q) j -> s p (q j)", p=P, q=4)[s])
+                nc.sync.dma_start(out=trig[:, slot].rearrange("p (s c) -> p s c", s=2), in_=angles.rearrange("(s p q) j -> p s (q j)", p=P, q=4))
+
+        def load_wd(th):
+            nc.sync.dma_start(out=wd_raw[th][:], in_=wd_view[:, 2 * th : 2 * th + 2, :])
+
+        def load_wu(part):
+            nc.sync.dma_start(out=wu_raw[part][:], in_=wu_view[:, 4 * part : 4 * part + 4, :])
 
         load_x(0, 0, 1)
-        nc.sync.dma_start(out=scale[:], in_=x_scale[0, 0].rearrange("(g p t) -> p g t", p=P, t=4))
         load_x(0, 1, 2)
-        nc.sync.dma_start(out=wd_raw[0][:], in_=wd_view[:, 0:2, :])
+        load_scale()
         load_x(1)
-        nc.sync.dma_start(out=wd_raw[1][:], in_=wd_view[:, 2:4, :])
-        nc.sync.dma_start(out=gain_row[0:1, :], in_=k_norm_w.unsqueeze(0))
+        load_gain()
         load_x(2)
-        nc.sync.dma_start(out=wu_raw[0][:], in_=wu_view[:, 0:4, :])
+        load_wd(0)
         load_x(3)
-        load_trig(0)
-        nc.sync.dma_start(out=wu_raw[1][:], in_=wu_view[:, 4:8, :])
-        load_trig(1)
+        load_wd(1)
+        load_wu(0)
         load_x(4)
-        load_x(FIRST_PRESCALED)
-        nc.sync.dma_start(out=scale_row[:], in_=x_scale[0, 0, 0:PASS].partition_broadcast(P))
-        for pair in range(FIRST_PRESCALED + 1, PAIRS):
+        load_trig()
+        load_x(5)
+        load_wu(1)
+        for pair in range(6, PAIRS):
             load_x(pair)
 
         banks = {}
@@ -99,30 +113,22 @@ def tile_mla_pa_t_kernel(tc, x_bytes, x_scale, w_kv_down, w_kv_up, k_norm_w, fre
             bank = psum.tile(shape, F32, tag=tag, name="bank")
             return bank
 
-        gain_quads = keep.tile([P, 2, HALF, 2], F32)
-        table_first = keep.tile([P, 2, 2 * D], F32)
-        table_rest = keep.tile([P, ROWS - 2, 2 * D], F32, align_bytes=64)
+        table = keep.tile([P, ROWS, 2 * D], F32)
 
         def spread_gain(tag):
-            bank = bank_tile(tag, [P, HALF, 2])
-            nc.tensor.matmul(bank[:].rearrange("p j e -> p (j e)"), lhsT=ones[:], rhs=gain_row[:], start=True, stop=True)
+            bank = bank_tile(tag, [P, 2, D])
+            for sign in range(2):
+                nc.tensor.matmul(bank[:, sign], lhsT=signs[:, sign], rhs=gain_row[:], start=True, stop=True)
             banks["gain"] = bank
 
-        def gain_out():
-            bank = banks["gain"]
-            nc.scalar.copy(out=gain_quads[:], in_=bank[:].rearrange("p j e -> p e j").unsqueeze(3).broadcast_to([P, 2, HALF, 2]))
-            nc.scalar.activation(out=gain_quads[:, 1, :, 0], in_=bank[:, :, 1], func=ACT.Copy, scale=-1.0)
-
-        def table(first, last):
-            return table_first[:, first:last] if first < 2 else table_rest[:, first - 2 : last - 2]
-
         def table_rows(first, last):
-            rows, q = last - first, first % 4
-            for e in range(2):
+            rows = last - first
+            gains = banks["gain"][:].rearrange("p r (j e) -> p e j r", e=2)
+            for e, gain in enumerate((gains[:, 0, :, 1:2].broadcast_to([P, HALF, 2]), gains[:, 1])):
                 nc.vector.tensor_tensor(
-                    out=table(first, last).rearrange("p n (e j r) -> p n e j r", e=2, r=2)[:, :, e],
-                    in0=trig[first // 4][:, :: 1 - 2 * e, HALF * q : HALF * (q + rows)].rearrange("p r (n j) -> p n j r", j=HALF),
-                    in1=gain_quads[:, e].unsqueeze(1).broadcast_to([P, rows, HALF, 2]),
+                    out=table[:, first:last].rearrange("p n (e j r) -> p n e j r", e=2, r=2)[:, :, e],
+                    in0=trig[:, :: 1 - 2 * e, HALF * first : HALF * last].rearrange("p r (n j) -> p n j r", j=HALF),
+                    in1=gain.unsqueeze(1).broadcast_to([P, rows, HALF, 2]),
                     op=ALU.mult,
                 )
 
@@ -133,7 +139,6 @@ def tile_mla_pa_t_kernel(tc, x_bytes, x_scale, w_kv_down, w_kv_up, k_norm_w, fre
         wu_codes = keep.tile([P, 2, FEAT], U32, align_bytes=64)
         wu_scales = keep.tile([P, 2, FEAT], U8, align_bytes=64)
         stages = [keep.tile([P, 2 * FEAT], F32, align_bytes=64, name="stage%d" % i) for i in range(STAGES)]
-        latents = [[keep.tile([P, SUB, 4], BF16, align_bytes=64, name="latent%d%d" % (a, i)) for i in range(2)] for a in range(2)]
 
         def turn_weight_rows(tag, rows):
             bank = bank_tile(tag, [P, 2, 2 * P])
@@ -142,27 +147,23 @@ def tile_mla_pa_t_kernel(tc, x_bytes, x_scale, w_kv_down, w_kv_up, k_norm_w, fre
                     nc.tensor.transpose(bank[:, u, P * i : P * (i + 1)], block.bitcast(F32)[:, u:WORDS:2], ident[:])
             return bank
 
-        def wd_turn(th, tag):
-            for g in range(2):
-                banks["wd", th, g] = turn_weight_rows("%s%d" % (tag, g), [wd_raw[th][:, i, PASS * g : PASS * (g + 1)] for i in range(2)])
+        def wd_turn(th, g, tag):
+            banks["wd", th, g] = turn_weight_rows(tag, [wd_raw[th][:, i, PASS * g : PASS * (g + 1)] for i in range(2)])
 
-        def wu_turn(part, tag):
-            for i in range(2):
-                banks["wu", part, i] = turn_weight_rows("%s%d" % (tag, i), [wu_raw[part][:, 2 * i + j, :] for j in range(2)])
+        def wu_turn(part, i, tag):
+            banks["wu", part, i] = turn_weight_rows(tag, [wu_raw[part][:, 2 * i + j, :] for j in range(2)])
 
-        def wd_out(th):
-            for g in range(2):
-                words = wd_grouped[:, th, g].rearrange("p n t -> p (n t)").bitcast(F32)
-                nc.scalar.copy(out=words.rearrange("p (n u) -> p n u", u=2), in_=banks["wd", th, g][:].rearrange("p u n -> p n u"))
+        def wd_out(th, g, copy=nc.scalar.copy):
+            words = wd_grouped[:, th, g].rearrange("p n t -> p (n t)").bitcast(F32)
+            copy(out=words.rearrange("p (n u) -> p n u", u=2), in_=banks["wd", th, g][:].rearrange("p u n -> p n u"))
 
-        def wu_out(part):
-            for i in range(2):
-                words = wu_grouped[:, part, 2 * P * i : 2 * P * (i + 1)].rearrange("p n t -> p (n t)").bitcast(F32)
-                bank = banks["wu", part, i]
-                if part == 0:
-                    nc.scalar.copy(out=words.rearrange("p (h e j u) -> p h e j u", h=2, e=2, u=2), in_=bank[:].rearrange("p u (h j e) -> p h e j u", h=2, e=2))
-                else:
-                    nc.scalar.copy(out=words.rearrange("p (n u) -> p n u", u=2), in_=bank[:].rearrange("p u n -> p n u"))
+        def wu_out(part, i, copy=nc.scalar.copy):
+            words = wu_grouped[:, part, 2 * P * i : 2 * P * (i + 1)].rearrange("p n t -> p (n t)").bitcast(F32)
+            bank = banks["wu", part, i]
+            if part == 0:
+                copy(out=words.rearrange("p (h e j u) -> p h e j u", h=2, e=2, u=2), in_=bank[:].rearrange("p u (h j e) -> p h e j u", h=2, e=2))
+            else:
+                copy(out=words.rearrange("p (n u) -> p n u", u=2), in_=bank[:].rearrange("p u n -> p n u"))
 
         def wd_quant(th):
             nc.vector.quantize_mx(
@@ -174,39 +175,48 @@ def tile_mla_pa_t_kernel(tc, x_bytes, x_scale, w_kv_down, w_kv_up, k_norm_w, fre
         def wu_quant(part):
             nc.vector.quantize_mx(out=wu_codes[:, part].bitcast(FP8X4), scales=wu_scales[:, part], in_=wu_grouped[:, part].rearrange("p n t -> p (n t)"))
 
-        wide, x_mx, latent_mx, sums, rstds, quads, values = {}, {}, {}, {}, {}, {}, {}
+        wide, words, x_mx, latents, latent_mx, sums, rstds, quads, values = {}, {}, {}, {}, {}, {}, {}, {}, {}
 
-        def widen(pair, a, copy=nc.scalar.copy):
+        def widen(pair, first=0, last=2, copy=nc.scalar.copy):
             if pair not in wide:
-                x_wide = work.tile([P, 2, C], BF16, tag="x_wide", bufs=WIDE_BUFS, align_bytes=64, name="x_wide")
+                x_wide = work.tile([P, 2 * C], BF16, tag="x_wide", bufs=WIDE_BUFS, align_bytes=64, name="x_wide")
                 wide[pair] = x_wide
-            copy(out=wide[pair][:, a, :], in_=x_tiles[pair][:, a, :].bitcast(FP8))
+            copy(out=wide[pair][:, C * first : C * last], in_=x_tiles[pair][:, first:last].rearrange("p a c -> p (a c)").bitcast(FP8))
 
-        def prescaled(pair):
-            return latents[1][(pair - 3) % 2][:].rearrange("p n t -> p (n t)")
-
-        def prescale(pair):
-            nc.gpsimd.tensor_tensor(out=prescaled(pair), in0=wide[pair][:, 1, 0:PASS], in1=scale_row[:], op=ALU.mult)
-
-        def turn(pair, a):
-            bank = bank_tile("xt%d" % a, [P, 2, SUB, 2])
-            for g in range(2):
-                rows = prescaled(pair) if pair >= FIRST_PRESCALED and (a, g) == (1, 0) else wide[pair][:, a, PASS * g : PASS * (g + 1)]
+        def turn(pair, g, tag=None):
+            bank = bank_tile(tag or "xt%d" % g, [P, 2, 2 * SUB])
+            for a in range(2):
+                rows = wide[pair][:, C * a + PASS * g : C * a + PASS * (g + 1)]
                 for u in range(2):
-                    nc.tensor.transpose(bank[:, g, :, u], rows.bitcast(F32)[:, u:WORDS:2], ident[:])
-            banks["xt", pair, a] = bank
+                    nc.tensor.transpose(bank[:, u, SUB * a : SUB * (a + 1)], rows.bitcast(F32)[:, u:WORDS:2], ident[:])
+            banks["xt", pair, g] = bank
 
-        def x_out(pair, a):
-            first = 1 if pair >= FIRST_PRESCALED and a == 1 else 0
-            nc.vector.tensor_tensor(
-                out=stages[pair % STAGES][:].bitcast(BF16).rearrange("p (g a n t) -> p a g n t", g=2, a=2, t=4)[:, a, first:],
-                in0=banks["xt", pair, a][:].rearrange("p g n u -> p (g n u)").bitcast(BF16).rearrange("p (g n t) -> p g n t", g=2, t=4)[:, first:],
-                in1=scale[:, first:].unsqueeze(2).broadcast_to([P, 2 - first, SUB, 4]),
+        def scale_x(engine, pair, g, turned, first, last):
+            engine.tensor_tensor(
+                out=stages[pair % STAGES][:].bitcast(BF16).rearrange("p (g n u e) -> p g n u e", g=2, u=2, e=2)[:, g, first:last],
+                in0=turned,
+                in1=scale[:, g].rearrange("p (u e) -> p u e", e=2).unsqueeze(1).broadcast_to([P, last - first, 2, 2]),
                 op=ALU.mult,
             )
 
-        def words_out(pair, copy):
-            copy(out=stages[pair % STAGES][:, 2 * SUB : 4 * SUB], in_=banks["xt", pair, 1][:, 0].rearrange("p n u -> p (n u)"))
+        def x_out(pair, g):
+            first = share(pair) if g == 1 else 0
+            if first == 2 * SUB:
+                return
+            bank = banks["xt", pair, g][:].rearrange("p u n -> p (u n)").bitcast(BF16).rearrange("p (u n e) -> p n u e", u=2, e=2)
+            scale_x(nc.vector, pair, g, bank[:, first:], first, 2 * SUB)
+
+        def words_out(pair, copy=nc.scalar.copy):
+            if 2 <= pair <= 3:
+                part = stages[pair - 1][:, 0 : 2 * share(pair)].rearrange("p (n u) -> p n u", u=2)
+            else:
+                part = work.tile([P, share(pair), 2], F32, tag="words", align_bytes=64, name="words")
+            copy(out=part[:], in_=banks["xt", pair, 1][:, :, 0 : share(pair)].rearrange("p u n -> p n u"))
+            words[pair] = part
+
+        def words_scale(pair):
+            turned = words[pair][:].rearrange("p n u -> p (n u)").bitcast(BF16).rearrange("p (n u e) -> p n u e", u=2, e=2)
+            scale_x(nc.gpsimd, pair, 1, turned, 0, share(pair))
 
         def x_quant(pair):
             codes = work.tile([P, 2, 2 * SUB], U32, tag="x_q", align_bytes=64, name="x_q")
@@ -218,8 +228,8 @@ def tile_mla_pa_t_kernel(tc, x_bytes, x_scale, w_kv_down, w_kv_up, k_norm_w, fre
             )
             x_mx[pair] = codes, scales
 
-        def down(pair, a):
-            bank = bank_tile("lat%d" % a, [P, 4, SUB])
+        def down(pair, a, tag=None):
+            bank = bank_tile(tag or "lat%d" % a, [P, 4, SUB])
             codes, scales = x_mx[pair]
             tokens = slice(SUB * a, SUB * (a + 1))
             for t in range(4):
@@ -236,13 +246,18 @@ def tile_mla_pa_t_kernel(tc, x_bytes, x_scale, w_kv_down, w_kv_up, k_norm_w, fre
                     )
             banks["lat", pair, a] = bank
 
-        def latent_out(pair, a):
-            nc.scalar.copy(out=latents[a][pair % 2][:], in_=banks["lat", pair, a][:].rearrange("p t n -> p n t"))
+        def latent_out(pair, a, copy=nc.scalar.copy):
+            if pair == PAIRS - 1:
+                latent = stages[(pair + 1) % STAGES][:, 2 * SUB * a : 2 * SUB * (a + 1)].bitcast(BF16).rearrange("p (n t) -> p n t", t=4)
+            else:
+                latent = work.tile([P, SUB, 4], BF16, tag="latent", bufs=SMALL_BUFS, align_bytes=64, name="latent")
+            copy(out=latent[:], in_=banks["lat", pair, a][:].rearrange("p t n -> p n t"))
+            latents[pair, a] = latent
 
         def latent_quant(pair, a):
-            codes = work.tile([P, SUB], U32, tag="l_q", bufs=SMALL_BUFS, align_bytes=64, name="l_q")
-            scales = work.tile([P, SUB], U8, tag="l_s", bufs=SMALL_BUFS, align_bytes=64, name="l_s")
-            nc.vector.quantize_mx(out=codes[:].bitcast(FP8X4), scales=scales[:], in_=latents[a][pair % 2][:].rearrange("p n t -> p (n t)"))
+            codes = work.tile([P, SUB], U32, tag="l_q", bufs=CODE_BUFS, align_bytes=64, name="l_q")
+            scales = work.tile([P, SUB], U8, tag="l_s", bufs=CODE_BUFS, align_bytes=64, name="l_s")
+            nc.vector.quantize_mx(out=codes[:].bitcast(FP8X4), scales=scales[:], in_=latents[pair, a][:].rearrange("p n t -> p (n t)"))
             latent_mx[pair, a] = codes, scales
 
         def up(pair, a, kind, tag=None):
@@ -305,13 +320,13 @@ def tile_mla_pa_t_kernel(tc, x_bytes, x_scale, w_kv_down, w_kv_up, k_norm_w, fre
                     out=quads[pair][:, a, h],
                     in0=banks["k", pair, a][:, D * h : D * (h + 1)].unsqueeze(2).broadcast_to([P, D, 2]),
                     scalar=rstds[pair, a][:, h : h + 1],
-                    in1=table(row, row + 1).rearrange("p n (d r) -> p (n d) r", r=2),
+                    in1=table[:, row].rearrange("p (d r) -> p d r", r=2),
                     op0=ALU.mult,
                     op1=ALU.mult,
                 )
 
         def keys_out(pair, first, last, adder):
-            keys = stages[(pair + 2) % STAGES]
+            keys = stages[(pair + 3) % STAGES]
             halves = quads[pair][:, first:last].rearrange("p a h (e j) r -> p (a h) e (j r)", e=2)
             adder.tensor_tensor(
                 out=keys[:, FEAT * first : FEAT * last].rearrange("p (n d) -> p n d", d=D),
@@ -321,187 +336,190 @@ def tile_mla_pa_t_kernel(tc, x_bytes, x_scale, w_kv_down, w_kv_up, k_norm_w, fre
             )
             store(out_0, keys, pair, first, last)
 
-        widen(0, 0, nc.vector.tensor_copy)
-        widen(0, 1)
+        widen(0, 0, 1, nc.vector.tensor_copy)
+        widen(0, 1, 2)
+        widen(1)
+        widen(2)
         turn(0, 0)
         turn(0, 1)
-        wd_turn(0, "lat")
-        widen(1, 0)
-        widen(1, 1)
-        for a in range(2):
-            x_out(0, a)
-            turn(1, a)
-        wd_turn(1, "k")
-        spread_gain("v0")
-        wd_out(0)
-        widen(2, 0)
-        widen(2, 1)
-        wd_out(1)
+        spread_gain("k1")
+        turn(1, 1, "v1")
+        turn(1, 0, "v0")
+        wd_turn(0, 0, "lat0")
+        wd_turn(0, 1, "lat1")
+        x_out(0, 0)
+        x_out(0, 1)
+        wd_turn(1, 0, "k0")
+        wd_turn(1, 1, "xt0")
+        words_out(1)
+        words_scale(1)
+        x_out(1, 0)
+        x_out(1, 1)
+        turn(2, 0, "v1")
+        turn(2, 1)
+        widen(3)
+        wd_out(0, 0)
+        wd_out(0, 1)
+        wd_out(1, 0)
+        wd_out(1, 1)
+        widen(4)
+        wu_turn(0, 0, "v0")
+        wu_turn(0, 1, "k0")
         x_quant(0)
-        for a in range(2):
-            x_out(1, a)
-            turn(2, a)
         wd_quant(0)
+        x_quant(1)
         wd_quant(1)
-        gain_out()
-
-        wu_turn(0, "v")
         down(0, 0)
         down(0, 1)
+        words_out(2)
+        words_scale(2)
+        wu_out(0, 0)
+        wu_out(0, 1)
+        down(1, 0, "xt0")
+        down(1, 1, "v0")
         x_out(2, 0)
-        x_out(2, 1)
-        widen(3, 0)
-        wu_out(0)
-        widen(3, 1)
+        turn(3, 0, "v1")
+        turn(3, 1)
+        table_rows(0, 4)
+        table_rows(4, ROWS)
         latent_out(0, 0)
         latent_out(0, 1)
-        x_quant(1)
         wu_quant(0)
         latent_quant(0, 0)
-        up(0, 0, "k")
-        table_rows(0, 2)
         latent_quant(0, 1)
-        table_rows(2, 4)
-        table_rows(4, ROWS)
-        down(1, 0)
+        up(0, 0, "k")
         up(0, 1, "k")
-        down(1, 1)
-
-        wu_turn(1, "v")
-        turn(3, 0)
-        turn(3, 1)
-        both_square_sums(0)
         latent_out(1, 0)
-        inverse_rms(0, 1)
         latent_out(1, 1)
-        wu_out(1)
-        rotate(0, 0)
-        rotate(0, 1)
-        for a in range(2):
-            latent_quant(1, a)
-            up(1, a, "k")
-        wu_quant(1)
-        up(0, 0, "v")
-        up(0, 1, "v")
-        widen(4, 0)
-        widen(4, 1)
         x_quant(2)
-
-        keys_out(0, 0, 2, nc.gpsimd)
-        both_square_sums(1)
-        values_out(0, 0)
-        inverse_rms(1, 1)
-        values_out(0, 1)
-        down(2, 0)
+        latent_quant(1, 0)
+        latent_quant(1, 1)
+        widen(5)
+        words_out(3)
+        words_scale(3)
         x_out(3, 0)
-        turn(4, 0)
-        up(1, 0, "v")
-        down(2, 1)
         x_out(3, 1)
-        up(1, 1, "v")
+        down(2, 0)
+        down(2, 1)
+        turn(4, 0)
         turn(4, 1)
-        for a in range(2):
-            latent_out(2, a)
-            values_out(1, a)
-        widen(5, 1)
-        widen(5, 0)
-        rotate(1, 0)
-        rotate(1, 1)
+        wu_turn(1, 0, "v0")
+        wu_turn(1, 1, "v1")
+        both_square_sums(0)
+        latent_out(2, 0)
+        inverse_rms(0, 1)
+        latent_out(2, 1)
+        rotate(0, 0)
+        up(1, 0, "k")
+        rotate(0, 1)
+        up(1, 1, "k")
+        wu_out(1, 0)
+        wu_out(1, 1)
+        words_out(4, nc.vector.tensor_copy)
+        square_sums(1, 0)
+        widen(6)
         latent_quant(2, 0)
-        up(2, 0, "k")
-        up(2, 0, "v")
         latent_quant(2, 1)
-        up(2, 1, "k")
+        wu_quant(1)
         x_quant(3)
 
-        for s in range(FIRST_STEP, PAIRS - 2):
-            prescale(s + 2)
-            keys_out(s - 2, 0, 2, nc.gpsimd)
+        value_pair = 0
+        for s in range(3, PAIRS - 2):
+            keys_out(s - 3, 0, 2, nc.gpsimd)
+            words_scale(s + 1)
             down(s, 0)
+            up(value_pair, 0, "v")
+            down(s, 1)
             x_out(s + 1, 0)
             turn(s + 2, 0)
-            down(s, 1)
-            up(s - 1, 1, "v")
+            up(value_pair, 1, "v")
             x_out(s + 1, 1)
-            if s % 2 == 0:
-                words_out(s + 1, nc.vector.tensor_copy)
-            both_square_sums(s - 1)
-            latent_out(s, 0)
-            inverse_rms(s - 1, 1)
-            if s % 2 == 1 and s + 1 >= FIRST_PRESCALED:
-                words_out(s + 1, nc.scalar.copy)
             turn(s + 2, 1)
-            values_out(s - 1, 0)
+            square_sums(s - 2, 1, 0, 1)
+            inverse_rms(s - 2, 0)
+            square_sums(s - 2, 1, 1, H)
+            latent_out(s, 0)
+            inverse_rms(s - 2, 1)
+            values_out(value_pair, 0)
             latent_out(s, 1)
-            if s + 3 < PAIRS:
-                widen(s + 3, 1)
-            values_out(s - 1, 1)
-            if s + 3 < PAIRS:
-                widen(s + 3, 0)
-            rotate(s - 1, 0)
-            rotate(s - 1, 1)
+            values_out(value_pair, 1)
+            value_pair += 1
+            if s + 4 < PAIRS:
+                widen(s + 4)
+            else:
+                for a in range(2):
+                    up(value_pair, a, "v")
+                    values_out(value_pair, a)
+                value_pair += 1
+            rotate(s - 2, 0)
+            up(s - 1, 0, "k")
+            rotate(s - 2, 1)
+            up(s - 1, 1, "k")
+            words_out(s + 2, nc.scalar.copy if s % 2 else nc.vector.tensor_copy)
+            square_sums(s - 1, 0)
             latent_quant(s, 0)
-            up(s, 0, "k")
-            up(s, 0, "v")
             latent_quant(s, 1)
-            up(s, 1, "k")
             x_quant(s + 1)
 
-        third, second, last = PAIRS - 3, PAIRS - 2, PAIRS - 1
-        keys_out(third - 1, 0, 2, nc.gpsimd)
+        fourth, third, second, last = PAIRS - 4, PAIRS - 3, PAIRS - 2, PAIRS - 1
+        keys_out(fourth - 1, 0, 2, nc.gpsimd)
+        words_scale(last)
         down(second, 0)
-        up(third, 1, "v")
+        up(third, 0, "v")
         down(second, 1)
         x_out(last, 0)
+        up(third, 0, "k", "xt")
+        up(third, 1, "v")
         x_out(last, 1)
-        square_sums(third, 0)
-        square_sums(third, 1, 0, 1)
-        inverse_rms(third, 0)
+        up(third, 1, "k", "xt")
+        square_sums(fourth, 1, 0, 1)
+        inverse_rms(fourth, 0)
+        square_sums(fourth, 1, 1, H)
         latent_out(second, 0)
-        words_out(last, nc.scalar.copy)
+        inverse_rms(fourth, 1)
         latent_out(second, 1)
-        square_sums(third, 1, 1, H)
-        values_out(third, 0)
-        inverse_rms(third, 1)
-        values_out(third, 1)
-        rotate(third, 0)
+        rotate(fourth, 0)
+        rotate(fourth, 1)
         latent_quant(second, 0)
         latent_quant(second, 1)
         x_quant(last)
-        up(second, 0, "k", "xt")
-        up(second, 1, "k", "xt")
-        up(second, 0, "v")
+        values_out(third, 0)
+        both_square_sums(third)
+        values_out(third, 1)
+        inverse_rms(third, 1)
+        keys_out(fourth, 0, 2, nc.gpsimd)
+        up(second, 0, "k")
+        up(second, 1, "k")
         down(last, 0)
+        up(second, 0, "v")
         down(last, 1)
         up(second, 1, "v")
-        rotate(third, 1)
-        keys_out(third, 0, 1, nc.gpsimd)
-
         square_sums(second, 0)
         latent_out(last, 0)
         inverse_rms(second, 0)
         latent_out(last, 1)
-        square_sums(second, 1)
+        rotate(third, 0)
+        rotate(third, 1)
         values_out(second, 0, nc.vector.tensor_copy)
-        keys_out(third, 1, 2, nc.vector)
-        for a in range(2):
-            latent_quant(last, a)
-            up(last, a, "k")
+        latent_quant(last, 0)
+        latent_quant(last, 1)
+        up(last, 0, "k", "xt")
+        up(last, 1, "k", "xt")
         up(last, 0, "v", "lat")
         up(last, 1, "v", "lat")
-
-        inverse_rms(second, 1)
-        square_sums(last, 0)
+        square_sums(second, 1)
         values_out(second, 1)
-        inverse_rms(last, 0)
+        inverse_rms(second, 1)
+        keys_out(third, 0, 1, nc.gpsimd)
+        both_square_sums(last)
+        values_out(last, 0)
+        keys_out(third, 1, 2, nc.gpsimd)
+        inverse_rms(last, 1)
+        values_out(last, 1)
         rotate(second, 0)
         keys_out(second, 0, 1, nc.gpsimd)
-        square_sums(last, 1)
-        values_out(last, 0)
-        inverse_rms(last, 1)
         rotate(second, 1)
         keys_out(second, 1, 2, nc.gpsimd)
-        values_out(last, 1)
         rotate(last, 0)
         rotate(last, 1)
         keys_out(last, 0, 1, nc.vector)

@@ -24,15 +24,15 @@ FP8X4 = mybir.dt.float8_e4m3fn_x4
 ACT = mybir.ActivationFunctionType
 ALU = mybir.AluOpType
 
-STAGES = 3
 WIDE_BUFS = 5
 SMALL_BUFS = 4
-CODE_BUFS = 8
+QUAD_BUFS = 3
+CODE_BUFS = 5
 SHARE = 128
 
 
 def share(pair):
-    return 0 if pair == 0 else 2 * SUB if pair == 2 else SHARE
+    return 0 if pair in (0, PAIRS - 1) else 2 * SUB if pair == 2 else SHARE
 
 
 def tile_mla_pa_t_kernel(tc, x_bytes, x_scale, w_kv_down, w_kv_up, k_norm_w, freqs_cos, freqs_sin, out_0, out_1):
@@ -70,9 +70,10 @@ def tile_mla_pa_t_kernel(tc, x_bytes, x_scale, w_kv_down, w_kv_up, k_norm_w, fre
 
         def load_x(pair, first=0, last=2):
             if first == 0:
-                x_codes = work.tile([P, 2, C], U8, tag="x_codes", bufs=PAIRS, align_bytes=64, name="x_codes")
-                x_tiles[pair] = x_codes
-            nc.sync.dma_start(out=x_tiles[pair][:, first:last], in_=pair_rows(x_bytes, pair, first, last))
+                x_codes = keep.tile([P, max(last, 2), C], U8, align_bytes=64, name="x_codes%d" % pair)
+                for i in range(max(last, 2) // 2):
+                    x_tiles[pair + i] = x_codes[:, 2 * i : 2 * i + 2]
+            nc.sync.dma_start(out=x_tiles[pair][:, first:last] if last <= 2 else x_codes[:], in_=pair_rows(x_bytes, pair, first, last))
 
         def load_scale():
             nc.sync.dma_start(out=scale[:], in_=x_scale[0, 0].rearrange("(g p t) -> p g t", p=P, t=4))
@@ -104,8 +105,8 @@ def tile_mla_pa_t_kernel(tc, x_bytes, x_scale, w_kv_down, w_kv_up, k_norm_w, fre
         load_trig()
         load_x(5)
         load_wu(1)
-        for pair in range(6, PAIRS):
-            load_x(pair)
+        for pair in range(6, PAIRS, 2):
+            load_x(pair, 0, 4)
 
         banks = {}
 
@@ -138,7 +139,11 @@ def tile_mla_pa_t_kernel(tc, x_bytes, x_scale, w_kv_down, w_kv_up, k_norm_w, fre
         wd_scales = keep.tile([P, 2, 2, 2 * P], U8, align_bytes=64)
         wu_codes = keep.tile([P, 2, FEAT], U32, align_bytes=64)
         wu_scales = keep.tile([P, 2, FEAT], U8, align_bytes=64)
-        stages = [keep.tile([P, 2 * FEAT], F32, align_bytes=64, name="stage%d" % i) for i in range(STAGES)]
+        stages = [keep.tile([P, 2 * FEAT], F32, align_bytes=64, name="stage%d" % i) for i in range(PAIRS - 4)]
+        for grouped in (wd_grouped[:].rearrange("p th g n t -> p th (g n t)"), wu_grouped[:].rearrange("p part n t -> p part (n t)")):
+            stages.extend(grouped[:, i].bitcast(F32) for i in range(2))
+        late_values = [keep.tile([P, 2 * FEAT], F32, name="late_values%d" % i) for i in range(2)]
+        late_values.extend(raw[:].rearrange("p i c -> p (i c)").bitcast(F32) for raw in wd_raw + wu_raw)
 
         def turn_weight_rows(tag, rows):
             bank = bank_tile(tag, [P, 2, 2 * P])
@@ -193,7 +198,7 @@ def tile_mla_pa_t_kernel(tc, x_bytes, x_scale, w_kv_down, w_kv_up, k_norm_w, fre
 
         def scale_x(engine, pair, g, turned, first, last):
             engine.tensor_tensor(
-                out=stages[pair % STAGES][:].bitcast(BF16).rearrange("p (g n u e) -> p g n u e", g=2, u=2, e=2)[:, g, first:last],
+                out=stages[pair][:].bitcast(BF16).rearrange("p (g n u e) -> p g n u e", g=2, u=2, e=2)[:, g, first:last],
                 in0=turned,
                 in1=scale[:, g].rearrange("p (u e) -> p u e", e=2).unsqueeze(1).broadcast_to([P, last - first, 2, 2]),
                 op=ALU.mult,
@@ -207,7 +212,7 @@ def tile_mla_pa_t_kernel(tc, x_bytes, x_scale, w_kv_down, w_kv_up, k_norm_w, fre
             scale_x(nc.vector, pair, g, bank[:, first:], first, 2 * SUB)
 
         def words_out(pair, copy=nc.scalar.copy):
-            if 2 <= pair <= 3:
+            if pair == 2:
                 part = stages[pair - 1][:, 0 : 2 * share(pair)].rearrange("p (n u) -> p n u", u=2)
             else:
                 part = work.tile([P, share(pair), 2], F32, tag="words", align_bytes=64, name="words")
@@ -224,7 +229,7 @@ def tile_mla_pa_t_kernel(tc, x_bytes, x_scale, w_kv_down, w_kv_up, k_norm_w, fre
             nc.vector.quantize_mx(
                 out=codes[:].rearrange("p g n -> p (g n)").bitcast(FP8X4),
                 scales=scales[:].rearrange("p g n -> p (g n)"),
-                in_=stages[pair % STAGES][:].bitcast(BF16),
+                in_=stages[pair][:].bitcast(BF16),
             )
             x_mx[pair] = codes, scales
 
@@ -247,27 +252,27 @@ def tile_mla_pa_t_kernel(tc, x_bytes, x_scale, w_kv_down, w_kv_up, k_norm_w, fre
             banks["lat", pair, a] = bank
 
         def latent_out(pair, a, copy=nc.scalar.copy):
-            if pair == PAIRS - 1:
-                latent = stages[(pair + 1) % STAGES][:, 2 * SUB * a : 2 * SUB * (a + 1)].bitcast(BF16).rearrange("p (n t) -> p n t", t=4)
-            else:
-                latent = work.tile([P, SUB, 4], BF16, tag="latent", bufs=SMALL_BUFS, align_bytes=64, name="latent")
-            copy(out=latent[:], in_=banks["lat", pair, a][:].rearrange("p t n -> p n t"))
-            latents[pair, a] = latent
+            if a == 0 and pair == PAIRS - 1:
+                latents[pair] = stages[0][:, 0:FEAT].bitcast(BF16)
+            elif a == 0:
+                latent = work.tile([P, 2 * SUB * 4], BF16, tag="latent", align_bytes=64, name="latent")
+                latents[pair] = latent
+            copy(out=latents[pair][:].rearrange("p (a n t) -> p a n t", a=2, t=4)[:, a], in_=banks["lat", pair, a][:].rearrange("p t n -> p n t"))
 
-        def latent_quant(pair, a):
-            codes = work.tile([P, SUB], U32, tag="l_q", bufs=CODE_BUFS, align_bytes=64, name="l_q")
-            scales = work.tile([P, SUB], U8, tag="l_s", bufs=CODE_BUFS, align_bytes=64, name="l_s")
-            nc.vector.quantize_mx(out=codes[:].bitcast(FP8X4), scales=scales[:], in_=latents[pair, a][:].rearrange("p n t -> p (n t)"))
-            latent_mx[pair, a] = codes, scales
+        def latent_quant(pair):
+            codes = work.tile([P, 2 * SUB], U32, tag="l_q", bufs=CODE_BUFS, align_bytes=64, name="l_q")
+            scales = work.tile([P, 2 * SUB], U8, tag="l_s", bufs=CODE_BUFS, align_bytes=64, name="l_s")
+            nc.vector.quantize_mx(out=codes[:].bitcast(FP8X4), scales=scales[:], in_=latents[pair][:])
+            latent_mx[pair] = codes, scales
 
         def up(pair, a, kind, tag=None):
             part = "kv".index(kind)
             bank = bank_tile("%s%d" % (tag or kind, a), [P, FEAT])
-            codes, scales = latent_mx[pair, a]
+            codes, scales = latent_mx[pair]
             nc.tensor.matmul_mx(
                 out=bank[:],
-                lhsT=codes[:].bitcast(FP8X4),
-                lhsT_scale=scales[:],
+                lhsT=codes[:, SUB * a : SUB * (a + 1)].bitcast(FP8X4),
+                lhsT_scale=scales[:, SUB * a : SUB * (a + 1)],
                 rhs=wu_codes[:, part].bitcast(FP8X4),
                 rhs_scale=wu_scales[:, part],
                 start=True,
@@ -275,24 +280,18 @@ def tile_mla_pa_t_kernel(tc, x_bytes, x_scale, w_kv_down, w_kv_up, k_norm_w, fre
             )
             banks[kind, pair, a] = bank
 
-        def square_sums(pair, a, first=0, last=H):
-            if first == 0:
-                head_sums = work.tile([P, H], F32, tag="sums", bufs=SMALL_BUFS, name="sums")
-                sums[pair, a] = head_sums
-            for h in range(first, last):
-                squares = work.tile([P, D], BF16, tag="squares", bufs=SMALL_BUFS, name="squares")
-                nc.scalar.activation(out=squares[:], in_=banks["k", pair, a][:, D * h : D * (h + 1)], func=ACT.Square, accum_out=sums[pair, a][:, h : h + 1])
+        def square_sums(pair, a):
+            if a == 0:
+                head_sums = work.tile([P, 2, H], F32, tag="sums", name="sums")
+                rstd = work.tile([P, 2, H], F32, tag="rstd", name="rstd")
+                sums[pair], rstds[pair] = head_sums, rstd
+            squares = work.tile([P, FEAT], BF16, tag="squares", bufs=SMALL_BUFS, name="squares")
+            for h in range(H):
+                head = slice(D * h, D * (h + 1))
+                nc.scalar.activation(out=squares[:, head], in_=banks["k", pair, a][:, head], func=ACT.Square, accum_out=sums[pair][:, a, h : h + 1])
 
-        def inverse_rms(pair, a):
-            rstd = work.tile([P, H], F32, tag="rstd", bufs=SMALL_BUFS, name="rstd")
-            nc.scalar.activation(out=rstd[:], in_=sums[pair, a][:], func=ACT.Abs_reciprocal_sqrt, bias=EPS, scale=1.0 / D)
-            rstds[pair, a] = rstd
-
-        def both_square_sums(pair):
-            square_sums(pair, 0)
-            square_sums(pair, 1, 0, 1)
-            inverse_rms(pair, 0)
-            square_sums(pair, 1, 1, H)
+        def inverse_rms(pair, first=0, last=2):
+            nc.scalar.activation(out=rstds[pair][:, first:last], in_=sums[pair][:, first:last], func=ACT.Abs_reciprocal_sqrt, bias=EPS, scale=1.0 / D)
 
         def store(out, tile, pair, first, last):
             nc.sync.dma_start(
@@ -301,7 +300,9 @@ def tile_mla_pa_t_kernel(tc, x_bytes, x_scale, w_kv_down, w_kv_up, k_norm_w, fre
             )
 
         def values_out(pair, a, copy=nc.scalar.copy):
-            if a == 0:
+            if pair >= PAIRS - len(late_values):
+                values[pair] = late_values[PAIRS - 1 - pair]
+            elif a == 0:
                 v_tile = work.tile([P, 2 * FEAT], F32, tag="v_tile", name="v_tile")
                 values[pair] = v_tile
             copy(out=values[pair][:, FEAT * a : FEAT * (a + 1)], in_=banks["v", pair, a][:])
@@ -312,21 +313,21 @@ def tile_mla_pa_t_kernel(tc, x_bytes, x_scale, w_kv_down, w_kv_up, k_norm_w, fre
 
         def rotate(pair, a):
             if a == 0:
-                pair_quads = work.tile([P, 2, H, D, 2], F32, tag="quads", name="quads")
+                pair_quads = work.tile([P, 2, H, D, 2], F32, tag="quads", bufs=QUAD_BUFS, name="quads")
                 quads[pair] = pair_quads
             row = (2 * pair + a) % ROWS
             for h in range(H):
                 nc.vector.scalar_tensor_tensor(
                     out=quads[pair][:, a, h],
                     in0=banks["k", pair, a][:, D * h : D * (h + 1)].unsqueeze(2).broadcast_to([P, D, 2]),
-                    scalar=rstds[pair, a][:, h : h + 1],
+                    scalar=rstds[pair][:, a, h : h + 1],
                     in1=table[:, row].rearrange("p (d r) -> p d r", r=2),
                     op0=ALU.mult,
                     op1=ALU.mult,
                 )
 
         def keys_out(pair, first, last, adder):
-            keys = stages[(pair + 3) % STAGES]
+            keys = stages[(pair + 3) % PAIRS]
             halves = quads[pair][:, first:last].rearrange("p a h (e j) r -> p (a h) e (j r)", e=2)
             adder.tensor_tensor(
                 out=keys[:, FEAT * first : FEAT * last].rearrange("p (n d) -> p n d", d=D),
@@ -385,136 +386,133 @@ def tile_mla_pa_t_kernel(tc, x_bytes, x_scale, w_kv_down, w_kv_up, k_norm_w, fre
         latent_out(0, 0)
         latent_out(0, 1)
         wu_quant(0)
-        latent_quant(0, 0)
-        latent_quant(0, 1)
+        latent_quant(0)
         up(0, 0, "k")
         up(0, 1, "k")
         latent_out(1, 0)
         latent_out(1, 1)
         x_quant(2)
-        latent_quant(1, 0)
-        latent_quant(1, 1)
+        latent_quant(1)
         widen(5)
-        words_out(3)
-        words_scale(3)
         x_out(3, 0)
         x_out(3, 1)
+        words_out(3, nc.vector.tensor_copy)
+        words_scale(3)
         down(2, 0)
         down(2, 1)
         turn(4, 0)
         turn(4, 1)
         wu_turn(1, 0, "v0")
         wu_turn(1, 1, "v1")
-        both_square_sums(0)
+        square_sums(0, 0)
+        square_sums(0, 1)
         latent_out(2, 0)
-        inverse_rms(0, 1)
+        inverse_rms(0)
         latent_out(2, 1)
+        widen(6)
         rotate(0, 0)
         up(1, 0, "k")
         rotate(0, 1)
         up(1, 1, "k")
         wu_out(1, 0)
         wu_out(1, 1)
-        words_out(4, nc.vector.tensor_copy)
         square_sums(1, 0)
-        widen(6)
-        latent_quant(2, 0)
-        latent_quant(2, 1)
+        latent_quant(2)
         wu_quant(1)
+        up(0, 0, "v")
         x_quant(3)
 
         value_pair = 0
         for s in range(3, PAIRS - 2):
+            twice = s + 4 >= PAIRS
             keys_out(s - 3, 0, 2, nc.gpsimd)
-            words_scale(s + 1)
             down(s, 0)
-            up(value_pair, 0, "v")
+            up(value_pair, 1, "v")
             down(s, 1)
             x_out(s + 1, 0)
-            turn(s + 2, 0)
-            up(value_pair, 1, "v")
             x_out(s + 1, 1)
-            turn(s + 2, 1)
-            square_sums(s - 2, 1, 0, 1)
-            inverse_rms(s - 2, 0)
-            square_sums(s - 2, 1, 1, H)
-            latent_out(s, 0)
-            inverse_rms(s - 2, 1)
+            square_sums(s - 2, 1)
             values_out(value_pair, 0)
+            if twice:
+                up(value_pair + 1, 0, "v")
+            turn(s + 2, 0)
+            inverse_rms(s - 2)
+            latent_out(s, 0)
+            words_out(s + 1, nc.scalar.copy if s % 2 else nc.vector.tensor_copy)
+            words_scale(s + 1)
+            turn(s + 2, 1)
             latent_out(s, 1)
             values_out(value_pair, 1)
             value_pair += 1
-            if s + 4 < PAIRS:
-                widen(s + 4)
+            if twice:
+                up(value_pair, 1, "v")
+                values_out(value_pair, 0)
             else:
-                for a in range(2):
-                    up(value_pair, a, "v")
-                    values_out(value_pair, a)
-                value_pair += 1
+                widen(s + 4)
             rotate(s - 2, 0)
             up(s - 1, 0, "k")
+            square_sums(s - 1, 0)
+            if twice:
+                values_out(value_pair, 1)
+                value_pair += 1
+            if value_pair < s:
+                up(value_pair, 0, "v")
             rotate(s - 2, 1)
             up(s - 1, 1, "k")
-            words_out(s + 2, nc.scalar.copy if s % 2 else nc.vector.tensor_copy)
-            square_sums(s - 1, 0)
-            latent_quant(s, 0)
-            latent_quant(s, 1)
+            latent_quant(s)
             x_quant(s + 1)
 
         fourth, third, second, last = PAIRS - 4, PAIRS - 3, PAIRS - 2, PAIRS - 1
         keys_out(fourth - 1, 0, 2, nc.gpsimd)
-        words_scale(last)
-        down(second, 0)
         up(third, 0, "v")
+        down(second, 0)
+        up(third, 1, "v")
         down(second, 1)
         x_out(last, 0)
         up(third, 0, "k", "xt")
-        up(third, 1, "v")
         x_out(last, 1)
         up(third, 1, "k", "xt")
-        square_sums(fourth, 1, 0, 1)
-        inverse_rms(fourth, 0)
-        square_sums(fourth, 1, 1, H)
+        square_sums(fourth, 1)
         latent_out(second, 0)
-        inverse_rms(fourth, 1)
+        inverse_rms(fourth)
         latent_out(second, 1)
         rotate(fourth, 0)
-        rotate(fourth, 1)
-        latent_quant(second, 0)
-        latent_quant(second, 1)
+        latent_quant(second)
         x_quant(last)
+        keys_out(fourth, 0, 1, nc.gpsimd)
+        square_sums(third, 0)
+        square_sums(third, 1)
         values_out(third, 0)
-        both_square_sums(third)
+        inverse_rms(third)
         values_out(third, 1)
-        inverse_rms(third, 1)
-        keys_out(fourth, 0, 2, nc.gpsimd)
         up(second, 0, "k")
-        up(second, 1, "k")
         down(last, 0)
-        up(second, 0, "v")
         down(last, 1)
+        rotate(fourth, 1)
+        keys_out(fourth, 1, 2, nc.gpsimd)
+        up(second, 1, "k")
+        up(second, 0, "v")
         up(second, 1, "v")
-        square_sums(second, 0)
         latent_out(last, 0)
-        inverse_rms(second, 0)
         latent_out(last, 1)
+        square_sums(second, 0)
+        square_sums(second, 1)
         rotate(third, 0)
-        rotate(third, 1)
-        values_out(second, 0, nc.vector.tensor_copy)
-        latent_quant(last, 0)
-        latent_quant(last, 1)
+        latent_quant(last)
+        keys_out(third, 0, 1, nc.gpsimd)
         up(last, 0, "k", "xt")
-        up(last, 1, "k", "xt")
         up(last, 0, "v", "lat")
         up(last, 1, "v", "lat")
-        square_sums(second, 1)
-        values_out(second, 1)
-        inverse_rms(second, 1)
-        keys_out(third, 0, 1, nc.gpsimd)
-        both_square_sums(last)
-        values_out(last, 0)
+        rotate(third, 1)
         keys_out(third, 1, 2, nc.gpsimd)
-        inverse_rms(last, 1)
+        up(last, 1, "k", "xt")
+        values_out(second, 0)
+        inverse_rms(second)
+        square_sums(last, 0)
+        values_out(second, 1)
+        square_sums(last, 1)
+        values_out(last, 0)
+        inverse_rms(last)
         values_out(last, 1)
         rotate(second, 0)
         keys_out(second, 0, 1, nc.gpsimd)

@@ -24,10 +24,10 @@ FP8X4 = mybir.dt.float8_e4m3fn_x4
 ACT = mybir.ActivationFunctionType
 ALU = mybir.AluOpType
 
-WIDE_BUFS = 5
+WIDE_BUFS = 4
 SMALL_BUFS = 4
 QUAD_BUFS = 3
-CODE_BUFS = 5
+CODE_BUFS = 4
 SHARE = 128
 
 
@@ -103,8 +103,8 @@ def tile_mla_pa_t_kernel(tc, x_bytes, x_scale, w_kv_down, w_kv_up, k_norm_w, fre
         load_wu(0)
         load_x(4)
         load_trig()
-        load_x(5)
         load_wu(1)
+        load_x(5)
         for pair in range(6, PAIRS, 2):
             load_x(pair, 0, 4)
 
@@ -142,8 +142,7 @@ def tile_mla_pa_t_kernel(tc, x_bytes, x_scale, w_kv_down, w_kv_up, k_norm_w, fre
         stages = [keep.tile([P, 2 * FEAT], F32, align_bytes=64, name="stage%d" % i) for i in range(PAIRS - 4)]
         for grouped in (wd_grouped[:].rearrange("p th g n t -> p th (g n t)"), wu_grouped[:].rearrange("p part n t -> p part (n t)")):
             stages.extend(grouped[:, i].bitcast(F32) for i in range(2))
-        late_values = [keep.tile([P, 2 * FEAT], F32, name="late_values%d" % i) for i in range(2)]
-        late_values.extend(raw[:].rearrange("p i c -> p (i c)").bitcast(F32) for raw in wd_raw + wu_raw)
+        late_values = [keep.tile([P, 2 * FEAT], F32, name="late_values%d" % i) for i in range(4)]
 
         def turn_weight_rows(tag, rows):
             bank = bank_tile(tag, [P, 2, 2 * P])
@@ -398,65 +397,68 @@ def tile_mla_pa_t_kernel(tc, x_bytes, x_scale, w_kv_down, w_kv_up, k_norm_w, fre
         x_out(3, 1)
         words_out(3, nc.vector.tensor_copy)
         words_scale(3)
+        wu_turn(1, 0, "v0")
         down(2, 0)
+        wu_turn(1, 1, "v1")
         down(2, 1)
         turn(4, 0)
         turn(4, 1)
-        wu_turn(1, 0, "v0")
-        wu_turn(1, 1, "v1")
         square_sums(0, 0)
+        inverse_rms(0, 0, 1)
         square_sums(0, 1)
+        wu_out(1, 0)
+        inverse_rms(0, 1, 2)
+        wu_out(1, 1)
         latent_out(2, 0)
-        inverse_rms(0)
         latent_out(2, 1)
-        widen(6)
         rotate(0, 0)
         up(1, 0, "k")
-        rotate(0, 1)
-        up(1, 1, "k")
-        wu_out(1, 0)
-        wu_out(1, 1)
-        square_sums(1, 0)
-        latent_quant(2)
         wu_quant(1)
         up(0, 0, "v")
+        up(0, 1, "v")
+        rotate(0, 1)
+        up(1, 1, "k")
+        square_sums(1, 0)
+        values_out(0, 0)
+        up(1, 0, "v")
+        values_out(0, 1)
+        latent_quant(2)
         x_quant(3)
 
-        value_pair = 0
         for s in range(3, PAIRS - 2):
-            twice = s + 4 >= PAIRS
             keys_out(s - 3, 0, 2, nc.gpsimd)
             down(s, 0)
-            up(value_pair, 1, "v")
+            up(s - 2, 1, "v")
             down(s, 1)
             x_out(s + 1, 0)
             x_out(s + 1, 1)
+            words_out(s + 1, nc.vector.tensor_copy)
+            words_scale(s + 1)
             square_sums(s - 2, 1)
-            values_out(value_pair, 0)
-            if twice:
-                up(value_pair + 1, 0, "v")
-            turn(s + 2, 0)
+            values_out(s - 2, 0)
             inverse_rms(s - 2)
             latent_out(s, 0)
-            words_out(s + 1, nc.scalar.copy if s % 2 else nc.vector.tensor_copy)
-            words_scale(s + 1)
-            turn(s + 2, 1)
-            latent_out(s, 1)
-            values_out(value_pair, 1)
-            value_pair += 1
-            if twice:
-                up(value_pair, 1, "v")
-                values_out(value_pair, 0)
+            if s + 3 < PAIRS:
+                turn(s + 2, 0)
+                turn(s + 2, 1)
+                latent_out(s, 1)
+                values_out(s - 2, 1)
+                widen(s + 3)
+                rotate(s - 2, 0)
+                up(s - 1, 0, "k")
+                up(s - 1, 0, "v")
             else:
-                widen(s + 4)
-            rotate(s - 2, 0)
-            up(s - 1, 0, "k")
+                values_out(s - 2, 1)
+                up(s - 1, 0, "v")
+                turn(s + 2, 0)
+                up(s - 1, 1, "v")
+                turn(s + 2, 1)
+                latent_out(s, 1)
+                values_out(s - 1, 0)
+                values_out(s - 1, 1)
+                rotate(s - 2, 0)
+                up(s - 1, 0, "k")
             square_sums(s - 1, 0)
-            if twice:
-                values_out(value_pair, 1)
-                value_pair += 1
-            if value_pair < s:
-                up(value_pair, 0, "v")
             rotate(s - 2, 1)
             up(s - 1, 1, "k")
             latent_quant(s)
@@ -464,14 +466,14 @@ def tile_mla_pa_t_kernel(tc, x_bytes, x_scale, w_kv_down, w_kv_up, k_norm_w, fre
 
         fourth, third, second, last = PAIRS - 4, PAIRS - 3, PAIRS - 2, PAIRS - 1
         keys_out(fourth - 1, 0, 2, nc.gpsimd)
-        up(third, 0, "v")
         down(second, 0)
-        up(third, 1, "v")
         down(second, 1)
         x_out(last, 0)
         up(third, 0, "k", "xt")
         x_out(last, 1)
         up(third, 1, "k", "xt")
+        up(third, 0, "v")
+        up(third, 1, "v")
         square_sums(fourth, 1)
         latent_out(second, 0)
         inverse_rms(fourth)
@@ -484,35 +486,36 @@ def tile_mla_pa_t_kernel(tc, x_bytes, x_scale, w_kv_down, w_kv_up, k_norm_w, fre
         square_sums(third, 1)
         values_out(third, 0)
         inverse_rms(third)
-        values_out(third, 1)
         up(second, 0, "k")
+        square_sums(second, 0)
         down(last, 0)
         down(last, 1)
         rotate(fourth, 1)
         keys_out(fourth, 1, 2, nc.gpsimd)
-        up(second, 1, "k")
         up(second, 0, "v")
-        up(second, 1, "v")
+        up(second, 1, "k")
         latent_out(last, 0)
         latent_out(last, 1)
-        square_sums(second, 0)
         square_sums(second, 1)
+        values_out(third, 1)
+        inverse_rms(second)
         rotate(third, 0)
+        values_out(second, 0, nc.vector.tensor_copy)
         latent_quant(last)
         keys_out(third, 0, 1, nc.gpsimd)
         up(last, 0, "k", "xt")
+        up(second, 1, "v")
         up(last, 0, "v", "lat")
         up(last, 1, "v", "lat")
         rotate(third, 1)
         keys_out(third, 1, 2, nc.gpsimd)
         up(last, 1, "k", "xt")
-        values_out(second, 0)
-        inverse_rms(second)
         square_sums(last, 0)
         values_out(second, 1)
+        inverse_rms(last, 0, 1)
         square_sums(last, 1)
         values_out(last, 0)
-        inverse_rms(last)
+        inverse_rms(last, 1, 2)
         values_out(last, 1)
         rotate(second, 0)
         keys_out(second, 0, 1, nc.gpsimd)

@@ -26,6 +26,8 @@ ALU = mybir.AluOpType
 
 WIDE_BUFS = 4
 SMALL_BUFS = 4
+FIRST_PAIRED = 4
+RUN = 4
 QUAD_BUFS = 3
 CODE_BUFS = 4
 SHARE = 128
@@ -159,7 +161,7 @@ def tile_mla_pa_t_kernel(tc, x_bytes, x_scale, w_kv_down, w_kv_up, k_norm_w, fre
 
         def wd_out(th, g, copy=nc.scalar.copy):
             words = wd_grouped[:, th, g].rearrange("p n t -> p (n t)").bitcast(F32)
-            copy(out=words.rearrange("p (n u) -> p n u", u=2), in_=banks["wd", th, g][:].rearrange("p u n -> p n u"))
+            copy(out=words.rearrange("p (c i u) -> p c u i", i=RUN, u=2), in_=banks["wd", th, g][:].rearrange("p u (c i) -> p c u i", i=RUN))
 
         def wu_out(part, i, copy=nc.scalar.copy):
             words = wu_grouped[:, part, 2 * P * i : 2 * P * (i + 1)].rearrange("p n t -> p (n t)").bitcast(F32)
@@ -167,7 +169,7 @@ def tile_mla_pa_t_kernel(tc, x_bytes, x_scale, w_kv_down, w_kv_up, k_norm_w, fre
             if part == 0:
                 copy(out=words.rearrange("p (h e j u) -> p h e j u", h=2, e=2, u=2), in_=bank[:].rearrange("p u (h j e) -> p h e j u", h=2, e=2))
             else:
-                copy(out=words.rearrange("p (n u) -> p n u", u=2), in_=bank[:].rearrange("p u n -> p n u"))
+                copy(out=words.rearrange("p (c i u) -> p c u i", i=RUN, u=2), in_=bank[:].rearrange("p u (c i) -> p c u i", i=RUN))
 
         def wd_quant(th):
             nc.vector.quantize_mx(
@@ -188,11 +190,12 @@ def tile_mla_pa_t_kernel(tc, x_bytes, x_scale, w_kv_down, w_kv_up, k_norm_w, fre
             copy(out=wide[pair][:, C * first : C * last], in_=x_tiles[pair][:, first:last].rearrange("p a c -> p (a c)").bitcast(FP8))
 
         def turn(pair, g, tag=None):
-            bank = bank_tile(tag or "xt%d" % g, [P, 2, 2 * SUB])
+            bank = bank_tile(tag or "xt%d" % g, [P, 4 * SUB])
+            turned = bank[:].rearrange("p (u n) -> p n u" if pair < FIRST_PAIRED else "p (n u) -> p n u", u=2)
             for a in range(2):
                 rows = wide[pair][:, C * a + PASS * g : C * a + PASS * (g + 1)]
                 for u in range(2):
-                    nc.tensor.transpose(bank[:, u, SUB * a : SUB * (a + 1)], rows.bitcast(F32)[:, u:WORDS:2], ident[:])
+                    nc.tensor.transpose(turned[:, SUB * a : SUB * (a + 1), u], rows.bitcast(F32)[:, u:WORDS:2], ident[:])
             banks["xt", pair, g] = bank
 
         def scale_x(engine, pair, g, turned, first, last):
@@ -207,7 +210,7 @@ def tile_mla_pa_t_kernel(tc, x_bytes, x_scale, w_kv_down, w_kv_up, k_norm_w, fre
             first = share(pair) if g == 1 else 0
             if first == 2 * SUB:
                 return
-            bank = banks["xt", pair, g][:].rearrange("p u n -> p (u n)").bitcast(BF16).rearrange("p (u n e) -> p n u e", u=2, e=2)
+            bank = banks["xt", pair, g][:].bitcast(BF16).rearrange("p (u n e) -> p n u e" if pair < FIRST_PAIRED else "p (n u e) -> p n u e", u=2, e=2)
             scale_x(nc.vector, pair, g, bank[:, first:], first, 2 * SUB)
 
         def words_out(pair, copy=nc.scalar.copy):
@@ -215,7 +218,7 @@ def tile_mla_pa_t_kernel(tc, x_bytes, x_scale, w_kv_down, w_kv_up, k_norm_w, fre
                 part = stages[pair - 1][:, 0 : 2 * share(pair)].rearrange("p (n u) -> p n u", u=2)
             else:
                 part = work.tile([P, share(pair), 2], F32, tag="words", align_bytes=64, name="words")
-            copy(out=part[:], in_=banks["xt", pair, 1][:, :, 0 : share(pair)].rearrange("p u n -> p n u"))
+            copy(out=part[:], in_=banks["xt", pair, 1][:].rearrange("p (u n) -> p n u" if pair < FIRST_PAIRED else "p (n u) -> p n u", u=2)[:, 0 : share(pair)])
             words[pair] = part
 
         def words_scale(pair):
@@ -256,7 +259,10 @@ def tile_mla_pa_t_kernel(tc, x_bytes, x_scale, w_kv_down, w_kv_up, k_norm_w, fre
             elif a == 0:
                 latent = work.tile([P, 2 * SUB * 4], BF16, tag="latent", align_bytes=64, name="latent")
                 latents[pair] = latent
-            copy(out=latents[pair][:].rearrange("p (a n t) -> p a n t", a=2, t=4)[:, a], in_=banks["lat", pair, a][:].rearrange("p t n -> p n t"))
+            copy(
+                out=latents[pair][:, 4 * SUB * a : 4 * SUB * (a + 1)].rearrange("p (c i t) -> p c t i", i=RUN, t=4),
+                in_=banks["lat", pair, a][:].rearrange("p t (c i) -> p c t i", i=RUN),
+            )
 
         def latent_quant(pair):
             codes = work.tile([P, 2 * SUB], U32, tag="l_q", bufs=CODE_BUFS, align_bytes=64, name="l_q")
@@ -432,12 +438,16 @@ def tile_mla_pa_t_kernel(tc, x_bytes, x_scale, w_kv_down, w_kv_up, k_norm_w, fre
             down(s, 1)
             x_out(s + 1, 0)
             x_out(s + 1, 1)
-            words_out(s + 1, nc.vector.tensor_copy)
-            words_scale(s + 1)
+            if s % 2 == 0:
+                words_out(s + 1, nc.vector.tensor_copy)
+                words_scale(s + 1)
             square_sums(s - 2, 1)
             values_out(s - 2, 0)
             inverse_rms(s - 2)
             latent_out(s, 0)
+            if s % 2 == 1:
+                words_out(s + 1)
+                words_scale(s + 1)
             if s + 3 < PAIRS:
                 turn(s + 2, 0)
                 turn(s + 2, 1)

@@ -50,16 +50,15 @@ def tile_mla_pa_t_kernel(tc, x_bytes, x_scale, w_kv_down, w_kv_up, k_norm_w, fre
         table_warm = keep.tile([P, 1], F32)
         nc.scalar.activation(out=table_warm[:], in_=one[:], func=ACT.Abs_reciprocal_sqrt)
 
-        ident = keep.tile([P, P], F32)
-        make_identity(nc, ident[:])
-
         scale = keep.tile([P, 2, 4], F32)
         trig = keep.tile([P, 2, ROWS * HALF], BF16)
         gain_row = keep.tile([P, D], BF16)
-        nc.vector.memset(gain_row[:], 0.0)
+        nc.gpsimd.memset(gain_row[:], 0.0)
         signs = keep.tile([P, 2, P], BF16)
-        nc.vector.memset(signs[:, 0], -1.0)
-        nc.vector.memset(signs[:, 1], 1.0)
+        ident = keep.tile([P, P], F32)
+        make_identity(nc, ident[:])
+        nc.gpsimd.memset(signs[:, 0], -1.0)
+        nc.gpsimd.memset(signs[:, 1], 1.0)
         wd_raw = [keep.tile([P, 2, C], BF16, align_bytes=64, name="wd_raw%d" % th) for th in range(2)]
         wu_raw = [keep.tile([P, 4, R], BF16, align_bytes=64, name="wu_raw%d" % part) for part in range(2)]
         wd_view = w_kv_down.rearrange("(m t) k -> m t k", t=4)
@@ -95,9 +94,9 @@ def tile_mla_pa_t_kernel(tc, x_bytes, x_scale, w_kv_down, w_kv_up, k_norm_w, fre
 
         load_x(0, 0, 1)
         load_x(0, 1, 2)
+        load_gain()
         load_scale()
         load_x(1)
-        load_gain()
         load_x(2)
         load_wd(0)
         load_x(3)
@@ -254,9 +253,9 @@ def tile_mla_pa_t_kernel(tc, x_bytes, x_scale, w_kv_down, w_kv_up, k_norm_w, fre
             banks["lat", pair, a] = bank
 
         def latent_out(pair, a, copy=nc.scalar.copy):
-            if a == 0 and pair == PAIRS - 1:
+            if pair not in latents and pair == PAIRS - 1:
                 latents[pair] = stages[0][:, 0:FEAT].bitcast(BF16)
-            elif a == 0:
+            elif pair not in latents:
                 latent = work.tile([P, 2 * SUB * 4], BF16, tag="latent", align_bytes=64, name="latent")
                 latents[pair] = latent
             copy(
@@ -311,7 +310,7 @@ def tile_mla_pa_t_kernel(tc, x_bytes, x_scale, w_kv_down, w_kv_up, k_norm_w, fre
                 v_tile = work.tile([P, 2 * FEAT], F32, tag="v_tile", name="v_tile")
                 values[pair] = v_tile
             copy(out=values[pair][:, FEAT * a : FEAT * (a + 1)], in_=banks["v", pair, a][:])
-            if pair >= PAIRS - 2:
+            if pair >= PAIRS - 3:
                 store(out_1, values[pair], pair, a, a + 1)
             elif a == 1:
                 store(out_1, values[pair], pair, 0, 2)
@@ -332,23 +331,19 @@ def tile_mla_pa_t_kernel(tc, x_bytes, x_scale, w_kv_down, w_kv_up, k_norm_w, fre
                 )
 
         def keys_out(pair, first, last, adder):
-            keys = stages[(pair + 3) % PAIRS]
-            halves = quads[pair][:, first:last].rearrange("p a h (e j) r -> p (a h) e (j r)", e=2)
-            adder.tensor_tensor(
-                out=keys[:, FEAT * first : FEAT * last].rearrange("p (n d) -> p n d", d=D),
-                in0=halves[:, :, 0, :],
-                in1=halves[:, :, 1, :],
-                op=ALU.add,
-            )
-            store(out_0, keys, pair, first, last)
+            keys = stages[(pair + 3) % PAIRS][:, D * first : D * last]
+            halves = quads[pair][:].rearrange("p a h (e j) r -> p (a h) e (j r)", e=2)[:, first:last]
+            adder.tensor_tensor(out=keys.rearrange("p (n d) -> p n d", d=D), in0=halves[:, :, 0, :], in1=halves[:, :, 1, :], op=ALU.add)
+            rows = pair_rows(out_0.rearrange("b t h d -> b t (h d)"), pair, 0, 2).rearrange("p a f -> p (a f)")
+            nc.sync.dma_start(out=rows[:, D * first : D * last], in_=keys)
 
         widen(0, 0, 1, nc.vector.tensor_copy)
         widen(0, 1, 2)
         widen(1)
         widen(2)
+        spread_gain("k1")
         turn(0, 0)
         turn(0, 1)
-        spread_gain("k1")
         turn(1, 1, "v1")
         turn(1, 0, "v0")
         wd_turn(0, 0, "lat0")
@@ -432,7 +427,7 @@ def tile_mla_pa_t_kernel(tc, x_bytes, x_scale, w_kv_down, w_kv_up, k_norm_w, fre
         x_quant(3)
 
         for s in range(3, PAIRS - 2):
-            keys_out(s - 3, 0, 2, nc.gpsimd)
+            keys_out(s - 3, 0, 2 * H, nc.gpsimd)
             down(s, 0)
             up(s - 2, 1, "v")
             down(s, 1)
@@ -442,8 +437,9 @@ def tile_mla_pa_t_kernel(tc, x_bytes, x_scale, w_kv_down, w_kv_up, k_norm_w, fre
                 words_out(s + 1, nc.vector.tensor_copy)
                 words_scale(s + 1)
             square_sums(s - 2, 1)
+            inverse_rms(s - 2, 0, 1)
             values_out(s - 2, 0)
-            inverse_rms(s - 2)
+            inverse_rms(s - 2, 1, 2)
             latent_out(s, 0)
             if s % 2 == 1:
                 words_out(s + 1)
@@ -475,63 +471,67 @@ def tile_mla_pa_t_kernel(tc, x_bytes, x_scale, w_kv_down, w_kv_up, k_norm_w, fre
             x_quant(s + 1)
 
         fourth, third, second, last = PAIRS - 4, PAIRS - 3, PAIRS - 2, PAIRS - 1
-        keys_out(fourth - 1, 0, 2, nc.gpsimd)
+        keys_out(fourth - 1, 0, 2 * H, nc.gpsimd)
         down(second, 0)
         down(second, 1)
         x_out(last, 0)
         up(third, 0, "k", "xt")
+        up(third, 0, "v")
         x_out(last, 1)
         up(third, 1, "k", "xt")
-        up(third, 0, "v")
         up(third, 1, "v")
         square_sums(fourth, 1)
+        inverse_rms(fourth, 0, 1)
         latent_out(second, 0)
-        inverse_rms(fourth)
+        inverse_rms(fourth, 1, 2)
         latent_out(second, 1)
         rotate(fourth, 0)
         latent_quant(second)
         x_quant(last)
-        keys_out(fourth, 0, 1, nc.gpsimd)
         square_sums(third, 0)
-        square_sums(third, 1)
         values_out(third, 0)
-        inverse_rms(third)
+        inverse_rms(third, 0, 1)
+        square_sums(third, 1)
+        values_out(third, 1)
+        keys_out(fourth, 0, H, nc.gpsimd)
+        inverse_rms(third, 1, 2)
         up(second, 0, "k")
-        square_sums(second, 0)
         down(last, 0)
         down(last, 1)
         rotate(fourth, 1)
-        keys_out(fourth, 1, 2, nc.gpsimd)
+        keys_out(fourth, H, 2 * H, nc.gpsimd)
         up(second, 0, "v")
         up(second, 1, "k")
+        up(second, 1, "v")
         latent_out(last, 0)
         latent_out(last, 1)
-        square_sums(second, 1)
-        values_out(third, 1)
-        inverse_rms(second)
+        square_sums(second, 0)
         rotate(third, 0)
         values_out(second, 0, nc.vector.tensor_copy)
         latent_quant(last)
-        keys_out(third, 0, 1, nc.gpsimd)
         up(last, 0, "k", "xt")
-        up(second, 1, "v")
         up(last, 0, "v", "lat")
         up(last, 1, "v", "lat")
         rotate(third, 1)
-        keys_out(third, 1, 2, nc.gpsimd)
         up(last, 1, "k", "xt")
-        square_sums(last, 0)
         values_out(second, 1)
+        keys_out(third, 0, H, nc.gpsimd)
+        inverse_rms(second, 0, 1)
+        square_sums(second, 1)
+        values_out(last, 0)
+        keys_out(third, H, 2 * H, nc.gpsimd)
+        inverse_rms(second, 1, 2)
+        square_sums(last, 0)
+        values_out(last, 1)
         inverse_rms(last, 0, 1)
         square_sums(last, 1)
-        values_out(last, 0)
         inverse_rms(last, 1, 2)
-        values_out(last, 1)
         rotate(second, 0)
-        keys_out(second, 0, 1, nc.gpsimd)
+        keys_out(second, 0, H, nc.gpsimd)
         rotate(second, 1)
-        keys_out(second, 1, 2, nc.gpsimd)
+        keys_out(second, H, 2 * H, nc.gpsimd)
         rotate(last, 0)
+        keys_out(last, 0, 2, nc.gpsimd)
         rotate(last, 1)
-        keys_out(last, 0, 1, nc.vector)
-        keys_out(last, 1, 2, nc.vector)
+        keys_out(last, 2, 5, nc.vector)
+        keys_out(last, 5, 8, nc.vector)

@@ -62,12 +62,12 @@ def tile_mla_pa_t_kernel(tc, x_bytes, x_scale, w_kv_down, w_kv_up, k_norm_w, fre
         wd_raw = [keep.tile([P, 2, C], BF16, align_bytes=64, name="wd_raw%d" % th) for th in range(2)]
         wu_raw = [keep.tile([P, 4, R], BF16, align_bytes=64, name="wu_raw%d" % part) for part in range(2)]
         wd_view = w_kv_down.rearrange("(m t) k -> m t k", t=4)
-        wu_view = w_kv_up.rearrange("(c m) r -> m c r", m=P)
+        wu_view = w_kv_up.rearrange("(part m c) r -> part m c r", part=2, c=4)
         x_tiles = {}
 
         def pair_rows(tensor, pair, first, last):
-            b, s, q = pair // 4, pair // 2 % 2, 2 * (pair % 2)
-            return tensor[b].rearrange("(s p q) f -> s p q f", p=P, q=4)[s][:, q + first : q + last, :]
+            b, q = divmod(2 * pair, ROWS)
+            return tensor[b].rearrange("(p q) f -> p q f", q=ROWS)[:, q + first : q + last, :]
 
         def load_x(pair, first=0, last=2):
             if first == 0:
@@ -84,26 +84,26 @@ def tile_mla_pa_t_kernel(tc, x_bytes, x_scale, w_kv_down, w_kv_up, k_norm_w, fre
 
         def load_trig():
             for slot, angles in enumerate((freqs_cos, freqs_sin)):
-                nc.sync.dma_start(out=trig[:, slot].rearrange("p (s c) -> p s c", s=2), in_=angles.rearrange("(s p q) j -> p s (q j)", p=P, q=4))
+                nc.sync.dma_start(out=trig[:, slot], in_=angles.rearrange("(p q) j -> p (q j)", q=ROWS))
 
         def load_wd(th):
             nc.sync.dma_start(out=wd_raw[th][:], in_=wd_view[:, 2 * th : 2 * th + 2, :])
 
         def load_wu(part):
-            nc.sync.dma_start(out=wu_raw[part][:], in_=wu_view[:, 4 * part : 4 * part + 4, :])
+            nc.sync.dma_start(out=wu_raw[part][:], in_=wu_view[part])
 
         load_x(0, 0, 1)
         load_x(0, 1, 2)
         load_gain()
         load_scale()
         load_x(1)
-        load_x(2)
         load_wd(0)
-        load_x(3)
+        load_x(2)
         load_wd(1)
         load_wu(0)
-        load_x(4)
+        load_x(3)
         load_trig()
+        load_x(4)
         load_wu(1)
         load_x(5)
         for pair in range(6, PAIRS, 2):
@@ -156,19 +156,16 @@ def tile_mla_pa_t_kernel(tc, x_bytes, x_scale, w_kv_down, w_kv_up, k_norm_w, fre
             banks["wd", th, g] = turn_weight_rows(tag, [wd_raw[th][:, i, PASS * g : PASS * (g + 1)] for i in range(2)])
 
         def wu_turn(part, i, tag):
-            banks["wu", part, i] = turn_weight_rows(tag, [wu_raw[part][:, 2 * i + j, :] for j in range(2)])
+            banks["wu", part, i] = turn_weight_rows(tag, [wu_raw[part][:, i + 2 * j if part == 0 else 2 * i + j, :] for j in range(2)])
 
         def wd_out(th, g, copy=nc.scalar.copy):
             words = wd_grouped[:, th, g].rearrange("p n t -> p (n t)").bitcast(F32)
             copy(out=words.rearrange("p (c i u) -> p c u i", i=RUN, u=2), in_=banks["wd", th, g][:].rearrange("p u (c i) -> p c u i", i=RUN))
 
-        def wu_out(part, i, copy=nc.scalar.copy):
-            words = wu_grouped[:, part, 2 * P * i : 2 * P * (i + 1)].rearrange("p n t -> p (n t)").bitcast(F32)
-            bank = banks["wu", part, i]
-            if part == 0:
-                copy(out=words.rearrange("p (h e j u) -> p h e j u", h=2, e=2, u=2), in_=bank[:].rearrange("p u (h j e) -> p h e j u", h=2, e=2))
-            else:
-                copy(out=words.rearrange("p (c i u) -> p c u i", i=RUN, u=2), in_=bank[:].rearrange("p u (c i) -> p c u i", i=RUN))
+        def wu_out(part, e, copy=nc.scalar.copy):
+            words = wu_grouped[:, part].rearrange("p n t -> p (n t)").bitcast(F32)
+            order = "p (h e m j u) -> p e h m j u" if part == 0 else "p (h m e j u) -> p e h m j u"
+            copy(out=words.rearrange(order, h=H, e=2, j=2, u=2)[:, e], in_=banks["wu", part, e][:].rearrange("p u (j h m) -> p h m j u", j=2, h=H))
 
         def wd_quant(th):
             nc.vector.quantize_mx(
@@ -339,8 +336,8 @@ def tile_mla_pa_t_kernel(tc, x_bytes, x_scale, w_kv_down, w_kv_up, k_norm_w, fre
 
         widen(0, 0, 1, nc.vector.tensor_copy)
         widen(0, 1, 2)
-        widen(1)
-        widen(2)
+        widen(1, 0, 1, nc.vector.tensor_copy)
+        widen(1, 1, 2)
         spread_gain("k1")
         turn(0, 0)
         turn(0, 1)
@@ -356,14 +353,14 @@ def tile_mla_pa_t_kernel(tc, x_bytes, x_scale, w_kv_down, w_kv_up, k_norm_w, fre
         words_scale(1)
         x_out(1, 0)
         x_out(1, 1)
+        widen(2)
         turn(2, 0, "v1")
         turn(2, 1)
-        widen(3)
         wd_out(0, 0)
         wd_out(0, 1)
         wd_out(1, 0)
         wd_out(1, 1)
-        widen(4)
+        widen(3)
         wu_turn(0, 0, "v0")
         wu_turn(0, 1, "k0")
         x_quant(0)
@@ -376,6 +373,7 @@ def tile_mla_pa_t_kernel(tc, x_bytes, x_scale, w_kv_down, w_kv_up, k_norm_w, fre
         words_scale(2)
         wu_out(0, 0)
         wu_out(0, 1)
+        widen(4)
         down(1, 0, "xt0")
         down(1, 1, "v0")
         x_out(2, 0)
@@ -402,8 +400,8 @@ def tile_mla_pa_t_kernel(tc, x_bytes, x_scale, w_kv_down, w_kv_up, k_norm_w, fre
         down(2, 0)
         wu_turn(1, 1, "v1")
         down(2, 1)
-        turn(4, 0)
         turn(4, 1)
+        turn(4, 0)
         square_sums(0, 0)
         inverse_rms(0, 0, 1)
         square_sums(0, 1)
@@ -414,51 +412,57 @@ def tile_mla_pa_t_kernel(tc, x_bytes, x_scale, w_kv_down, w_kv_up, k_norm_w, fre
         latent_out(2, 1)
         rotate(0, 0)
         up(1, 0, "k")
+        rotate(0, 1)
+        up(1, 1, "k")
         wu_quant(1)
         up(0, 0, "v")
         up(0, 1, "v")
-        rotate(0, 1)
-        up(1, 1, "k")
+        widen(6)
         square_sums(1, 0)
-        values_out(0, 0)
-        up(1, 0, "v")
-        values_out(0, 1)
         latent_quant(2)
         x_quant(3)
 
         for s in range(3, PAIRS - 2):
             keys_out(s - 3, 0, 2 * H, nc.gpsimd)
             down(s, 0)
-            up(s - 2, 1, "v")
+            if s > 3:
+                up(s - 2, 1, "v")
             down(s, 1)
-            x_out(s + 1, 0)
             x_out(s + 1, 1)
-            if s % 2 == 0:
+            if s % 3 == 0:
                 words_out(s + 1, nc.vector.tensor_copy)
                 words_scale(s + 1)
+            x_out(s + 1, 0)
             square_sums(s - 2, 1)
             inverse_rms(s - 2, 0, 1)
-            values_out(s - 2, 0)
+            values_out(s - 2 if s > 3 else 0, 0)
             inverse_rms(s - 2, 1, 2)
-            latent_out(s, 0)
-            if s % 2 == 1:
+            if s == 3:
+                values_out(0, 1)
+                up(1, 0, "v")
+                up(1, 1, "v")
+            if s % 3 != 0:
                 words_out(s + 1)
                 words_scale(s + 1)
+            latent_out(s, 0)
             if s + 3 < PAIRS:
-                turn(s + 2, 0)
                 turn(s + 2, 1)
+                turn(s + 2, 0)
                 latent_out(s, 1)
+                if s == 3:
+                    values_out(1, 0)
+                else:
+                    widen(s + 3)
                 values_out(s - 2, 1)
-                widen(s + 3)
                 rotate(s - 2, 0)
                 up(s - 1, 0, "k")
                 up(s - 1, 0, "v")
             else:
                 values_out(s - 2, 1)
                 up(s - 1, 0, "v")
-                turn(s + 2, 0)
-                up(s - 1, 1, "v")
                 turn(s + 2, 1)
+                up(s - 1, 1, "v")
+                turn(s + 2, 0)
                 latent_out(s, 1)
                 values_out(s - 1, 0)
                 values_out(s - 1, 1)

from contextlib import ExitStack

import concourse.mybir as mybir
from concourse.masks import make_identity

B, T, C, H, D, R = 4, 1024, 1024, 4, 128, 512
EPS = 1e-6
P = 128
SUB = 128
PAIRS = B * T // (2 * SUB)
PASS = 512
WORDS = PASS // 2
FEAT = H * D
HALF = D // 2
ROWS = T // P
FLOPS = 2 * B * T * C * R + 2 * B * T * R * 2 * FEAT + 10 * B * T * FEAT

F32 = mybir.dt.float32
BF16 = mybir.dt.bfloat16
U32 = mybir.dt.uint32
U8 = mybir.dt.uint8
FP8 = mybir.dt.float8_e4m3fn
FP8X4 = mybir.dt.float8_e4m3fn_x4
ACT = mybir.ActivationFunctionType
ALU = mybir.AluOpType

WIDE_BUFS = 4
SMALL_BUFS = 4
FIRST_PAIRED = 4
RUN = 4
QUAD_BUFS = 3
CODE_BUFS = 4
SHARE = 128


def share(pair):
    return 0 if pair in (0, PAIRS - 1) else 2 * SUB if pair == 2 else SHARE


def tile_mla_pa_t_kernel(tc, x_bytes, x_scale, w_kv_down, w_kv_up, k_norm_w, freqs_cos, freqs_sin, out_0, out_1):
    nc = tc.nc
    with ExitStack() as ctx:
        keep = ctx.enter_context(tc.tile_pool(name="keep", bufs=1))
        work = ctx.enter_context(tc.tile_pool(name="work", bufs=3))
        psum = ctx.enter_context(tc.psum_pool(name="psum", bufs=1))
        ctx.enter_context(tc.manual_schedule())

        one = keep.tile([P, 1], F32)
        nc.vector.memset(one[:], 1.0)
        table_warm = keep.tile([P, 1], F32)
        nc.scalar.activation(out=table_warm[:], in_=one[:], func=ACT.Abs_reciprocal_sqrt)

        scale = keep.tile([P, 2, 4], F32)
        trig = keep.tile([P, 2, ROWS * HALF], BF16)
        gain_row = keep.tile([P, D], BF16)
        nc.gpsimd.memset(gain_row[:], 0.0)
        signs = keep.tile([P, 2, P], BF16)
        ident = keep.tile([P, P], F32)
        make_identity(nc, ident[:])
        nc.gpsimd.memset(signs[:, 0], -1.0)
        nc.gpsimd.memset(signs[:, 1], 1.0)
        wd_raw = [keep.tile([P, 2, C], BF16, align_bytes=64, name="wd_raw%d" % th) for th in range(2)]
        wu_raw = [keep.tile([P, 4, R], BF16, align_bytes=64, name="wu_raw%d" % part) for part in range(2)]
        wd_view = w_kv_down.rearrange("(m t) k -> m t k", t=4)
        wu_view = w_kv_up.rearrange("(part m c) r -> part m c r", part=2, c=4)
        x_tiles = {}

        def pair_rows(tensor, pair, first, last):
            b, q = divmod(2 * pair, ROWS)
            return tensor[b].rearrange("(p q) f -> p q f", q=ROWS)[:, q + first : q + last, :]

        def load_x(pair, first=0, last=2):
            if first == 0:
                x_codes = keep.tile([P, max(last, 2), C], U8, align_bytes=64, name="x_codes%d" % pair)
                for i in range(max(last, 2) // 2):
                    x_tiles[pair + i] = x_codes[:, 2 * i : 2 * i + 2]
            nc.sync.dma_start(out=x_tiles[pair][:, first:last] if last <= 2 else x_codes[:], in_=pair_rows(x_bytes, pair, first, last))

        def load_scale():
            nc.sync.dma_start(out=scale[:], in_=x_scale[0, 0].rearrange("(g p t) -> p g t", p=P, t=4))

        def load_gain():
            nc.sync.dma_start(out=gain_row[0:1, :], in_=k_norm_w.unsqueeze(0))

        def load_trig():
            for slot, angles in enumerate((freqs_cos, freqs_sin)):
                nc.sync.dma_start(out=trig[:, slot], in_=angles.rearrange("(p q) j -> p (q j)", q=ROWS))

        def load_wd(th):
            nc.sync.dma_start(out=wd_raw[th][:], in_=wd_view[:, 2 * th : 2 * th + 2, :])

        def load_wu(part):
            nc.sync.dma_start(out=wu_raw[part][:], in_=wu_view[part])

        load_x(0, 0, 1)
        load_x(0, 1, 2)
        load_gain()
        load_scale()
        load_x(1)
        load_wd(0)
        load_x(2)
        load_wd(1)
        load_wu(0)
        load_x(3)
        load_trig()
        load_x(4)
        load_wu(1)
        load_x(5)
        for pair in range(6, PAIRS, 2):
            load_x(pair, 0, 4)

        banks = {}

        def bank_tile(tag, shape):
            bank = psum.tile(shape, F32, tag=tag, name="bank")
            return bank

        table = keep.tile([P, ROWS, 2 * D], F32)

        def spread_gain(tag):
            bank = bank_tile(tag, [P, 2, D])
            for sign in range(2):
                nc.tensor.matmul(bank[:, sign], lhsT=signs[:, sign], rhs=gain_row[:], start=True, stop=True)
            banks["gain"] = bank

        def table_rows(first, last):
            rows = last - first
            gains = banks["gain"][:].rearrange("p r (j e) -> p e j r", e=2)
            for e, gain in enumerate((gains[:, 0, :, 1:2].broadcast_to([P, HALF, 2]), gains[:, 1])):
                nc.vector.tensor_tensor(
                    out=table[:, first:last].rearrange("p n (e j r) -> p n e j r", e=2, r=2)[:, :, e],
                    in0=trig[:, :: 1 - 2 * e, HALF * first : HALF * last].rearrange("p r (n j) -> p n j r", j=HALF),
                    in1=gain.unsqueeze(1).broadcast_to([P, rows, HALF, 2]),
                    op=ALU.mult,
                )

        wd_grouped = keep.tile([P, 2, 2, 2 * P, 4], BF16, align_bytes=64)
        wu_grouped = keep.tile([P, 2, FEAT, 4], BF16, align_bytes=64)
        wd_codes = keep.tile([P, 2, 2, 2 * P], U32, align_bytes=64)
        wd_scales = keep.tile([P, 2, 2, 2 * P], U8, align_bytes=64)
        wu_codes = keep.tile([P, 2, FEAT], U32, align_bytes=64)
        wu_scales = keep.tile([P, 2, FEAT], U8, align_bytes=64)
        stages = [keep.tile([P, 2 * FEAT], F32, align_bytes=64, name="stage%d" % i) for i in range(PAIRS - 4)]
        for grouped in (wd_grouped[:].rearrange("p th g n t -> p th (g n t)"), wu_grouped[:].rearrange("p part n t -> p part (n t)")):
            stages.extend(grouped[:, i].bitcast(F32) for i in range(2))
        late_values = [keep.tile([P, 2 * FEAT], F32, name="late_values%d" % i) for i in range(4)]

        def turn_weight_rows(tag, rows):
            bank = bank_tile(tag, [P, 2, 2 * P])
            for i, block in enumerate(rows):
                for u in range(2):
                    nc.tensor.transpose(bank[:, u, P * i : P * (i + 1)], block.bitcast(F32)[:, u:WORDS:2], ident[:])
            return bank

        def wd_turn(th, g, tag):
            banks["wd", th, g] = turn_weight_rows(tag, [wd_raw[th][:, i, PASS * g : PASS * (g + 1)] for i in range(2)])

        def wu_turn(part, i, tag):
            banks["wu", part, i] = turn_weight_rows(tag, [wu_raw[part][:, i + 2 * j if part == 0 else 2 * i + j, :] for j in range(2)])

        def wd_out(th, g, copy=nc.scalar.copy):
            words = wd_grouped[:, th, g].rearrange("p n t -> p (n t)").bitcast(F32)
            copy(out=words.rearrange("p (c i u) -> p c u i", i=RUN, u=2), in_=banks["wd", th, g][:].rearrange("p u (c i) -> p c u i", i=RUN))

        def wu_out(part, e, copy=nc.scalar.copy):
            words = wu_grouped[:, part].rearrange("p n t -> p (n t)").bitcast(F32)
            order = "p (h e m j u) -> p e h m j u" if part == 0 else "p (h m e j u) -> p e h m j u"
            copy(out=words.rearrange(order, h=H, e=2, j=2, u=2)[:, e], in_=banks["wu", part, e][:].rearrange("p u (j h m) -> p h m j u", j=2, h=H))

        def wd_quant(th):
            nc.vector.quantize_mx(
                out=wd_codes[:, th].rearrange("p g n -> p (g n)").bitcast(FP8X4),
                scales=wd_scales[:, th].rearrange("p g n -> p (g n)"),
                in_=wd_grouped[:, th].rearrange("p g n t -> p (g n t)"),
            )

        def wu_quant(part):
            nc.vector.quantize_mx(out=wu_codes[:, part].bitcast(FP8X4), scales=wu_scales[:, part], in_=wu_grouped[:, part].rearrange("p n t -> p (n t)"))

        wide, words, x_mx, latents, latent_mx, sums, rstds, quads, values = {}, {}, {}, {}, {}, {}, {}, {}, {}

        def widen(pair, first=0, last=2, copy=nc.scalar.copy):
            if pair not in wide:
                x_wide = work.tile([P, 2 * C], BF16, tag="x_wide", bufs=WIDE_BUFS, align_bytes=64, name="x_wide")
                wide[pair] = x_wide
            copy(out=wide[pair][:, C * first : C * last], in_=x_tiles[pair][:, first:last].rearrange("p a c -> p (a c)").bitcast(FP8))

        def turn(pair, g, tag=None):
            bank = bank_tile(tag or "xt%d" % g, [P, 4 * SUB])
            turned = bank[:].rearrange("p (u n) -> p n u" if pair < FIRST_PAIRED else "p (n u) -> p n u", u=2)
            for a in range(2):
                rows = wide[pair][:, C * a + PASS * g : C * a + PASS * (g + 1)]
                for u in range(2):
                    nc.tensor.transpose(turned[:, SUB * a : SUB * (a + 1), u], rows.bitcast(F32)[:, u:WORDS:2], ident[:])
            banks["xt", pair, g] = bank

        def scale_x(engine, pair, g, turned, first, last):
            engine.tensor_tensor(
                out=stages[pair][:].bitcast(BF16).rearrange("p (g n u e) -> p g n u e", g=2, u=2, e=2)[:, g, first:last],
                in0=turned,
                in1=scale[:, g].rearrange("p (u e) -> p u e", e=2).unsqueeze(1).broadcast_to([P, last - first, 2, 2]),
                op=ALU.mult,
            )

        def x_out(pair, g):
            first = share(pair) if g == 1 else 0
            if first == 2 * SUB:
                return
            bank = banks["xt", pair, g][:].bitcast(BF16).rearrange("p (u n e) -> p n u e" if pair < FIRST_PAIRED else "p (n u e) -> p n u e", u=2, e=2)
            scale_x(nc.vector, pair, g, bank[:, first:], first, 2 * SUB)

        def words_out(pair, copy=nc.scalar.copy):
            if pair == 2:
                part = stages[pair - 1][:, 0 : 2 * share(pair)].rearrange("p (n u) -> p n u", u=2)
            else:
                part = work.tile([P, share(pair), 2], F32, tag="words", align_bytes=64, name="words")
            copy(out=part[:], in_=banks["xt", pair, 1][:].rearrange("p (u n) -> p n u" if pair < FIRST_PAIRED else "p (n u) -> p n u", u=2)[:, 0 : share(pair)])
            words[pair] = part

        def words_scale(pair):
            turned = words[pair][:].rearrange("p n u -> p (n u)").bitcast(BF16).rearrange("p (n u e) -> p n u e", u=2, e=2)
            scale_x(nc.gpsimd, pair, 1, turned, 0, share(pair))

        def x_quant(pair):
            codes = work.tile([P, 2, 2 * SUB], U32, tag="x_q", align_bytes=64, name="x_q")
            scales = work.tile([P, 2, 2 * SUB], U8, tag="x_s", align_bytes=64, name="x_s")
            nc.vector.quantize_mx(
                out=codes[:].rearrange("p g n -> p (g n)").bitcast(FP8X4),
                scales=scales[:].rearrange("p g n -> p (g n)"),
                in_=stages[pair][:].bitcast(BF16),
            )
            x_mx[pair] = codes, scales

        def down(pair, a, tag=None):
            bank = bank_tile(tag or "lat%d" % a, [P, 4, SUB])
            codes, scales = x_mx[pair]
            tokens = slice(SUB * a, SUB * (a + 1))
            for t in range(4):
                th, columns = t // 2, slice(P * (t % 2), P * (t % 2 + 1))
                for g in range(2):
                    nc.tensor.matmul_mx(
                        out=bank[:, t, :],
                        lhsT=wd_codes[:, th, g, columns].bitcast(FP8X4),
                        lhsT_scale=wd_scales[:, th, g, columns],
                        rhs=codes[:, g, tokens].bitcast(FP8X4),
                        rhs_scale=scales[:, g, tokens],
                        start=(g == 0),
                        stop=(g == 1),
                    )
            banks["lat", pair, a] = bank

        def latent_out(pair, a, copy=nc.scalar.copy):
            if pair not in latents and pair == PAIRS - 1:
                latents[pair] = stages[0][:, 0:FEAT].bitcast(BF16)
            elif pair not in latents:
                latent = work.tile([P, 2 * SUB * 4], BF16, tag="latent", align_bytes=64, name="latent")
                latents[pair] = latent
            copy(
                out=latents[pair][:, 4 * SUB * a : 4 * SUB * (a + 1)].rearrange("p (c i t) -> p c t i", i=RUN, t=4),
                in_=banks["lat", pair, a][:].rearrange("p t (c i) -> p c t i", i=RUN),
            )

        def latent_quant(pair):
            codes = work.tile([P, 2 * SUB], U32, tag="l_q", bufs=CODE_BUFS, align_bytes=64, name="l_q")
            scales = work.tile([P, 2 * SUB], U8, tag="l_s", bufs=CODE_BUFS, align_bytes=64, name="l_s")
            nc.vector.quantize_mx(out=codes[:].bitcast(FP8X4), scales=scales[:], in_=latents[pair][:])
            latent_mx[pair] = codes, scales

        def up(pair, a, kind, tag=None):
            part = "kv".index(kind)
            bank = bank_tile("%s%d" % (tag or kind, a), [P, FEAT])
            codes, scales = latent_mx[pair]
            nc.tensor.matmul_mx(
                out=bank[:],
                lhsT=codes[:, SUB * a : SUB * (a + 1)].bitcast(FP8X4),
                lhsT_scale=scales[:, SUB * a : SUB * (a + 1)],
                rhs=wu_codes[:, part].bitcast(FP8X4),
                rhs_scale=wu_scales[:, part],
                start=True,
                stop=True,
            )
            banks[kind, pair, a] = bank

        def square_sums(pair, a):
            if a == 0:
                head_sums = work.tile([P, 2, H], F32, tag="sums", name="sums")
                rstd = work.tile([P, 2, H], F32, tag="rstd", name="rstd")
                sums[pair], rstds[pair] = head_sums, rstd
            squares = work.tile([P, FEAT], BF16, tag="squares", bufs=SMALL_BUFS, name="squares")
            for h in range(H):
                head = slice(D * h, D * (h + 1))
                nc.scalar.activation(out=squares[:, head], in_=banks["k", pair, a][:, head], func=ACT.Square, accum_out=sums[pair][:, a, h : h + 1])

        def inverse_rms(pair, first=0, last=2):
            nc.scalar.activation(out=rstds[pair][:, first:last], in_=sums[pair][:, first:last], func=ACT.Abs_reciprocal_sqrt, bias=EPS, scale=1.0 / D)

        def store(out, tile, pair, first, last):
            nc.sync.dma_start(
                out=pair_rows(out.rearrange("b t h d -> b t (h d)"), pair, first, last),
                in_=tile[:].rearrange("p (a f) -> p a f", a=2)[:, first:last],
            )

        def values_out(pair, a, copy=nc.scalar.copy):
            if pair >= PAIRS - len(late_values):
                values[pair] = late_values[PAIRS - 1 - pair]
            elif a == 0:
                v_tile = work.tile([P, 2 * FEAT], F32, tag="v_tile", name="v_tile")
                values[pair] = v_tile
            copy(out=values[pair][:, FEAT * a : FEAT * (a + 1)], in_=banks["v", pair, a][:])
            if pair >= PAIRS - 3:
                store(out_1, values[pair], pair, a, a + 1)
            elif a == 1:
                store(out_1, values[pair], pair, 0, 2)

        def rotate(pair, a):
            if a == 0:
                pair_quads = work.tile([P, 2, H, D, 2], F32, tag="quads", bufs=QUAD_BUFS, name="quads")
                quads[pair] = pair_quads
            row = (2 * pair + a) % ROWS
            for h in range(H):
                nc.vector.scalar_tensor_tensor(
                    out=quads[pair][:, a, h],
                    in0=banks["k", pair, a][:, D * h : D * (h + 1)].unsqueeze(2).broadcast_to([P, D, 2]),
                    scalar=rstds[pair][:, a, h : h + 1],
                    in1=table[:, row].rearrange("p (d r) -> p d r", r=2),
                    op0=ALU.mult,
                    op1=ALU.mult,
                )

        def keys_out(pair, first, last, adder):
            keys = stages[(pair + 3) % PAIRS][:, D * first : D * last]
            halves = quads[pair][:].rearrange("p a h (e j) r -> p (a h) e (j r)", e=2)[:, first:last]
            adder.tensor_tensor(out=keys.rearrange("p (n d) -> p n d", d=D), in0=halves[:, :, 0, :], in1=halves[:, :, 1, :], op=ALU.add)
            rows = pair_rows(out_0.rearrange("b t h d -> b t (h d)"), pair, 0, 2).rearrange("p a f -> p (a f)")
            nc.sync.dma_start(out=rows[:, D * first : D * last], in_=keys)

        widen(0, 0, 1, nc.vector.tensor_copy)
        widen(0, 1, 2)
        widen(1, 0, 1, nc.vector.tensor_copy)
        widen(1, 1, 2)
        spread_gain("k1")
        turn(0, 0)
        turn(0, 1)
        turn(1, 1, "v1")
        turn(1, 0, "v0")
        wd_turn(0, 0, "lat0")
        wd_turn(0, 1, "lat1")
        x_out(0, 0)
        x_out(0, 1)
        wd_turn(1, 0, "k0")
        wd_turn(1, 1, "xt0")
        words_out(1)
        words_scale(1)
        x_out(1, 0)
        x_out(1, 1)
        widen(2)
        turn(2, 0, "v1")
        turn(2, 1)
        wd_out(0, 0)
        wd_out(0, 1)
        wd_out(1, 0)
        wd_out(1, 1)
        widen(3)
        wu_turn(0, 0, "v0")
        wu_turn(0, 1, "k0")
        x_quant(0)
        wd_quant(0)
        x_quant(1)
        wd_quant(1)
        down(0, 0)
        down(0, 1)
        words_out(2)
        words_scale(2)
        wu_out(0, 0)
        wu_out(0, 1)
        widen(4)
        down(1, 0, "xt0")
        down(1, 1, "v0")
        x_out(2, 0)
        turn(3, 0, "v1")
        turn(3, 1)
        table_rows(0, 4)
        table_rows(4, ROWS)
        latent_out(0, 0)
        latent_out(0, 1)
        wu_quant(0)
        latent_quant(0)
        up(0, 0, "k")
        up(0, 1, "k")
        latent_out(1, 0)
        latent_out(1, 1)
        x_quant(2)
        latent_quant(1)
        widen(5)
        x_out(3, 0)
        x_out(3, 1)
        words_out(3, nc.vector.tensor_copy)
        words_scale(3)
        wu_turn(1, 0, "v0")
        down(2, 0)
        wu_turn(1, 1, "v1")
        down(2, 1)
        turn(4, 1)
        turn(4, 0)
        square_sums(0, 0)
        inverse_rms(0, 0, 1)
        square_sums(0, 1)
        wu_out(1, 0)
        inverse_rms(0, 1, 2)
        wu_out(1, 1)
        latent_out(2, 0)
        latent_out(2, 1)
        rotate(0, 0)
        up(1, 0, "k")
        rotate(0, 1)
        up(1, 1, "k")
        wu_quant(1)
        up(0, 0, "v")
        up(0, 1, "v")
        widen(6)
        square_sums(1, 0)
        latent_quant(2)
        x_quant(3)

        for s in range(3, PAIRS - 2):
            keys_out(s - 3, 0, 2 * H, nc.gpsimd)
            down(s, 0)
            if s > 3:
                up(s - 2, 1, "v")
            down(s, 1)
            x_out(s + 1, 1)
            if s % 3 == 0:
                words_out(s + 1, nc.vector.tensor_copy)
                words_scale(s + 1)
            x_out(s + 1, 0)
            square_sums(s - 2, 1)
            inverse_rms(s - 2, 0, 1)
            values_out(s - 2 if s > 3 else 0, 0)
            inverse_rms(s - 2, 1, 2)
            if s == 3:
                values_out(0, 1)
                up(1, 0, "v")
                up(1, 1, "v")
            if s % 3 != 0:
                words_out(s + 1)
                words_scale(s + 1)
            latent_out(s, 0)
            if s + 3 < PAIRS:
                turn(s + 2, 1)
                turn(s + 2, 0)
                latent_out(s, 1)
                if s == 3:
                    values_out(1, 0)
                else:
                    widen(s + 3)
                values_out(s - 2, 1)
                rotate(s - 2, 0)
                up(s - 1, 0, "k")
                up(s - 1, 0, "v")
            else:
                values_out(s - 2, 1)
                up(s - 1, 0, "v")
                turn(s + 2, 1)
                up(s - 1, 1, "v")
                turn(s + 2, 0)
                latent_out(s, 1)
                values_out(s - 1, 0)
                values_out(s - 1, 1)
                rotate(s - 2, 0)
                up(s - 1, 0, "k")
            square_sums(s - 1, 0)
            rotate(s - 2, 1)
            up(s - 1, 1, "k")
            latent_quant(s)
            x_quant(s + 1)

        fourth, third, second, last = PAIRS - 4, PAIRS - 3, PAIRS - 2, PAIRS - 1
        keys_out(fourth - 1, 0, 2 * H, nc.gpsimd)
        down(second, 0)
        down(second, 1)
        x_out(last, 0)
        up(third, 0, "k", "xt")
        up(third, 0, "v")
        x_out(last, 1)
        up(third, 1, "k", "xt")
        up(third, 1, "v")
        square_sums(fourth, 1)
        inverse_rms(fourth, 0, 1)
        latent_out(second, 0)
        inverse_rms(fourth, 1, 2)
        latent_out(second, 1)
        rotate(fourth, 0)
        latent_quant(second)
        x_quant(last)
        square_sums(third, 0)
        values_out(third, 0)
        inverse_rms(third, 0, 1)
        square_sums(third, 1)
        values_out(third, 1)
        keys_out(fourth, 0, H, nc.gpsimd)
        inverse_rms(third, 1, 2)
        up(second, 0, "k")
        down(last, 0)
        down(last, 1)
        rotate(fourth, 1)
        keys_out(fourth, H, 2 * H, nc.gpsimd)
        up(second, 0, "v")
        up(second, 1, "k")
        up(second, 1, "v")
        latent_out(last, 0)
        latent_out(last, 1)
        square_sums(second, 0)
        rotate(third, 0)
        values_out(second, 0, nc.vector.tensor_copy)
        latent_quant(last)
        up(last, 0, "k", "xt")
        up(last, 0, "v", "lat")
        up(last, 1, "v", "lat")
        rotate(third, 1)
        up(last, 1, "k", "xt")
        values_out(second, 1)
        keys_out(third, 0, H, nc.gpsimd)
        inverse_rms(second, 0, 1)
        square_sums(second, 1)
        values_out(last, 0)
        keys_out(third, H, 2 * H, nc.gpsimd)
        inverse_rms(second, 1, 2)
        square_sums(last, 0)
        values_out(last, 1)
        inverse_rms(last, 0, 1)
        square_sums(last, 1)
        inverse_rms(last, 1, 2)
        rotate(second, 0)
        keys_out(second, 0, H, nc.gpsimd)
        rotate(second, 1)
        keys_out(second, H, 2 * H, nc.gpsimd)
        rotate(last, 0)
        keys_out(last, 0, 2, nc.gpsimd)
        rotate(last, 1)
        keys_out(last, 2, 5, nc.vector)
        keys_out(last, 5, 8, nc.vector)
